import numpy as np
import ml_dtypes


def mxq(x, axis, fmt="e4m3"):
    dtype, down = {"e4m3": (ml_dtypes.float8_e4m3fn, 7), "e5m2": (ml_dtypes.float8_e5m2, 14)}[fmt]
    v = np.moveaxis(np.asarray(x, np.float32).astype(ml_dtypes.bfloat16).astype(np.float64), axis, -1)
    blocks = v.reshape(v.shape[:-1] + (-1, 32))
    amax = np.abs(blocks).max(-1, keepdims=True)
    byte = np.maximum(np.where(amax > 0, np.frexp(amax)[1] - 1 + 127, 0) - down, 1)
    scale = np.exp2(byte - 127.0)
    codes = (blocks / scale).astype(np.float32).astype(dtype).astype(np.float64)
    return np.moveaxis((codes * scale).reshape(v.shape), -1, axis)


WIDE = False


def mx_kscale(k):
    if not WIDE:
        return np.ones(k)
    levels = np.array([10, -10, 5, -5, 0])
    a = np.random.permutation(np.resize(levels, k // 512 * 4)).reshape(k // 512, 4)
    idx = np.arange(k)
    return np.exp2(a[idx // 512, idx % 128 // 32])


BF16 = ml_dtypes.bfloat16


def bf(x):
    return np.asarray(x, np.float32).astype(BF16)


def f64(x):
    return np.asarray(x).astype(np.float64)


E2M1 = np.array([0.0, 0.5, 1.0, 1.5, 2.0, 3.0, 4.0, 6.0, -0.0, -0.5, -1.0, -1.5, -2.0, -3.0, -4.0, -6.0])


def pack_weight(w, fmt):
    k, n = w.shape
    w = f64(bf(w)).reshape(k // 32, 32, n)
    amax = np.abs(w).max(1)
    if fmt == "e4m3":
        byte = np.frexp(amax)[1] - 1 + 127 - 7
    else:
        mant, ex = np.frexp(amax / 6.0)
        byte = np.where(mant > 0.5, ex, ex - 1) + 127
    byte = np.clip(np.where(amax > 0, byte, 1), 1, 254)
    scaled = (w * np.exp2(127.0 - byte)[:, None, :]).reshape(k, n).astype(np.float32)
    by_word = np.ascontiguousarray(scaled.reshape(k // 512, 128, 4, n).transpose(0, 1, 3, 2))
    if fmt == "e4m3":
        words = by_word.astype(ml_dtypes.float8_e4m3fn).view(np.uint8)
    else:
        c = by_word.astype(ml_dtypes.float4_e2m1fn).view(np.uint8) & 0xF
        words = c[..., 0::2] | (c[..., 1::2] << 4)
    return np.ascontiguousarray(words), np.ascontiguousarray(byte.astype(np.uint8).reshape(k // 512, 16, n))


def unpack_weight(words, scales, fmt):
    g, p, n, _ = words.shape
    if fmt == "e4m3":
        vals = np.ascontiguousarray(words).view(ml_dtypes.float8_e4m3fn).astype(np.float64)
    else:
        nib = np.empty((g, p, n, 4), np.uint8)
        nib[..., 0::2] = words & 0xF
        nib[..., 1::2] = words >> 4
        vals = E2M1[nib]
    vals = vals * np.repeat(np.exp2(scales.astype(np.float64) - 127.0), 8, axis=1)[..., None]
    return vals.transpose(0, 1, 3, 2).reshape(g * 512, n)


N, DEG, A, B, H = 32, 32, 1024, 256, 1024
FMT = "e4m3"


def setup_inputs():
    s, t = mx_kscale(A), mx_kscale(H)
    src_h = bf(np.random.standard_normal((N, DEG, A)) * s)
    he = bf(np.random.standard_normal((N, DEG, B)))
    Wcf_w = np.random.standard_normal((H, A)) / np.sqrt(A) / s[None, :]
    Wcf_b = bf(np.random.standard_normal(H) * 0.3)
    Wdf_w = bf(np.random.standard_normal((H, B)) / np.sqrt(B) * t[:, None])
    Wdf_b = bf(np.random.standard_normal(H) * 0.3 * t)
    Wfc_w = np.random.standard_normal((A, H)) * 0.8 / np.sqrt(H) / t[None, :]
    Wfc_b = bf(np.random.standard_normal(A) * 0.2)
    Wcf_w_words, Wcf_w_scales = pack_weight(np.ascontiguousarray(Wcf_w.T), FMT)
    Wfc_w_words, Wfc_w_scales = pack_weight(np.ascontiguousarray(Wfc_w.T), FMT)
    return {
        "src_h": src_h,
        "he": he,
        "Wcf_w_words": Wcf_w_words,
        "Wcf_w_scales": Wcf_w_scales,
        "Wcf_b": Wcf_b,
        "Wdf_w": Wdf_w,
        "Wdf_b": Wdf_b,
        "Wfc_w_words": Wfc_w_words,
        "Wfc_w_scales": Wfc_w_scales,
        "Wfc_b": Wfc_b,
    }


def reference(src_h, he, Wcf_w_words, Wcf_w_scales, Wcf_b, Wdf_w, Wdf_b, Wfc_w_words, Wfc_w_scales, Wfc_b):
    h_w = (mxq(f64(src_h), 2, "e4m3") @ unpack_weight(Wcf_w_words, Wcf_w_scales, FMT)) + f64(Wcf_b)
    e_vw = f64(he) @ f64(Wdf_w).T + f64(Wdf_b)
    h = h_w * e_vw
    h = (mxq(h, 2, "e4m3") @ unpack_weight(Wfc_w_words, Wfc_w_scales, FMT)) + f64(Wfc_b)
    return np.sum(np.tanh(h), axis=1)

@@ -1,0 +1,267 @@
+from contextlib import ExitStack
+
+import concourse.mybir as mybir
+from concourse.masks import make_identity
+
+F32 = mybir.dt.float32
+BF16 = mybir.dt.bfloat16
+I32 = mybir.dt.int32
+U32 = mybir.dt.uint32
+U8 = mybir.dt.uint8
+FP8X4 = mybir.dt.float8_e4m3fn_x4
+ADD = mybir.AluOpType.add
+MULT = mybir.AluOpType.mult
+ACT = mybir.ActivationFunctionType
+
+P = 128
+PACK = 4
+K_PASS = P * PACK
+NODES = 32
+DEG = 32
+ATOM = 1024
+BOND = 256
+HID = 1024
+TOK = NODES * DEG
+TOK_TILES = TOK // P
+BANK = 512
+TILES_PER_HALF = BANK // P
+GROUPS = ATOM // K_PASS
+CHUNKS = HID // P
+ATOM_CHUNKS = ATOM // P
+NODES_PER_HALF = BANK // DEG
+TRANSPOSE_LAG = 2
+
+FLOPS = 2 * TOK * (ATOM * HID + BOND * HID + HID * ATOM)
+
+
+def tile_dtnnmsg_kernel(
+    tc, src_h, he, Wcf_w_words, Wcf_w_scales, Wcf_b, Wdf_w, Wdf_b, Wfc_w_words, Wfc_w_scales, Wfc_b, out
+):
+    nc = tc.nc
+    with ExitStack() as ctx:
+        keep = ctx.enter_context(tc.tile_pool(name="keep", bufs=1))
+        stage = ctx.enter_context(tc.tile_pool(name="stage", bufs=3))
+        psum_acc = ctx.enter_context(tc.psum_pool(name="psum_acc", bufs=4))
+        psum_tr = ctx.enter_context(tc.psum_pool(name="psum_tr", bufs=4))
+
+        ident = keep.tile([P, P], F32)
+        make_identity(nc, ident[:])
+        ones = keep.tile([P, P], BF16)
+        nc.vector.memset(ones[:], 1.0)
+        planes = keep.tile([P, HID], U8, align_bytes=64)
+        nc.vector.memset(planes[:].bitcast(I32), 0)
+        bias1_row = keep.tile([P, HID], BF16)
+        nc.vector.memset(bias1_row[:], 0.0)
+        bias3_rows = keep.tile([P, P], BF16)
+        nc.vector.memset(bias3_rows[:], 0.0)
+
+        x_dram = src_h.flatten_outer_dims().rearrange("(i p) a -> p i a", p=P)
+        he_dram = he.flatten_outer_dims().rearrange("(i p) b -> p i b", p=P)
+        he_sb = keep.tile([P, TOK_TILES, BOND], BF16)
+        wdf_sb = keep.tile([P, CHUNKS, BOND], BF16)
+        x_sb = keep.tile([P, TOK_TILES, ATOM], BF16)
+        wcf = keep.tile([P, GROUPS, PACK * HID], U8, align_bytes=64)
+        wfc = keep.tile([P, GROUPS, PACK * ATOM], U8, align_bytes=64)
+
+        def load_x(i):
+            nc.sync.dma_start(out=x_sb[:, i, :], in_=x_dram[:, i, :])
+
+        def load_words(tile_u8, words):
+            for g in range(GROUPS):
+                nc.sync.dma_start(
+                    out=tile_u8[:, g, :].bitcast(I32),
+                    in_=words[g].rearrange("p n t -> p (n t)").bitcast(I32),
+                )
+
+        def load_planes(first_plane, scales):
+            for quadrant in range(4):
+                start = 32 * quadrant + PACK * first_plane
+                nc.sync.dma_start(
+                    out=planes[start : start + PACK * GROUPS, :].bitcast(I32),
+                    in_=scales[:, PACK * quadrant : PACK * (quadrant + 1), :].bitcast(I32),
+                )
+
+        nc.sync.dma_start(out=he_sb[:], in_=he_dram)
+        nc.sync.dma_start(
+            out=wdf_sb[:].rearrange("m (g t) b -> m g t b", g=GROUPS),
+            in_=Wdf_w.rearrange("(g m t) b -> m g t b", g=GROUPS, t=PACK),
+        )
+        load_x(0)
+        load_x(1)
+        load_planes(0, Wcf_w_scales)
+        load_planes(GROUPS, Wfc_w_scales)
+        load_words(wcf, Wcf_w_words)
+        for i in range(2, TOK_TILES):
+            load_x(i)
+        load_words(wfc, Wfc_w_words)
+
+        bias2_bf = keep.tile([P, CHUNKS], BF16)
+        nc.scalar.dma_start(
+            out=bias2_bf[:].rearrange("m (g t) -> m g t", g=GROUPS),
+            in_=Wdf_b.rearrange("(g m t) -> m g t", g=GROUPS, t=PACK),
+        )
+        nc.scalar.dma_start(out=bias1_row[0:1, :], in_=Wcf_b.rearrange("(o h) -> o h", o=1))
+        nc.scalar.dma_start(out=bias3_rows[0:ATOM_CHUNKS, :], in_=Wfc_b.rearrange("(a m) -> a m", m=P))
+        warm = keep.tile([P, 1], F32)
+        nc.vector.memset(warm[:], 0.0)
+        nc.scalar.activation(out=warm[:], in_=warm[:], func=ACT.Tanh)
+
+        heT = keep.tile([P, TOK], F32)
+        wdfT = keep.tile([P, CHUNKS * P], F32)
+        for source, flipped in ((he_sb, heT), (wdf_sb, wdfT)):
+            for j in range(2):
+                bank = psum_tr.tile([P, 4, P], F32, tag="tr")
+                for q in range(4):
+                    nc.tensor.transpose(bank[:, q, :], source[:, 4 * j + q, :].bitcast(F32), ident[:])
+                nc.vector.tensor_copy(
+                    out=flipped[:, BANK * j : BANK * (j + 1)], in_=bank[:].rearrange("p q r -> p (q r)")
+                )
+        heT_bf = heT[:].bitcast(BF16).rearrange("p (r e) -> p r e", e=2)
+        wdfT_bf = wdfT[:].bitcast(BF16).rearrange("p (c m e) -> p c m e", c=CHUNKS, e=2)
+
+        bias2 = keep.tile([P, CHUNKS], F32)
+        nc.vector.tensor_copy(out=bias2[:], in_=bias2_bf[:])
+        bias1 = keep.tile([P, GROUPS, PACK, P], F32)
+        for g in range(GROUPS):
+            acc = psum_acc.tile([P, BANK], F32, tag="acc")
+            nc.tensor.matmul(
+                out=acc[:], lhsT=ones[:], rhs=bias1_row[:, BANK * g : BANK * (g + 1)], start=True, stop=True
+            )
+            nc.vector.tensor_copy(out=bias1[:, g, :, :], in_=acc[:].rearrange("p (m t) -> p t m", t=PACK))
+        bias3_rows_f = keep.tile([P, P], F32)
+        nc.vector.tensor_copy(out=bias3_rows_f[:], in_=bias3_rows[:])
+        bias3_bank = psum_tr.tile([P, P], F32, tag="tr")
+        nc.tensor.transpose(bias3_bank[:], bias3_rows_f[:], ident[:])
+        bias3 = keep.tile([P, ATOM_CHUNKS], F32)
+        nc.vector.tensor_copy(out=bias3[:], in_=bias3_bank[:, 0:ATOM_CHUNKS])
+
+        e_sb = keep.tile([P, CHUNKS, TOK], F32)
+        x_codes = keep.tile([P, TOK_TILES, GROUPS * P], U32, align_bytes=64)
+        x_scales = keep.tile([P, TOK_TILES, GROUPS * P], U8, align_bytes=64)
+        h_codes = keep.tile([P, GROUPS, TOK], U32, align_bytes=64)
+        h_scales = keep.tile([P, GROUPS, TOK], U8, align_bytes=64)
+        sums = keep.tile([P, ATOM_CHUNKS, NODES], F32)
+        hw_tiles = {}
+
+        def bond_product(c, half):
+            cols = slice(BANK * half, BANK * (half + 1))
+            acc = psum_acc.tile([P, BANK], F32, tag="acc")
+            for e in range(2):
+                nc.tensor.matmul(
+                    out=acc[:], lhsT=wdfT_bf[:, c, :, e], rhs=heT_bf[:, cols, e], start=(e == 0), stop=(e == 1)
+                )
+            nc.scalar.activation(
+                out=e_sb[:, c, cols], in_=acc[:], func=ACT.Identity, bias=bias2[:, c : c + 1], scale=1.0
+            )
+
+        def quantise_x(i):
+            words = x_sb[:, i, :].bitcast(F32)
+            bank = psum_tr.tile([P, GROUPS, 2, P], F32, tag="tr")
+            for g in range(GROUPS):
+                for u in range(2):
+                    nc.tensor.transpose(
+                        bank[:, g, u, :], words[:, 256 * g + u : 256 * (g + 1) : 2], ident[:]
+                    )
+            grouped = stage.tile([P, GROUPS * P * PACK], BF16, align_bytes=64, tag="x_grouped")
+            nc.vector.tensor_copy(
+                out=grouped[:].bitcast(F32).rearrange("p (g r u) -> p g r u", g=GROUPS, u=2),
+                in_=bank[:].rearrange("p g u r -> p g r u"),
+            )
+            nc.vector.quantize_mx(
+                out=x_codes[:, i, :].bitcast(FP8X4), scales=x_scales[:, i, :], in_=grouped[:]
+            )
+
+        def atom_product(i):
+            hw = stage.tile([P, GROUPS, PACK, P], F32, tag="hw")
+            hw_tiles[i] = hw
+            for gh in range(GROUPS):
+                acc = psum_acc.tile([P, BANK], F32, tag="acc")
+                for g in range(GROUPS):
+                    toks = slice(P * g, P * (g + 1))
+                    nc.tensor.matmul_mx(
+                        out=acc[:],
+                        lhsT=x_codes[:, i, toks].bitcast(FP8X4),
+                        lhsT_scale=x_scales[:, i, toks],
+                        rhs=wcf[:, g, PACK * BANK * gh : PACK * BANK * (gh + 1)].bitcast(FP8X4),
+                        rhs_scale=planes[PACK * g : P, BANK * gh : BANK * (gh + 1)],
+                        start=(g == 0),
+                        stop=(g == GROUPS - 1),
+                    )
+                nc.vector.tensor_tensor(
+                    out=hw[:, gh, :, :],
+                    in0=acc[:].rearrange("p (m t) -> p t m", t=PACK),
+                    in1=bias1[:, gh, :, :],
+                    op=ADD,
+                )
+
+        def quantise_h(i):
+            hw = hw_tiles[i]
+            toks = slice(P * i, P * (i + 1))
+            for gh in range(GROUPS):
+                bank = psum_tr.tile([P, PACK, P], F32, tag="tr")
+                for t in range(PACK):
+                    nc.tensor.transpose(bank[:, t, :], hw[:, gh, t, :], ident[:])
+                grouped = stage.tile([P, P, PACK], BF16, align_bytes=64, tag="h_grouped")
+                nc.vector.tensor_tensor(
+                    out=grouped[:],
+                    in0=bank[:].rearrange("p t r -> p r t"),
+                    in1=e_sb[:, PACK * gh : PACK * (gh + 1), toks].rearrange("p t r -> p r t"),
+                    op=MULT,
+                )
+                nc.vector.quantize_mx(
+                    out=h_codes[:, gh, toks].bitcast(FP8X4),
+                    scales=h_scales[:, gh, toks],
+                    in_=grouped[:].rearrange("p r t -> p (r t)"),
+                )
+
+        def hidden_product(half, a):
+            cols = slice(BANK * half, BANK * (half + 1))
+            acc = psum_acc.tile([P, BANK], F32, tag="acc")
+            for gh in range(GROUPS):
+                nc.tensor.matmul_mx(
+                    out=acc[:],
+                    lhsT=wfc[:, gh, PACK * P * a : PACK * P * (a + 1)].bitcast(FP8X4),
+                    lhsT_scale=planes[PACK * (GROUPS + gh) : P, P * a : P * (a + 1)],
+                    rhs=h_codes[:, gh, cols].bitcast(FP8X4),
+                    rhs_scale=h_scales[:, gh, cols],
+                    start=(gh == 0),
+                    stop=(gh == GROUPS - 1),
+                )
+            th = stage.tile([P, BANK], F32, tag="th")
+            nc.scalar.activation(out=th[:], in_=acc[:], func=ACT.Tanh, bias=bias3[:, a : a + 1], scale=1.0)
+            nc.vector.tensor_reduce(
+                out=sums[:, a, NODES_PER_HALF * half : NODES_PER_HALF * (half + 1)],
+                in_=th[:].rearrange("p (n d) -> p n d", d=DEG),
+                axis=mybir.AxisListType.X,
+                op=ADD,
+            )
+
+        def store(j):
+            bank = psum_tr.tile([P, P], F32, tag="tr")
+            nc.tensor.transpose(bank[:], sums[:, 4 * j : 4 * (j + 1), :].rearrange("p a n -> p (a n)"), ident[:])
+            rows = stage.tile([P, P], F32, tag="rows")
+            nc.vector.tensor_copy(out=rows[:], in_=bank[:])
+            nc.sync.dma_start(out=out.rearrange("n (a m) -> a n m", m=P)[4 * j : 4 * (j + 1)], in_=rows[:])
+
+        for c in range(CHUNKS):
+            bond_product(c, 0)
+        quantise_x(0)
+        quantise_x(1)
+        for r in range(TOK_TILES + TRANSPOSE_LAG):
+            done = r - TRANSPOSE_LAG
+            if r < TOK_TILES:
+                atom_product(r)
+            if r < TILES_PER_HALF:
+                bond_product(2 * r, 1)
+                bond_product(2 * r + 1, 1)
+            if r + 2 < TOK_TILES:
+                quantise_x(r + 2)
+            if done >= 0:
+                quantise_h(done)
+            if done >= TILES_PER_HALF:
+                hidden_product(0, 2 * (done - TILES_PER_HALF))
+                hidden_product(0, 2 * (done - TILES_PER_HALF) + 1)
+        for a in range(ATOM_CHUNKS):
+            hidden_product(1, a)
+            if a % 4 == 3:
+                store(a // 4)

@@ -163,7 +163,7 @@ def tile_dtnnmsg_kernel(
                         bank[:, g, u, :], words[:, 256 * g + u : 256 * (g + 1) : 2], ident[:]
                     )
             grouped = stage.tile([P, GROUPS * P * PACK], BF16, align_bytes=64, tag="x_grouped")
-            nc.vector.tensor_copy(
+            nc.scalar.copy(
                 out=grouped[:].bitcast(F32).rearrange("p (g r u) -> p g r u", g=GROUPS, u=2),
                 in_=bank[:].rearrange("p g u r -> p g r u"),
             )
@@ -187,12 +187,8 @@ def tile_dtnnmsg_kernel(
                         start=(g == 0),
                         stop=(g == GROUPS - 1),
                     )
-                nc.vector.tensor_tensor(
-                    out=hw[:, gh, :, :],
-                    in0=acc[:].rearrange("p (m t) -> p t m", t=PACK),
-                    in1=bias1[:, gh, :, :],
-                    op=ADD,
-                )
+                nc.scalar.copy(out=hw[:, gh, :, :], in_=acc[:].rearrange("p (m t) -> p t m", t=PACK))
+                nc.gpsimd.tensor_tensor(out=hw[:, gh, :, :], in0=hw[:, gh, :, :], in1=bias1[:, gh, :, :], op=ADD)
 
         def quantise_h(i):
             hw = hw_tiles[i]

@@ -30,6 +30,7 @@ CHUNKS = HID // P
 ATOM_CHUNKS = ATOM // P
 NODES_PER_HALF = BANK // DEG
 TRANSPOSE_LAG = 2
+STORE_LAG = 3
 
 FLOPS = 2 * TOK * (ATOM * HID + BOND * HID + HID * ATOM)
 
@@ -40,31 +41,40 @@ def tile_dtnnmsg_kernel(
     nc = tc.nc
     with ExitStack() as ctx:
         keep = ctx.enter_context(tc.tile_pool(name="keep", bufs=1))
-        stage = ctx.enter_context(tc.tile_pool(name="stage", bufs=3))
+        stage = ctx.enter_context(tc.tile_pool(name="stage", bufs=4))
         psum_acc = ctx.enter_context(tc.psum_pool(name="psum_acc", bufs=4))
         psum_tr = ctx.enter_context(tc.psum_pool(name="psum_tr", bufs=4))
+        ctx.enter_context(tc.manual_schedule())
 
         ident = keep.tile([P, P], F32)
         make_identity(nc, ident[:])
-        ones = keep.tile([P, P], BF16)
-        nc.vector.memset(ones[:], 1.0)
         planes = keep.tile([P, HID], U8, align_bytes=64)
         nc.vector.memset(planes[:].bitcast(I32), 0)
         bias1_row = keep.tile([P, HID], BF16)
         nc.vector.memset(bias1_row[:], 0.0)
         bias3_rows = keep.tile([P, P], BF16)
         nc.vector.memset(bias3_rows[:], 0.0)
+        ones = keep.tile([P, P], BF16)
+        nc.vector.memset(ones[:], 1.0)
+        warm = keep.tile([P, 1], F32)
+        nc.vector.memset(warm[:], 0.0)
 
         x_dram = src_h.flatten_outer_dims().rearrange("(i p) a -> p i a", p=P)
         he_dram = he.flatten_outer_dims().rearrange("(i p) b -> p i b", p=P)
+        wdf_dram = Wdf_w.rearrange("(g m t) b -> m g t b", g=GROUPS, t=PACK)
         he_sb = keep.tile([P, TOK_TILES, BOND], BF16)
-        wdf_sb = keep.tile([P, CHUNKS, BOND], BF16)
+        wdf_sb = keep.tile([P, GROUPS, PACK, BOND], BF16)
         x_sb = keep.tile([P, TOK_TILES, ATOM], BF16)
         wcf = keep.tile([P, GROUPS, PACK * HID], U8, align_bytes=64)
         wfc = keep.tile([P, GROUPS, PACK * ATOM], U8, align_bytes=64)
 
-        def load_x(i):
-            nc.sync.dma_start(out=x_sb[:, i, :], in_=x_dram[:, i, :])
+        def load_he(half):
+            tiles = slice(TILES_PER_HALF * half, TILES_PER_HALF * (half + 1))
+            nc.sync.dma_start(out=he_sb[:, tiles, :], in_=he_dram[:, tiles, :])
+
+        def load_x(half):
+            for i in range(TILES_PER_HALF * half, TILES_PER_HALF * (half + 1)):
+                nc.sync.dma_start(out=x_sb[:, i, :], in_=x_dram[:, i, :])
 
         def load_words(tile_u8, words):
             for g in range(GROUPS):
@@ -81,18 +91,15 @@ def tile_dtnnmsg_kernel(
                     in_=scales[:, PACK * quadrant : PACK * (quadrant + 1), :].bitcast(I32),
                 )
 
-        nc.sync.dma_start(out=he_sb[:], in_=he_dram)
-        nc.sync.dma_start(
-            out=wdf_sb[:].rearrange("m (g t) b -> m g t b", g=GROUPS),
-            in_=Wdf_w.rearrange("(g m t) b -> m g t b", g=GROUPS, t=PACK),
-        )
+        load_he(0)
+        for g in range(GROUPS):
+            nc.sync.dma_start(out=wdf_sb[:, g, :, :], in_=wdf_dram[:, g, :, :])
+        load_he(1)
         load_x(0)
-        load_x(1)
         load_planes(0, Wcf_w_scales)
         load_planes(GROUPS, Wfc_w_scales)
         load_words(wcf, Wcf_w_words)
-        for i in range(2, TOK_TILES):
-            load_x(i)
+        load_x(1)
         load_words(wfc, Wfc_w_words)
 
         bias2_bf = keep.tile([P, CHUNKS], BF16)
@@ -102,20 +109,24 @@ def tile_dtnnmsg_kernel(
         )
         nc.scalar.dma_start(out=bias1_row[0:1, :], in_=Wcf_b.rearrange("(o h) -> o h", o=1))
         nc.scalar.dma_start(out=bias3_rows[0:ATOM_CHUNKS, :], in_=Wfc_b.rearrange("(a m) -> a m", m=P))
-        warm = keep.tile([P, 1], F32)
-        nc.vector.memset(warm[:], 0.0)
         nc.scalar.activation(out=warm[:], in_=warm[:], func=ACT.Tanh)
 
         heT = keep.tile([P, TOK], F32)
         wdfT = keep.tile([P, CHUNKS * P], F32)
-        for source, flipped in ((he_sb, heT), (wdf_sb, wdfT)):
-            for j in range(2):
-                bank = psum_tr.tile([P, 4, P], F32, tag="tr")
-                for q in range(4):
-                    nc.tensor.transpose(bank[:, q, :], source[:, 4 * j + q, :].bitcast(F32), ident[:])
-                nc.vector.tensor_copy(
-                    out=flipped[:, BANK * j : BANK * (j + 1)], in_=bank[:].rearrange("p q r -> p (q r)")
-                )
+
+        def transpose_four(rows_of):
+            bank = psum_tr.tile([P, 4, P], F32, tag="tr")
+            for q in range(4):
+                nc.tensor.transpose(bank[:, q, :], rows_of(q).bitcast(F32), ident[:])
+            return bank[:].rearrange("p q r -> p (q r)")
+
+        he_bank = transpose_four(lambda q: he_sb[:, q, :])
+        nc.vector.tensor_copy(out=heT[:, 0:BANK], in_=he_bank)
+        for g in range(GROUPS):
+            wdf_bank = transpose_four(lambda t: wdf_sb[:, g, t, :])
+            nc.scalar.copy(out=wdfT[:, BANK * g : BANK * (g + 1)], in_=wdf_bank)
+        he_bank = transpose_four(lambda q: he_sb[:, TILES_PER_HALF + q, :])
+        nc.vector.tensor_copy(out=heT[:, BANK : 2 * BANK], in_=he_bank)
         heT_bf = heT[:].bitcast(BF16).rearrange("p (r e) -> p r e", e=2)
         wdfT_bf = wdfT[:].bitcast(BF16).rearrange("p (c m e) -> p c m e", c=CHUNKS, e=2)
 
@@ -141,35 +152,36 @@ def tile_dtnnmsg_kernel(
         h_codes = keep.tile([P, GROUPS, TOK], U32, align_bytes=64)
         h_scales = keep.tile([P, GROUPS, TOK], U8, align_bytes=64)
         sums = keep.tile([P, ATOM_CHUNKS, NODES], F32)
+        x_banks = {}
         hw_tiles = {}
 
-        def bond_product(c, half):
+        def bond_product_and_x(c, half):
             cols = slice(BANK * half, BANK * (half + 1))
+            i = TILES_PER_HALF * half + c // GROUPS
+            g = c % GROUPS
+            if g == 0:
+                x_banks[i] = psum_tr.tile([P, GROUPS, 2, P], F32, tag="tr", name="x_bank")
+            words = x_sb[:, i, :].bitcast(F32)
             acc = psum_acc.tile([P, BANK], F32, tag="acc")
-            for e in range(2):
+            for u in range(2):
                 nc.tensor.matmul(
-                    out=acc[:], lhsT=wdfT_bf[:, c, :, e], rhs=heT_bf[:, cols, e], start=(e == 0), stop=(e == 1)
+                    out=acc[:], lhsT=wdfT_bf[:, c, :, u], rhs=heT_bf[:, cols, u], start=(u == 0), stop=(u == 1)
+                )
+                nc.tensor.transpose(
+                    x_banks[i][:, g, u, :], words[:, 256 * g + u : 256 * (g + 1) : 2], ident[:]
                 )
             nc.scalar.activation(
                 out=e_sb[:, c, cols], in_=acc[:], func=ACT.Identity, bias=bias2[:, c : c + 1], scale=1.0
             )
-
-        def quantise_x(i):
-            words = x_sb[:, i, :].bitcast(F32)
-            bank = psum_tr.tile([P, GROUPS, 2, P], F32, tag="tr")
-            for g in range(GROUPS):
-                for u in range(2):
-                    nc.tensor.transpose(
-                        bank[:, g, u, :], words[:, 256 * g + u : 256 * (g + 1) : 2], ident[:]
-                    )
-            grouped = stage.tile([P, GROUPS * P * PACK], BF16, align_bytes=64, tag="x_grouped")
-            nc.scalar.copy(
-                out=grouped[:].bitcast(F32).rearrange("p (g r u) -> p g r u", g=GROUPS, u=2),
-                in_=bank[:].rearrange("p g u r -> p g r u"),
-            )
-            nc.vector.quantize_mx(
-                out=x_codes[:, i, :].bitcast(FP8X4), scales=x_scales[:, i, :], in_=grouped[:]
-            )
+            if g == GROUPS - 1:
+                grouped = stage.tile([P, GROUPS * P * PACK], BF16, align_bytes=64, tag="x_grouped")
+                nc.scalar.copy(
+                    out=grouped[:].bitcast(F32).rearrange("p (g r u) -> p g r u", g=GROUPS, u=2),
+                    in_=x_banks[i][:].rearrange("p g u r -> p g r u"),
+                )
+                nc.vector.quantize_mx(
+                    out=x_codes[:, i, :].bitcast(FP8X4), scales=x_scales[:, i, :], in_=grouped[:]
+                )
 
         def atom_product(i):
             hw = stage.tile([P, GROUPS, PACK, P], F32, tag="hw")
@@ -193,21 +205,22 @@ def tile_dtnnmsg_kernel(
         def quantise_h(i):
             hw = hw_tiles[i]
             toks = slice(P * i, P * (i + 1))
+            grouped = stage.tile([P, GROUPS, P, PACK], BF16, align_bytes=64, tag="h_grouped")
             for gh in range(GROUPS):
                 bank = psum_tr.tile([P, PACK, P], F32, tag="tr")
                 for t in range(PACK):
                     nc.tensor.transpose(bank[:, t, :], hw[:, gh, t, :], ident[:])
-                grouped = stage.tile([P, P, PACK], BF16, align_bytes=64, tag="h_grouped")
                 nc.vector.tensor_tensor(
-                    out=grouped[:],
+                    out=grouped[:, gh, :, :],
                     in0=bank[:].rearrange("p t r -> p r t"),
                     in1=e_sb[:, PACK * gh : PACK * (gh + 1), toks].rearrange("p t r -> p r t"),
                     op=MULT,
                 )
+            for gh in range(GROUPS):
                 nc.vector.quantize_mx(
                     out=h_codes[:, gh, toks].bitcast(FP8X4),
                     scales=h_scales[:, gh, toks],
-                    in_=grouped[:].rearrange("p r t -> p (r t)"),
+                    in_=grouped[:, gh, :, :].rearrange("p r t -> p (r t)"),
                 )
 
         def hidden_product(half, a):
@@ -236,22 +249,18 @@ def tile_dtnnmsg_kernel(
             bank = psum_tr.tile([P, P], F32, tag="tr")
             nc.tensor.transpose(bank[:], sums[:, 4 * j : 4 * (j + 1), :].rearrange("p a n -> p (a n)"), ident[:])
             rows = stage.tile([P, P], F32, tag="rows")
-            nc.vector.tensor_copy(out=rows[:], in_=bank[:])
+            nc.scalar.copy(out=rows[:], in_=bank[:])
             nc.sync.dma_start(out=out.rearrange("n (a m) -> a n m", m=P)[4 * j : 4 * (j + 1)], in_=rows[:])
 
         for c in range(CHUNKS):
-            bond_product(c, 0)
-        quantise_x(0)
-        quantise_x(1)
+            bond_product_and_x(c, 0)
         for r in range(TOK_TILES + TRANSPOSE_LAG):
             done = r - TRANSPOSE_LAG
             if r < TOK_TILES:
                 atom_product(r)
             if r < TILES_PER_HALF:
-                bond_product(2 * r, 1)
-                bond_product(2 * r + 1, 1)
-            if r + 2 < TOK_TILES:
-                quantise_x(r + 2)
+                bond_product_and_x(2 * r, 1)
+                bond_product_and_x(2 * r + 1, 1)
             if done >= 0:
                 quantise_h(done)
             if done >= TILES_PER_HALF:
@@ -259,5 +268,6 @@ def tile_dtnnmsg_kernel(
                 hidden_product(0, 2 * (done - TILES_PER_HALF) + 1)
         for a in range(ATOM_CHUNKS):
             hidden_product(1, a)
-            if a % 4 == 3:
-                store(a // 4)
+            if a == ATOM_CHUNKS // 2 - 1 + STORE_LAG:
+                store(0)
+        store(1)

@@ -29,8 +29,8 @@ GROUPS = ATOM // K_PASS
 CHUNKS = HID // P
 ATOM_CHUNKS = ATOM // P
 NODES_PER_HALF = BANK // DEG
-TRANSPOSE_LAG = 2
 STORE_LAG = 3
+INTERLEAVE_ON = "gpsimd"
 
 FLOPS = 2 * TOK * (ATOM * HID + BOND * HID + HID * ATOM)
 
@@ -41,21 +41,18 @@ def tile_dtnnmsg_kernel(
     nc = tc.nc
     with ExitStack() as ctx:
         keep = ctx.enter_context(tc.tile_pool(name="keep", bufs=1))
-        stage = ctx.enter_context(tc.tile_pool(name="stage", bufs=4))
-        psum_acc = ctx.enter_context(tc.psum_pool(name="psum_acc", bufs=4))
-        psum_tr = ctx.enter_context(tc.psum_pool(name="psum_tr", bufs=4))
+        stage = ctx.enter_context(tc.tile_pool(name="stage", bufs=3))
+        psum_mx = ctx.enter_context(tc.psum_pool(name="psum_mx", bufs=4))
+        psum_b = ctx.enter_context(tc.psum_pool(name="psum_b", bufs=2))
+        psum_tr = ctx.enter_context(tc.psum_pool(name="psum_tr", bufs=2))
         ctx.enter_context(tc.manual_schedule())
 
         ident = keep.tile([P, P], F32)
         make_identity(nc, ident[:])
         planes = keep.tile([P, HID], U8, align_bytes=64)
         nc.vector.memset(planes[:].bitcast(I32), 0)
-        bias1_row = keep.tile([P, HID], BF16)
-        nc.vector.memset(bias1_row[:], 0.0)
         bias3_rows = keep.tile([P, P], BF16)
         nc.vector.memset(bias3_rows[:], 0.0)
-        ones = keep.tile([P, P], BF16)
-        nc.vector.memset(ones[:], 1.0)
         warm = keep.tile([P, 1], F32)
         nc.vector.memset(warm[:], 0.0)
 
@@ -72,8 +69,8 @@ def tile_dtnnmsg_kernel(
             tiles = slice(TILES_PER_HALF * half, TILES_PER_HALF * (half + 1))
             nc.sync.dma_start(out=he_sb[:, tiles, :], in_=he_dram[:, tiles, :])
 
-        def load_x(half):
-            for i in range(TILES_PER_HALF * half, TILES_PER_HALF * (half + 1)):
+        def load_x(first, last):
+            for i in range(first, last):
                 nc.sync.dma_start(out=x_sb[:, i, :], in_=x_dram[:, i, :])
 
         def load_words(tile_u8, words):
@@ -94,12 +91,13 @@ def tile_dtnnmsg_kernel(
         load_he(0)
         for g in range(GROUPS):
             nc.sync.dma_start(out=wdf_sb[:, g, :, :], in_=wdf_dram[:, g, :, :])
-        load_he(1)
-        load_x(0)
+        load_x(0, 2)
         load_planes(0, Wcf_w_scales)
         load_planes(GROUPS, Wfc_w_scales)
+        load_x(2, 4)
+        load_he(1)
         load_words(wcf, Wcf_w_words)
-        load_x(1)
+        load_x(4, 8)
         load_words(wfc, Wfc_w_words)
 
         bias2_bf = keep.tile([P, CHUNKS], BF16)
@@ -107,62 +105,61 @@ def tile_dtnnmsg_kernel(
             out=bias2_bf[:].rearrange("m (g t) -> m g t", g=GROUPS),
             in_=Wdf_b.rearrange("(g m t) -> m g t", g=GROUPS, t=PACK),
         )
-        nc.scalar.dma_start(out=bias1_row[0:1, :], in_=Wcf_b.rearrange("(o h) -> o h", o=1))
+        bias1_bf = keep.tile([P, CHUNKS], BF16)
+        nc.scalar.dma_start(
+            out=bias1_bf[:].rearrange("m (g t) -> m g t", g=GROUPS),
+            in_=Wcf_b.rearrange("(g m t) -> m g t", g=GROUPS, t=PACK),
+        )
         nc.scalar.dma_start(out=bias3_rows[0:ATOM_CHUNKS, :], in_=Wfc_b.rearrange("(a m) -> a m", m=P))
         nc.scalar.activation(out=warm[:], in_=warm[:], func=ACT.Tanh)
 
         heT = keep.tile([P, TOK], F32)
         wdfT = keep.tile([P, CHUNKS * P], F32)
 
-        def transpose_four(rows_of):
-            bank = psum_tr.tile([P, 4, P], F32, tag="tr")
+        def transpose_four(pool, tag, rows_of):
+            bank = pool.tile([P, 4, P], F32, tag=tag, name="four_bank")
             for q in range(4):
                 nc.tensor.transpose(bank[:, q, :], rows_of(q).bitcast(F32), ident[:])
             return bank[:].rearrange("p q r -> p (q r)")
 
-        he_bank = transpose_four(lambda q: he_sb[:, q, :])
+        he_bank = transpose_four(psum_tr, "tr", lambda q: he_sb[:, q, :])
         nc.vector.tensor_copy(out=heT[:, 0:BANK], in_=he_bank)
-        for g in range(GROUPS):
-            wdf_bank = transpose_four(lambda t: wdf_sb[:, g, t, :])
-            nc.scalar.copy(out=wdfT[:, BANK * g : BANK * (g + 1)], in_=wdf_bank)
-        he_bank = transpose_four(lambda q: he_sb[:, TILES_PER_HALF + q, :])
-        nc.vector.tensor_copy(out=heT[:, BANK : 2 * BANK], in_=he_bank)
+        wdf_bank = transpose_four(psum_b, "b", lambda t: wdf_sb[:, 0, t, :])
+        nc.scalar.copy(out=wdfT[:, 0:BANK], in_=wdf_bank)
+        wdf_bank = transpose_four(psum_b, "b", lambda t: wdf_sb[:, 1, t, :])
+        nc.vector.tensor_copy(out=wdfT[:, BANK : 2 * BANK], in_=wdf_bank)
         heT_bf = heT[:].bitcast(BF16).rearrange("p (r e) -> p r e", e=2)
         wdfT_bf = wdfT[:].bitcast(BF16).rearrange("p (c m e) -> p c m e", c=CHUNKS, e=2)
 
         bias2 = keep.tile([P, CHUNKS], F32)
         nc.vector.tensor_copy(out=bias2[:], in_=bias2_bf[:])
-        bias1 = keep.tile([P, GROUPS, PACK, P], F32)
-        for g in range(GROUPS):
-            acc = psum_acc.tile([P, BANK], F32, tag="acc")
-            nc.tensor.matmul(
-                out=acc[:], lhsT=ones[:], rhs=bias1_row[:, BANK * g : BANK * (g + 1)], start=True, stop=True
-            )
-            nc.vector.tensor_copy(out=bias1[:, g, :, :], in_=acc[:].rearrange("p (m t) -> p t m", t=PACK))
+        bias1 = keep.tile([P, CHUNKS], F32)
+        nc.vector.tensor_copy(out=bias1[:], in_=bias1_bf[:])
         bias3_rows_f = keep.tile([P, P], F32)
         nc.vector.tensor_copy(out=bias3_rows_f[:], in_=bias3_rows[:])
-        bias3_bank = psum_tr.tile([P, P], F32, tag="tr")
-        nc.tensor.transpose(bias3_bank[:], bias3_rows_f[:], ident[:])
         bias3 = keep.tile([P, ATOM_CHUNKS], F32)
-        nc.vector.tensor_copy(out=bias3[:], in_=bias3_bank[:, 0:ATOM_CHUNKS])
 
         e_sb = keep.tile([P, CHUNKS, TOK], F32)
-        x_codes = keep.tile([P, TOK_TILES, GROUPS * P], U32, align_bytes=64)
-        x_scales = keep.tile([P, TOK_TILES, GROUPS * P], U8, align_bytes=64)
+        x_codes = keep.tile([P, GROUPS, TOK], U32, align_bytes=64)
+        x_scales = keep.tile([P, GROUPS, TOK], U8, align_bytes=64)
+        wcf_perm = keep.tile([P, GROUPS, HID], I32, align_bytes=64)
+        planes_perm = keep.tile([P, HID], U8, align_bytes=64)
         h_codes = keep.tile([P, GROUPS, TOK], U32, align_bytes=64)
         h_scales = keep.tile([P, GROUPS, TOK], U8, align_bytes=64)
         sums = keep.tile([P, ATOM_CHUNKS, NODES], F32)
         x_banks = {}
-        hw_tiles = {}
+        x_grouped = {}
+        h_prod = {}
+        h_grouped = {}
 
-        def bond_product_and_x(c, half):
+        def bond_product(c, half):
             cols = slice(BANK * half, BANK * (half + 1))
             i = TILES_PER_HALF * half + c // GROUPS
             g = c % GROUPS
             if g == 0:
                 x_banks[i] = psum_tr.tile([P, GROUPS, 2, P], F32, tag="tr", name="x_bank")
             words = x_sb[:, i, :].bitcast(F32)
-            acc = psum_acc.tile([P, BANK], F32, tag="acc")
+            acc = psum_b.tile([P, BANK], F32, tag="b", name="acc_b")
             for u in range(2):
                 nc.tensor.matmul(
                     out=acc[:], lhsT=wdfT_bf[:, c, :, u], rhs=heT_bf[:, cols, u], start=(u == 0), stop=(u == 1)
@@ -170,62 +167,84 @@ def tile_dtnnmsg_kernel(
                 nc.tensor.transpose(
                     x_banks[i][:, g, u, :], words[:, 256 * g + u : 256 * (g + 1) : 2], ident[:]
                 )
+            return acc
+
+        def copy_e(acc, c, half):
+            cols = slice(BANK * half, BANK * (half + 1))
             nc.scalar.activation(
                 out=e_sb[:, c, cols], in_=acc[:], func=ACT.Identity, bias=bias2[:, c : c + 1], scale=1.0
             )
-            if g == GROUPS - 1:
-                grouped = stage.tile([P, GROUPS * P * PACK], BF16, align_bytes=64, tag="x_grouped")
-                nc.scalar.copy(
-                    out=grouped[:].bitcast(F32).rearrange("p (g r u) -> p g r u", g=GROUPS, u=2),
-                    in_=x_banks[i][:].rearrange("p g u r -> p g r u"),
-                )
-                nc.vector.quantize_mx(
-                    out=x_codes[:, i, :].bitcast(FP8X4), scales=x_scales[:, i, :], in_=grouped[:]
-                )
 
-        def atom_product(i):
-            hw = stage.tile([P, GROUPS, PACK, P], F32, tag="hw")
-            hw_tiles[i] = hw
-            for gh in range(GROUPS):
-                acc = psum_acc.tile([P, BANK], F32, tag="acc")
-                for g in range(GROUPS):
-                    toks = slice(P * g, P * (g + 1))
-                    nc.tensor.matmul_mx(
-                        out=acc[:],
-                        lhsT=x_codes[:, i, toks].bitcast(FP8X4),
-                        lhsT_scale=x_scales[:, i, toks],
-                        rhs=wcf[:, g, PACK * BANK * gh : PACK * BANK * (gh + 1)].bitcast(FP8X4),
-                        rhs_scale=planes[PACK * g : P, BANK * gh : BANK * (gh + 1)],
-                        start=(g == 0),
-                        stop=(g == GROUPS - 1),
-                    )
-                nc.scalar.copy(out=hw[:, gh, :, :], in_=acc[:].rearrange("p (m t) -> p t m", t=PACK))
-                nc.gpsimd.tensor_tensor(out=hw[:, gh, :, :], in0=hw[:, gh, :, :], in1=bias1[:, gh, :, :], op=ADD)
+        def copy_x(i, engine):
+            grouped = stage.tile([P, GROUPS * P * PACK], BF16, align_bytes=64, tag="x_grouped", name="x_grp")
+            x_grouped[i] = grouped
+            dst = grouped[:].bitcast(F32).rearrange("p (g r u) -> p g r u", g=GROUPS, u=2)
+            src = x_banks[i][:].rearrange("p g u r -> p g r u")
+            if engine == "scalar":
+                nc.scalar.copy(out=dst, in_=src)
+            else:
+                nc.vector.tensor_copy(out=dst, in_=src)
 
-        def quantise_h(i):
-            hw = hw_tiles[i]
+        def quantise_x(i):
             toks = slice(P * i, P * (i + 1))
-            grouped = stage.tile([P, GROUPS, P, PACK], BF16, align_bytes=64, tag="h_grouped")
-            for gh in range(GROUPS):
-                bank = psum_tr.tile([P, PACK, P], F32, tag="tr")
-                for t in range(PACK):
-                    nc.tensor.transpose(bank[:, t, :], hw[:, gh, t, :], ident[:])
-                nc.vector.tensor_tensor(
-                    out=grouped[:, gh, :, :],
-                    in0=bank[:].rearrange("p t r -> p r t"),
-                    in1=e_sb[:, PACK * gh : PACK * (gh + 1), toks].rearrange("p t r -> p r t"),
-                    op=MULT,
-                )
-            for gh in range(GROUPS):
+            for g in range(GROUPS):
                 nc.vector.quantize_mx(
-                    out=h_codes[:, gh, toks].bitcast(FP8X4),
-                    scales=h_scales[:, gh, toks],
-                    in_=grouped[:, gh, :, :].rearrange("p r t -> p (r t)"),
+                    out=x_codes[:, g, toks].bitcast(FP8X4),
+                    scales=x_scales[:, g, toks],
+                    in_=x_grouped[i][:, K_PASS * g : K_PASS * (g + 1)],
                 )
 
-        def hidden_product(half, a):
+        def atom_product(c, half):
             cols = slice(BANK * half, BANK * (half + 1))
-            acc = psum_acc.tile([P, BANK], F32, tag="acc")
+            acc = psum_mx.tile([P, BANK], F32, tag="mx", name="acc_mx")
+            for g in range(GROUPS):
+                nc.tensor.matmul_mx(
+                    out=acc[:],
+                    lhsT=wcf_perm[:, g, P * c : P * (c + 1)].bitcast(FP8X4),
+                    lhsT_scale=planes_perm[PACK * g : P, P * c : P * (c + 1)],
+                    rhs=x_codes[:, g, cols].bitcast(FP8X4),
+                    rhs_scale=x_scales[:, g, cols],
+                    start=(g == 0),
+                    stop=(g == GROUPS - 1),
+                )
+            return acc
+
+        def hidden_values(acc, c, half):
+            cols = slice(BANK * half, BANK * (half + 1))
+            gh, t = c // PACK, c % PACK
+            if t == 0:
+                h_prod[(gh, half)] = stage.tile([P, PACK, BANK], BF16, tag="h_prod", name="h_prd")
+            nc.vector.scalar_tensor_tensor(
+                out=h_prod[(gh, half)][:, t, :],
+                in0=acc[:],
+                scalar=bias1[:, c : c + 1],
+                in1=e_sb[:, c, cols],
+                op0=ADD,
+                op1=MULT,
+            )
+
+        def interleave_h(gh, half, engine):
+            grouped = stage.tile([P, BANK, PACK], BF16, align_bytes=64, tag="h_grouped", name="h_grp")
+            h_grouped[(gh, half)] = grouped
+            src = h_prod[(gh, half)][:].rearrange("p t r -> p r t")
+            if engine == "gpsimd":
+                nc.gpsimd.tensor_scalar(out=grouped[:], in0=src, scalar1=1.0, scalar2=0.0, op0=MULT, op1=ADD)
+            elif engine == "scalar":
+                nc.scalar.copy(out=grouped[:], in_=src)
+            else:
+                nc.vector.tensor_copy(out=grouped[:], in_=src)
+
+        def quantise_h(gh, half):
+            cols = slice(BANK * half, BANK * (half + 1))
+            nc.vector.quantize_mx(
+                out=h_codes[:, gh, cols].bitcast(FP8X4),
+                scales=h_scales[:, gh, cols],
+                in_=h_grouped[(gh, half)][:].rearrange("p r t -> p (r t)"),
+            )
+
+        def hidden_product(half, a, pool, tag):
+            cols = slice(BANK * half, BANK * (half + 1))
+            acc = pool.tile([P, BANK], F32, tag=tag, name="acc_z")
             for gh in range(GROUPS):
                 nc.tensor.matmul_mx(
                     out=acc[:],
@@ -236,7 +255,7 @@ def tile_dtnnmsg_kernel(
                     start=(gh == 0),
                     stop=(gh == GROUPS - 1),
                 )
-            th = stage.tile([P, BANK], F32, tag="th")
+            th = stage.tile([P, BANK], F32, tag="th", name="th")
             nc.scalar.activation(out=th[:], in_=acc[:], func=ACT.Tanh, bias=bias3[:, a : a + 1], scale=1.0)
             nc.vector.tensor_reduce(
                 out=sums[:, a, NODES_PER_HALF * half : NODES_PER_HALF * (half + 1)],
@@ -246,28 +265,76 @@ def tile_dtnnmsg_kernel(
             )
 
         def store(j):
-            bank = psum_tr.tile([P, P], F32, tag="tr")
+            bank = psum_tr.tile([P, P], F32, tag="tr", name="store_bank")
             nc.tensor.transpose(bank[:], sums[:, 4 * j : 4 * (j + 1), :].rearrange("p a n -> p (a n)"), ident[:])
-            rows = stage.tile([P, P], F32, tag="rows")
+            rows = stage.tile([P, P], F32, tag="rows", name="rows")
             nc.scalar.copy(out=rows[:], in_=bank[:])
             nc.sync.dma_start(out=out.rearrange("n (a m) -> a n m", m=P)[4 * j : 4 * (j + 1)], in_=rows[:])
 
+        nc.gpsimd.tensor_copy(
+            out=planes_perm[:].rearrange("p (h t m) -> p h m t", h=GROUPS, t=PACK),
+            in_=planes[:].rearrange("p (h m t) -> p h m t", h=GROUPS, t=PACK),
+        )
+
         for c in range(CHUNKS):
-            bond_product_and_x(c, 0)
-        for r in range(TOK_TILES + TRANSPOSE_LAG):
-            done = r - TRANSPOSE_LAG
-            if r < TOK_TILES:
-                atom_product(r)
-            if r < TILES_PER_HALF:
-                bond_product_and_x(2 * r, 1)
-                bond_product_and_x(2 * r + 1, 1)
-            if done >= 0:
-                quantise_h(done)
-            if done >= TILES_PER_HALF:
-                hidden_product(0, 2 * (done - TILES_PER_HALF))
-                hidden_product(0, 2 * (done - TILES_PER_HALF) + 1)
+            acc = bond_product(c, 0)
+            copy_e(acc, c, 0)
+            if c % 2 == 1:
+                copy_x(c // 2, "vector")
+                quantise_x(c // 2)
+            if c == 5:
+                he_bank = transpose_four(psum_tr, "tr", lambda q: he_sb[:, TILES_PER_HALF + q, :])
+                nc.vector.tensor_copy(out=heT[:, BANK : 2 * BANK], in_=he_bank)
+                bias3_bank = psum_mx.tile([P, P], F32, tag="mx", name="bias3_bank")
+                nc.tensor.transpose(bias3_bank[:], bias3_rows_f[:], ident[:])
+                nc.vector.tensor_copy(out=bias3[:], in_=bias3_bank[:, 0:ATOM_CHUNKS])
+                for g in range(GROUPS):
+                    nc.vector.tensor_copy(
+                        out=wcf_perm[:, g, :].rearrange("p (h t m) -> p h t m", h=GROUPS, t=PACK),
+                        in_=wcf[:, g, :].bitcast(I32).rearrange("p (h m t) -> p h t m", h=GROUPS, t=PACK),
+                    )
+
+        def bond_second(c):
+            acc_b = bond_product(c, 1)
+            if c % 2 == 1:
+                copy_x(TILES_PER_HALF + c // 2, "scalar")
+            copy_e(acc_b, c, 1)
+
+        bond_second(0)
+        bond_second(1)
+        for c in range(CHUNKS):
+            acc = atom_product(c, 0)
+            if c + 2 < CHUNKS:
+                bond_second(c + 2)
+            if c % 2 == 0 and c < 6:
+                hidden_values(acc, c, 0)
+                quantise_x(TILES_PER_HALF + c // 2)
+            elif c == 6:
+                quantise_x(TOK_TILES - 1)
+                hidden_values(acc, c, 0)
+            else:
+                hidden_values(acc, c, 0)
+            if c % PACK == PACK - 1:
+                interleave_h(c // PACK, 0, INTERLEAVE_ON)
+        quantise_h(0, 0)
+
+        for c in range(CHUNKS):
+            acc = atom_product(c, 1)
+            hidden_values(acc, c, 1)
+            if c % PACK == PACK - 1:
+                interleave_h(c // PACK, 1, INTERLEAVE_ON)
+            if c == 4:
+                quantise_h(1, 0)
+
+        banks = [(psum_b, "b"), (psum_b, "b"), (psum_tr, "tr"), (psum_tr, "tr")] + [(psum_mx, "mx")] * 4
         for a in range(ATOM_CHUNKS):
-            hidden_product(1, a)
+            hidden_product(0, a, banks[a][0], banks[a][1])
+            if a == 1:
+                quantise_h(0, 1)
+            if a == 5:
+                quantise_h(1, 1)
+        for a in range(ATOM_CHUNKS):
+            hidden_product(1, a, banks[a][0], banks[a][1])
             if a == ATOM_CHUNKS // 2 - 1 + STORE_LAG:
                 store(0)
         store(1)

@@ -49,6 +49,8 @@ def tile_dtnnmsg_kernel(
 
         ident = keep.tile([P, P], F32)
         make_identity(nc, ident[:])
+        ident_bf = keep.tile([P, P], BF16)
+        make_identity(nc, ident_bf[:])
         planes = keep.tile([P, HID], U8, align_bytes=64)
         nc.vector.memset(planes[:].bitcast(I32), 0)
         bias3_rows = keep.tile([P, P], BF16)
@@ -113,23 +115,32 @@ def tile_dtnnmsg_kernel(
         nc.scalar.dma_start(out=bias3_rows[0:ATOM_CHUNKS, :], in_=Wfc_b.rearrange("(a m) -> a m", m=P))
         nc.scalar.activation(out=warm[:], in_=warm[:], func=ACT.Tanh)
 
-        heT = keep.tile([P, TOK], F32)
-        wdfT = keep.tile([P, CHUNKS * P], F32)
+        KB = BOND // P
+        heT = keep.tile([P, KB, TOK], BF16)
+        wdfT = keep.tile([P, KB, HID], BF16)
 
         def transpose_four(pool, tag, rows_of):
-            bank = pool.tile([P, 4, P], F32, tag=tag, name="four_bank")
+            bank = pool.tile([P, 4, P], BF16, tag=tag, name="four_bank")
             for q in range(4):
-                nc.tensor.transpose(bank[:, q, :], rows_of(q).bitcast(F32), ident[:])
+                nc.tensor.transpose(bank[:, q, :], rows_of(q), ident_bf[:])
             return bank[:].rearrange("p q r -> p (q r)")
 
-        he_bank = transpose_four(psum_tr, "tr", lambda q: he_sb[:, q, :])
-        nc.vector.tensor_copy(out=heT[:, 0:BANK], in_=he_bank)
-        wdf_bank = transpose_four(psum_b, "b", lambda t: wdf_sb[:, 0, t, :])
-        nc.scalar.copy(out=wdfT[:, 0:BANK], in_=wdf_bank)
-        wdf_bank = transpose_four(psum_b, "b", lambda t: wdf_sb[:, 1, t, :])
-        nc.vector.tensor_copy(out=wdfT[:, BANK : 2 * BANK], in_=wdf_bank)
-        heT_bf = heT[:].bitcast(BF16).rearrange("p (r e) -> p r e", e=2)
-        wdfT_bf = wdfT[:].bitcast(BF16).rearrange("p (c m e) -> p c m e", c=CHUNKS, e=2)
+        def transpose_he(half, pools):
+            for kb in range(KB):
+                bank = transpose_four(
+                    pools[kb][0], pools[kb][1], lambda q: he_sb[:, TILES_PER_HALF * half + q, P * kb : P * (kb + 1)]
+                )
+                nc.vector.tensor_copy(out=heT[:, kb, BANK * half : BANK * (half + 1)], in_=bank)
+
+        transpose_he(0, [(psum_tr, "tr"), (psum_tr, "tr")])
+        for g in range(GROUPS):
+            for kb in range(KB):
+                pool, tag = [(psum_b, "b"), (psum_mx, "mx")][kb]
+                bank = transpose_four(pool, tag, lambda t: wdf_sb[:, g, t, P * kb : P * (kb + 1)])
+                if kb == 0:
+                    nc.scalar.copy(out=wdfT[:, kb, BANK * g : BANK * (g + 1)], in_=bank)
+                else:
+                    nc.vector.tensor_copy(out=wdfT[:, kb, BANK * g : BANK * (g + 1)], in_=bank)
 
         bias2 = keep.tile([P, CHUNKS], F32)
         nc.vector.tensor_copy(out=bias2[:], in_=bias2_bf[:])
@@ -162,7 +173,11 @@ def tile_dtnnmsg_kernel(
             acc = psum_b.tile([P, BANK], F32, tag="b", name="acc_b")
             for u in range(2):
                 nc.tensor.matmul(
-                    out=acc[:], lhsT=wdfT_bf[:, c, :, u], rhs=heT_bf[:, cols, u], start=(u == 0), stop=(u == 1)
+                    out=acc[:],
+                    lhsT=wdfT[:, u, P * c : P * (c + 1)],
+                    rhs=heT[:, u, cols],
+                    start=(u == 0),
+                    stop=(u == 1),
                 )
                 nc.tensor.transpose(
                     x_banks[i][:, g, u, :], words[:, 256 * g + u : 256 * (g + 1) : 2], ident[:]
@@ -283,8 +298,7 @@ def tile_dtnnmsg_kernel(
                 copy_x(c // 2, "vector")
                 quantise_x(c // 2)
             if c == 5:
-                he_bank = transpose_four(psum_tr, "tr", lambda q: he_sb[:, TILES_PER_HALF + q, :])
-                nc.vector.tensor_copy(out=heT[:, BANK : 2 * BANK], in_=he_bank)
+                transpose_he(1, [(psum_tr, "tr"), (psum_mx, "mx")])
                 bias3_bank = psum_mx.tile([P, P], F32, tag="mx", name="bias3_bank")
                 nc.tensor.transpose(bias3_bank[:], bias3_rows_f[:], ident[:])
                 nc.vector.tensor_copy(out=bias3[:], in_=bias3_bank[:, 0:ATOM_CHUNKS])

@@ -30,7 +30,6 @@ CHUNKS = HID // P
 ATOM_CHUNKS = ATOM // P
 NODES_PER_HALF = BANK // DEG
 STORE_LAG = 3
-INTERLEAVE_ON = "gpsimd"
 
 FLOPS = 2 * TOK * (ATOM * HID + BOND * HID + HID * ATOM)
 
@@ -76,11 +75,13 @@ def tile_dtnnmsg_kernel(
                 nc.sync.dma_start(out=x_sb[:, i, :], in_=x_dram[:, i, :])
 
         def load_words(tile_u8, words):
-            for g in range(GROUPS):
-                nc.sync.dma_start(
-                    out=tile_u8[:, g, :].bitcast(I32),
-                    in_=words[g].rearrange("p n t -> p (n t)").bitcast(I32),
-                )
+            for h in range(2):
+                cols = slice(PACK * BANK * h, PACK * BANK * (h + 1))
+                for g in range(GROUPS):
+                    nc.sync.dma_start(
+                        out=tile_u8[:, g, cols].bitcast(I32),
+                        in_=words[g].rearrange("p n t -> p (n t)")[:, cols].bitcast(I32),
+                    )
 
         def load_planes(first_plane, scales):
             for quadrant in range(4):
@@ -97,8 +98,8 @@ def tile_dtnnmsg_kernel(
         load_planes(0, Wcf_w_scales)
         load_planes(GROUPS, Wfc_w_scales)
         load_x(2, 4)
-        load_he(1)
         load_words(wcf, Wcf_w_words)
+        load_he(1)
         load_x(4, 8)
         load_words(wfc, Wfc_w_words)
 
@@ -132,15 +133,16 @@ def tile_dtnnmsg_kernel(
                 )
                 nc.vector.tensor_copy(out=heT[:, kb, BANK * half : BANK * (half + 1)], in_=bank)
 
-        transpose_he(0, [(psum_tr, "tr"), (psum_tr, "tr")])
-        for g in range(GROUPS):
+        def transpose_wdf(g):
             for kb in range(KB):
-                pool, tag = [(psum_b, "b"), (psum_mx, "mx")][kb]
-                bank = transpose_four(pool, tag, lambda t: wdf_sb[:, g, t, P * kb : P * (kb + 1)])
+                bank = transpose_four(psum_mx, "mx", lambda t: wdf_sb[:, g, t, P * kb : P * (kb + 1)])
                 if kb == 0:
                     nc.scalar.copy(out=wdfT[:, kb, BANK * g : BANK * (g + 1)], in_=bank)
                 else:
                     nc.vector.tensor_copy(out=wdfT[:, kb, BANK * g : BANK * (g + 1)], in_=bank)
+
+        transpose_he(0, [(psum_tr, "tr"), (psum_tr, "tr")])
+        transpose_wdf(0)
 
         bias2 = keep.tile([P, CHUNKS], F32)
         nc.vector.tensor_copy(out=bias2[:], in_=bias2_bf[:])
@@ -163,25 +165,26 @@ def tile_dtnnmsg_kernel(
         h_prod = {}
         h_grouped = {}
 
-        def bond_product(c, half):
+        def bond_product(c, half, x_tile):
             cols = slice(BANK * half, BANK * (half + 1))
-            i = TILES_PER_HALF * half + c // GROUPS
-            g = c % GROUPS
-            if g == 0:
-                x_banks[i] = psum_tr.tile([P, GROUPS, 2, P], F32, tag="tr", name="x_bank")
-            words = x_sb[:, i, :].bitcast(F32)
             acc = psum_b.tile([P, BANK], F32, tag="b", name="acc_b")
-            for u in range(2):
+            if x_tile is not None:
+                x_banks[x_tile] = psum_tr.tile([P, GROUPS, 2, P], F32, tag="tr", name="x_bank")
+            for kb in range(KB):
                 nc.tensor.matmul(
                     out=acc[:],
-                    lhsT=wdfT[:, u, P * c : P * (c + 1)],
-                    rhs=heT[:, u, cols],
-                    start=(u == 0),
-                    stop=(u == 1),
+                    lhsT=wdfT[:, kb, P * c : P * (c + 1)],
+                    rhs=heT[:, kb, cols],
+                    start=(kb == 0),
+                    stop=(kb == KB - 1),
                 )
-                nc.tensor.transpose(
-                    x_banks[i][:, g, u, :], words[:, 256 * g + u : 256 * (g + 1) : 2], ident[:]
-                )
+                if x_tile is not None and kb == 0:
+                    words = x_sb[:, x_tile, :].bitcast(F32)
+                    for g in range(GROUPS):
+                        for u in range(2):
+                            nc.tensor.transpose(
+                                x_banks[x_tile][:, g, u, :], words[:, 256 * g + u : 256 * (g + 1) : 2], ident[:]
+                            )
             return acc
 
         def copy_e(acc, c, half):
@@ -286,66 +289,66 @@ def tile_dtnnmsg_kernel(
             nc.scalar.copy(out=rows[:], in_=bank[:])
             nc.sync.dma_start(out=out.rearrange("n (a m) -> a n m", m=P)[4 * j : 4 * (j + 1)], in_=rows[:])
 
-        nc.gpsimd.tensor_copy(
-            out=planes_perm[:].rearrange("p (h t m) -> p h m t", h=GROUPS, t=PACK),
-            in_=planes[:].rearrange("p (h m t) -> p h m t", h=GROUPS, t=PACK),
-        )
+        LEAD = 6
 
-        for c in range(CHUNKS):
-            acc = bond_product(c, 0)
-            copy_e(acc, c, 0)
-            if c % 2 == 1:
-                copy_x(c // 2, "vector")
-                quantise_x(c // 2)
-            if c == 5:
-                transpose_he(1, [(psum_tr, "tr"), (psum_mx, "mx")])
-                bias3_bank = psum_mx.tile([P, P], F32, tag="mx", name="bias3_bank")
-                nc.tensor.transpose(bias3_bank[:], bias3_rows_f[:], ident[:])
-                nc.vector.tensor_copy(out=bias3[:], in_=bias3_bank[:, 0:ATOM_CHUNKS])
-                for g in range(GROUPS):
-                    nc.vector.tensor_copy(
-                        out=wcf_perm[:, g, :].rearrange("p (h t m) -> p h t m", h=GROUPS, t=PACK),
-                        in_=wcf[:, g, :].bitcast(I32).rearrange("p (h m t) -> p h t m", h=GROUPS, t=PACK),
-                    )
+        def sort_wcf(h):
+            for g in range(GROUPS):
+                nc.vector.tensor_copy(
+                    out=wcf_perm[:, g, BANK * h : BANK * (h + 1)].rearrange("p (t m) -> p t m", t=PACK),
+                    in_=wcf[:, g, PACK * BANK * h : PACK * BANK * (h + 1)].bitcast(I32).rearrange("p (m t) -> p t m", t=PACK),
+                )
+        ENGINE_OF_GROUP = ["gpsimd", "gpsimd", "scalar", "gpsimd"]
 
-        def bond_second(c):
-            acc_b = bond_product(c, 1)
-            if c % 2 == 1:
-                copy_x(TILES_PER_HALF + c // 2, "scalar")
-            copy_e(acc_b, c, 1)
+        def bond(b):
+            half, c = b // CHUNKS, b % CHUNKS
+            x_tile = TILES_PER_HALF * half + c if c < TILES_PER_HALF else None
+            acc_b = bond_product(c, half, x_tile)
+            if x_tile is not None and x_tile >= TILES_PER_HALF - 1:
+                copy_x(x_tile, "scalar")
+            copy_e(acc_b, c, half)
+            if x_tile is not None and x_tile < TILES_PER_HALF - 1:
+                copy_x(x_tile, "vector")
+                quantise_x(x_tile)
 
-        bond_second(0)
-        bond_second(1)
-        for c in range(CHUNKS):
-            acc = atom_product(c, 0)
-            if c + 2 < CHUNKS:
-                bond_second(c + 2)
-            if c % 2 == 0 and c < 6:
-                hidden_values(acc, c, 0)
-                quantise_x(TILES_PER_HALF + c // 2)
-            elif c == 6:
-                quantise_x(TOK_TILES - 1)
-                hidden_values(acc, c, 0)
-            else:
-                hidden_values(acc, c, 0)
-            if c % PACK == PACK - 1:
-                interleave_h(c // PACK, 0, INTERLEAVE_ON)
-        quantise_h(0, 0)
+        for b in range(LEAD):
+            bond(b)
+            if b == 0:
+                nc.vector.tensor_copy(
+                    out=planes_perm[:].rearrange("p (h t m) -> p h m t", h=GROUPS, t=PACK),
+                    in_=planes[:].rearrange("p (h m t) -> p h m t", h=GROUPS, t=PACK),
+                )
+            if b == 1:
+                transpose_wdf(1)
+            if b == TILES_PER_HALF - 1:
+                sort_wcf(0)
+                quantise_x(TILES_PER_HALF - 1)
+                sort_wcf(1)
+        transpose_he(1, [(psum_tr, "tr"), (psum_mx, "mx")])
+        bias3_bank = psum_mx.tile([P, P], F32, tag="mx", name="bias3_bank")
+        nc.tensor.transpose(bias3_bank[:], bias3_rows_f[:], ident[:])
+        nc.vector.tensor_copy(out=bias3[:], in_=bias3_bank[:, 0:ATOM_CHUNKS])
 
-        for c in range(CHUNKS):
-            acc = atom_product(c, 1)
-            hidden_values(acc, c, 1)
-            if c % PACK == PACK - 1:
-                interleave_h(c // PACK, 1, INTERLEAVE_ON)
-            if c == 4:
+        for m in range(2 * CHUNKS):
+            half, c = m // CHUNKS, m % CHUNKS
+            acc = atom_product(c, half)
+            if m + LEAD < 2 * CHUNKS:
+                bond(m + LEAD)
+            hidden_values(acc, c, half)
+            if 3 <= m <= 6:
+                quantise_x(m + 1)
+            if m % PACK == PACK - 1:
+                interleave_h(c // PACK, half, ENGINE_OF_GROUP[m // PACK])
+            if m == 6:
+                quantise_h(0, 0)
+            if m == 11:
                 quantise_h(1, 0)
 
         banks = [(psum_b, "b"), (psum_b, "b"), (psum_tr, "tr"), (psum_tr, "tr")] + [(psum_mx, "mx")] * 4
         for a in range(ATOM_CHUNKS):
             hidden_product(0, a, banks[a][0], banks[a][1])
-            if a == 1:
+            if a == 0:
                 quantise_h(0, 1)
-            if a == 5:
+            if a == 4:
                 quantise_h(1, 1)
         for a in range(ATOM_CHUNKS):
             hidden_product(1, a, banks[a][0], banks[a][1])

@@ -161,6 +161,13 @@ def tile_dtnnmsg_kernel(
         h_scales = keep.tile([P, GROUPS, TOK], U8, align_bytes=64)
         sums = keep.tile([P, ATOM_CHUNKS, NODES], F32)
         x_banks = {}
+        x_sorted = keep.tile([P, TILES_PER_HALF, ATOM // 2], F32)
+
+        def sort_x(i):
+            nc.vector.tensor_copy(
+                out=x_sorted[:, i - TILES_PER_HALF, :].rearrange("p (g u w) -> p g u w", g=GROUPS, u=2),
+                in_=x_sb[:, i, :].bitcast(F32).rearrange("p (g w u) -> p g u w", g=GROUPS, u=2),
+            )
         x_grouped = {}
         h_prod = {}
         h_grouped = {}
@@ -182,9 +189,12 @@ def tile_dtnnmsg_kernel(
                     words = x_sb[:, x_tile, :].bitcast(F32)
                     for g in range(GROUPS):
                         for u in range(2):
-                            nc.tensor.transpose(
-                                x_banks[x_tile][:, g, u, :], words[:, 256 * g + u : 256 * (g + 1) : 2], ident[:]
-                            )
+                            if x_tile >= TILES_PER_HALF:
+                                first = P * (2 * g + u)
+                                rows = x_sorted[:, x_tile - TILES_PER_HALF, first : first + P]
+                            else:
+                                rows = words[:, 256 * g + u : 256 * (g + 1) : 2]
+                            nc.tensor.transpose(x_banks[x_tile][:, g, u, :], rows, ident[:])
             return acc
 
         def copy_e(acc, c, half):
@@ -303,9 +313,9 @@ def tile_dtnnmsg_kernel(
             half, c = b // CHUNKS, b % CHUNKS
             x_tile = TILES_PER_HALF * half + c if c < TILES_PER_HALF else None
             acc_b = bond_product(c, half, x_tile)
+            copy_e(acc_b, c, half)
             if x_tile is not None and x_tile >= TILES_PER_HALF - 1:
                 copy_x(x_tile, "scalar")
-            copy_e(acc_b, c, half)
             if x_tile is not None and x_tile < TILES_PER_HALF - 1:
                 copy_x(x_tile, "vector")
                 quantise_x(x_tile)
@@ -328,12 +338,16 @@ def tile_dtnnmsg_kernel(
         nc.tensor.transpose(bias3_bank[:], bias3_rows_f[:], ident[:])
         nc.vector.tensor_copy(out=bias3[:], in_=bias3_bank[:, 0:ATOM_CHUNKS])
 
+        sort_x(TILES_PER_HALF)
+        sort_x(TILES_PER_HALF + 1)
         for m in range(2 * CHUNKS):
             half, c = m // CHUNKS, m % CHUNKS
             acc = atom_product(c, half)
             if m + LEAD < 2 * CHUNKS:
                 bond(m + LEAD)
             hidden_values(acc, c, half)
+            if m < TILES_PER_HALF - 2:
+                sort_x(TILES_PER_HALF + 2 + m)
             if 3 <= m <= 6:
                 quantise_x(m + 1)
             if m % PACK == PACK - 1:

@@ -40,7 +40,7 @@ def tile_dtnnmsg_kernel(
     nc = tc.nc
     with ExitStack() as ctx:
         keep = ctx.enter_context(tc.tile_pool(name="keep", bufs=1))
-        stage = ctx.enter_context(tc.tile_pool(name="stage", bufs=3))
+        stage = ctx.enter_context(tc.tile_pool(name="stage", bufs=4))
         psum_mx = ctx.enter_context(tc.psum_pool(name="psum_mx", bufs=4))
         psum_b = ctx.enter_context(tc.psum_pool(name="psum_b", bufs=2))
         psum_tr = ctx.enter_context(tc.psum_pool(name="psum_tr", bufs=2))
@@ -285,9 +285,15 @@ def tile_dtnnmsg_kernel(
                 )
             th = stage.tile([P, BANK], F32, tag="th", name="th")
             nc.scalar.activation(out=th[:], in_=acc[:], func=ACT.Tanh, bias=bias3[:, a : a + 1], scale=1.0)
+            th_nd = th[:].rearrange("p (n d) -> p n d", d=DEG)
+            if (half == 1 or a >= 4) and not (half == 1 and a == ATOM_CHUNKS - 1):
+                nc.gpsimd.tensor_tensor(
+                    out=th_nd[:, :, 8 : 16], in0=th_nd[:, :, 8 : 16], in1=th_nd[:, :, 0 : 8], op=ADD
+                )
+                th_nd = th_nd[:, :, 8 : DEG]
             nc.vector.tensor_reduce(
                 out=sums[:, a, NODES_PER_HALF * half : NODES_PER_HALF * (half + 1)],
-                in_=th[:].rearrange("p (n d) -> p n d", d=DEG),
+                in_=th_nd,
                 axis=mybir.AxisListType.X,
                 op=ADD,
             )
@@ -307,7 +313,7 @@ def tile_dtnnmsg_kernel(
                     out=wcf_perm[:, g, BANK * h : BANK * (h + 1)].rearrange("p (t m) -> p t m", t=PACK),
                     in_=wcf[:, g, PACK * BANK * h : PACK * BANK * (h + 1)].bitcast(I32).rearrange("p (m t) -> p t m", t=PACK),
                 )
-        ENGINE_OF_GROUP = ["gpsimd", "gpsimd", "scalar", "gpsimd"]
+        ENGINE_OF_GROUP = ["gpsimd","gpsimd","gpsimd","gpsimd"]
 
         def bond(b):
             half, c = b // CHUNKS, b % CHUNKS
@@ -358,11 +364,17 @@ def tile_dtnnmsg_kernel(
                 quantise_h(1, 0)
 
         banks = [(psum_b, "b"), (psum_b, "b"), (psum_tr, "tr"), (psum_tr, "tr")] + [(psum_mx, "mx")] * 4
+        if 3 == -2:
+            quantise_h(1, 1)
+        if 1 < 0:
+            quantise_h(0, 1)
+        if 3 == -1:
+            quantise_h(1, 1)
         for a in range(ATOM_CHUNKS):
             hidden_product(0, a, banks[a][0], banks[a][1])
-            if a == 0:
+            if a == 1:
                 quantise_h(0, 1)
-            if a == 4:
+            if a == 3:
                 quantise_h(1, 1)
         for a in range(ATOM_CHUNKS):
             hidden_product(1, a, banks[a][0], banks[a][1])

@@ -52,6 +52,8 @@ def tile_dtnnmsg_kernel(
         make_identity(nc, ident_bf[:])
         planes = keep.tile([P, HID], U8, align_bytes=64)
         nc.vector.memset(planes[:].bitcast(I32), 0)
+        planes_fc = keep.tile([P, ATOM], U8, align_bytes=64)
+        nc.vector.memset(planes_fc[:].bitcast(I32), 0)
         bias3_rows = keep.tile([P, P], BF16)
         nc.vector.memset(bias3_rows[:], 0.0)
         warm = keep.tile([P, 1], F32)
@@ -83,24 +85,23 @@ def tile_dtnnmsg_kernel(
                         in_=words[g].rearrange("p n t -> p (n t)")[:, cols].bitcast(I32),
                     )
 
-        def load_planes(first_plane, scales):
+        def load_planes(tile_u8, scales):
             for quadrant in range(4):
-                start = 32 * quadrant + PACK * first_plane
+                start = 32 * quadrant
                 nc.sync.dma_start(
-                    out=planes[start : start + PACK * GROUPS, :].bitcast(I32),
+                    out=tile_u8[start : start + PACK * GROUPS, :].bitcast(I32),
                     in_=scales[:, PACK * quadrant : PACK * (quadrant + 1), :].bitcast(I32),
                 )
 
         load_he(0)
         for g in range(GROUPS):
             nc.sync.dma_start(out=wdf_sb[:, g, :, :], in_=wdf_dram[:, g, :, :])
-        load_x(0, 2)
-        load_planes(0, Wcf_w_scales)
-        load_planes(GROUPS, Wfc_w_scales)
-        load_x(2, 4)
+        load_x(0, 4)
+        load_planes(planes, Wcf_w_scales)
         load_words(wcf, Wcf_w_words)
         load_he(1)
         load_x(4, 8)
+        load_planes(planes_fc, Wfc_w_scales)
         load_words(wfc, Wfc_w_words)
 
         bias2_bf = keep.tile([P, CHUNKS], BF16)
@@ -131,12 +132,15 @@ def tile_dtnnmsg_kernel(
                 bank = transpose_four(
                     pools[kb][0], pools[kb][1], lambda q: he_sb[:, TILES_PER_HALF * half + q, P * kb : P * (kb + 1)]
                 )
-                nc.vector.tensor_copy(out=heT[:, kb, BANK * half : BANK * (half + 1)], in_=bank)
+                if half == 0:
+                    nc.vector.tensor_copy(out=heT[:, kb, BANK * half : BANK * (half + 1)], in_=bank)
+                else:
+                    nc.scalar.copy(out=heT[:, kb, BANK * half : BANK * (half + 1)], in_=bank)
 
         def transpose_wdf(g):
             for kb in range(KB):
                 bank = transpose_four(psum_mx, "mx", lambda t: wdf_sb[:, g, t, P * kb : P * (kb + 1)])
-                if kb == 0:
+                if kb == 0 or g == 1:
                     nc.scalar.copy(out=wdfT[:, kb, BANK * g : BANK * (g + 1)], in_=bank)
                 else:
                     nc.vector.tensor_copy(out=wdfT[:, kb, BANK * g : BANK * (g + 1)], in_=bank)
@@ -277,7 +281,7 @@ def tile_dtnnmsg_kernel(
                 nc.tensor.matmul_mx(
                     out=acc[:],
                     lhsT=wfc[:, gh, PACK * P * a : PACK * P * (a + 1)].bitcast(FP8X4),
-                    lhsT_scale=planes[PACK * (GROUPS + gh) : P, P * a : P * (a + 1)],
+                    lhsT_scale=planes_fc[PACK * gh : P, P * a : P * (a + 1)],
                     rhs=h_codes[:, gh, cols].bitcast(FP8X4),
                     rhs_scale=h_scales[:, gh, cols],
                     start=(gh == 0),
@@ -328,7 +332,7 @@ def tile_dtnnmsg_kernel(
 
         for b in range(LEAD):
             bond(b)
-            if b == 0:
+            if b == 2:
                 nc.vector.tensor_copy(
                     out=planes_perm[:].rearrange("p (h t m) -> p h m t", h=GROUPS, t=PACK),
                     in_=planes[:].rearrange("p (h m t) -> p h m t", h=GROUPS, t=PACK),
@@ -338,22 +342,22 @@ def tile_dtnnmsg_kernel(
             if b == TILES_PER_HALF - 1:
                 sort_wcf(0)
                 quantise_x(TILES_PER_HALF - 1)
-                sort_wcf(1)
         transpose_he(1, [(psum_tr, "tr"), (psum_mx, "mx")])
         bias3_bank = psum_mx.tile([P, P], F32, tag="mx", name="bias3_bank")
         nc.tensor.transpose(bias3_bank[:], bias3_rows_f[:], ident[:])
-        nc.vector.tensor_copy(out=bias3[:], in_=bias3_bank[:, 0:ATOM_CHUNKS])
-
         sort_x(TILES_PER_HALF)
-        sort_x(TILES_PER_HALF + 1)
         for m in range(2 * CHUNKS):
             half, c = m // CHUNKS, m % CHUNKS
             acc = atom_product(c, half)
             if m + LEAD < 2 * CHUNKS:
                 bond(m + LEAD)
             hidden_values(acc, c, half)
-            if m < TILES_PER_HALF - 2:
-                sort_x(TILES_PER_HALF + 2 + m)
+            if m < TILES_PER_HALF - 1:
+                sort_x(TILES_PER_HALF + 1 + m)
+            if m == 1:
+                sort_wcf(1)
+            if m == 3:
+                nc.vector.tensor_copy(out=bias3[:], in_=bias3_bank[:, 0:ATOM_CHUNKS])
             if 3 <= m <= 6:
                 quantise_x(m + 1)
             if m % PACK == PACK - 1:

@@ -260,7 +260,16 @@ def tile_dtnnmsg_kernel(
             h_grouped[(gh, half)] = grouped
             src = h_prod[(gh, half)][:].rearrange("p t r -> p r t")
             if engine == "gpsimd":
-                nc.gpsimd.tensor_scalar(out=grouped[:], in0=src, scalar1=1.0, scalar2=0.0, op0=MULT, op1=ADD)
+                step = BANK // 1
+                for k in range(1):
+                    nc.gpsimd.tensor_scalar(
+                        out=grouped[:, step * k : step * (k + 1), :],
+                        in0=src[:, step * k : step * (k + 1), :],
+                        scalar1=1.0,
+                        scalar2=0.0,
+                        op0=MULT,
+                        op1=ADD,
+                    )
             elif engine == "scalar":
                 nc.scalar.copy(out=grouped[:], in_=src)
             else:
@@ -290,7 +299,7 @@ def tile_dtnnmsg_kernel(
             th = stage.tile([P, BANK], F32, tag="th", name="th")
             nc.scalar.activation(out=th[:], in_=acc[:], func=ACT.Tanh, bias=bias3[:, a : a + 1], scale=1.0)
             th_nd = th[:].rearrange("p (n d) -> p n d", d=DEG)
-            if (half == 1 or a >= 4) and not (half == 1 and a == ATOM_CHUNKS - 1):
+            if half == 1 and a < ATOM_CHUNKS - 1:
                 nc.gpsimd.tensor_tensor(
                     out=th_nd[:, :, 8 : 16], in0=th_nd[:, :, 8 : 16], in1=th_nd[:, :, 0 : 8], op=ADD
                 )
@@ -317,7 +326,13 @@ def tile_dtnnmsg_kernel(
                     out=wcf_perm[:, g, BANK * h : BANK * (h + 1)].rearrange("p (t m) -> p t m", t=PACK),
                     in_=wcf[:, g, PACK * BANK * h : PACK * BANK * (h + 1)].bitcast(I32).rearrange("p (m t) -> p t m", t=PACK),
                 )
-        ENGINE_OF_GROUP = ["gpsimd","gpsimd","gpsimd","gpsimd"]
+        ENGINE_OF_GROUP = ["vector","gpsimd","scalar","gpsimd"]
+        QPOS = [4,11,19,19]
+
+        def quantises_at(r):
+            for q in range(4):
+                if QPOS[q] == r:
+                    quantise_h(q % 2, q // 2)
 
         def bond(b):
             half, c = b // CHUNKS, b % CHUNKS
@@ -362,10 +377,7 @@ def tile_dtnnmsg_kernel(
                 quantise_x(m + 1)
             if m % PACK == PACK - 1:
                 interleave_h(c // PACK, half, ENGINE_OF_GROUP[m // PACK])
-            if m == 6:
-                quantise_h(0, 0)
-            if m == 11:
-                quantise_h(1, 0)
+            quantises_at(m)
 
         banks = [(psum_b, "b"), (psum_b, "b"), (psum_tr, "tr"), (psum_tr, "tr")] + [(psum_mx, "mx")] * 4
         if 3 == -2:
@@ -376,10 +388,7 @@ def tile_dtnnmsg_kernel(
             quantise_h(1, 1)
         for a in range(ATOM_CHUNKS):
             hidden_product(0, a, banks[a][0], banks[a][1])
-            if a == 1:
-                quantise_h(0, 1)
-            if a == 3:
-                quantise_h(1, 1)
+            quantises_at(16 + a)
         for a in range(ATOM_CHUNKS):
             hidden_product(1, a, banks[a][0], banks[a][1])
             if a == ATOM_CHUNKS // 2 - 1 + STORE_LAG:

@@ -391,6 +391,7 @@ def tile_dtnnmsg_kernel(
             quantises_at(16 + a)
         for a in range(ATOM_CHUNKS):
             hidden_product(1, a, banks[a][0], banks[a][1])
-            if a == ATOM_CHUNKS // 2 - 1 + STORE_LAG:
+            if a == ATOM_CHUNKS // 2 - 1 + STORE_LAG + 99:
                 store(0)
+        store(0)
         store(1)

@@ -41,6 +41,7 @@ def tile_dtnnmsg_kernel(
     with ExitStack() as ctx:
         keep = ctx.enter_context(tc.tile_pool(name="keep", bufs=1))
         stage = ctx.enter_context(tc.tile_pool(name="stage", bufs=4))
+        th_pool = ctx.enter_context(tc.tile_pool(name="th_pool", bufs=8))
         psum_mx = ctx.enter_context(tc.psum_pool(name="psum_mx", bufs=4))
         psum_b = ctx.enter_context(tc.psum_pool(name="psum_b", bufs=2))
         psum_tr = ctx.enter_context(tc.psum_pool(name="psum_tr", bufs=2))
@@ -296,10 +297,10 @@ def tile_dtnnmsg_kernel(
                     start=(gh == 0),
                     stop=(gh == GROUPS - 1),
                 )
-            th = stage.tile([P, BANK], F32, tag="th", name="th")
+            th = th_pool.tile([P, BANK], F32, tag="th", name="th")
             nc.scalar.activation(out=th[:], in_=acc[:], func=ACT.Tanh, bias=bias3[:, a : a + 1], scale=1.0)
             th_nd = th[:].rearrange("p (n d) -> p n d", d=DEG)
-            if half == 1 and a < ATOM_CHUNKS - 1:
+            if half == 0 or a < ATOM_CHUNKS - 1:
                 nc.gpsimd.tensor_tensor(
                     out=th_nd[:, :, 8 : 16], in0=th_nd[:, :, 8 : 16], in1=th_nd[:, :, 0 : 8], op=ADD
                 )
@@ -326,8 +327,8 @@ def tile_dtnnmsg_kernel(
                     out=wcf_perm[:, g, BANK * h : BANK * (h + 1)].rearrange("p (t m) -> p t m", t=PACK),
                     in_=wcf[:, g, PACK * BANK * h : PACK * BANK * (h + 1)].bitcast(I32).rearrange("p (m t) -> p t m", t=PACK),
                 )
-        ENGINE_OF_GROUP = ["vector","gpsimd","scalar","gpsimd"]
-        QPOS = [4,11,19,19]
+        ENGINE_OF_GROUP = ["vector","gpsimd","scalar","vector"]
+        QPOS = [4,11,15,15]
 
         def quantises_at(r):
             for q in range(4):

@@ -12,6 +12,7 @@ FP8X4 = mybir.dt.float8_e4m3fn_x4
 ADD = mybir.AluOpType.add
 MULT = mybir.AluOpType.mult
 ACT = mybir.ActivationFunctionType
+AXES = mybir.AxisListType
 
 P = 128
 PACK = 4
@@ -22,14 +23,15 @@ ATOM = 1024
 BOND = 256
 HID = 1024
 TOK = NODES * DEG
-TOK_TILES = TOK // P
 BANK = 512
-TILES_PER_HALF = BANK // P
+HALVES = TOK // BANK
+TILES = BANK // P
 GROUPS = ATOM // K_PASS
 CHUNKS = HID // P
 ATOM_CHUNKS = ATOM // P
-NODES_PER_HALF = BANK // DEG
-STORE_LAG = 3
+HALF_NODES = BANK // DEG
+KB = BOND // P
+RUN = P // HALF_NODES
 
 FLOPS = 2 * TOK * (ATOM * HID + BOND * HID + HID * ATOM)
 
@@ -47,10 +49,12 @@ def tile_dtnnmsg_kernel(
         psum_tr = ctx.enter_context(tc.psum_pool(name="psum_tr", bufs=2))
         ctx.enter_context(tc.manual_schedule())
 
-        ident = keep.tile([P, P], F32)
-        make_identity(nc, ident[:])
         ident_bf = keep.tile([P, P], BF16)
         make_identity(nc, ident_bf[:])
+        ident = keep.tile([P, P], F32)
+        make_identity(nc, ident[:])
+        zeros = keep.tile([P, BANK], BF16)
+        nc.vector.memset(zeros[:], 0.0)
         planes = keep.tile([P, HID], U8, align_bytes=64)
         nc.vector.memset(planes[:].bitcast(I32), 0)
         planes_fc = keep.tile([P, ATOM], U8, align_bytes=64)
@@ -60,31 +64,32 @@ def tile_dtnnmsg_kernel(
         warm = keep.tile([P, 1], F32)
         nc.vector.memset(warm[:], 0.0)
 
-        x_dram = src_h.flatten_outer_dims().rearrange("(i p) a -> p i a", p=P)
-        he_dram = he.flatten_outer_dims().rearrange("(i p) b -> p i b", p=P)
+        x_dram = src_h.flatten_outer_dims().rearrange("(h p q) a -> p h q a", h=HALVES, q=TILES)
+        he_dram = he.flatten_outer_dims().rearrange("(h p q) b -> p h q b", h=HALVES, q=TILES)
         wdf_dram = Wdf_w.rearrange("(g m t) b -> m g t b", g=GROUPS, t=PACK)
-        he_sb = keep.tile([P, TOK_TILES, BOND], BF16)
+        he_sb = keep.tile([P, HALVES, TILES, BOND], BF16)
         wdf_sb = keep.tile([P, GROUPS, PACK, BOND], BF16)
-        x_sb = keep.tile([P, TOK_TILES, ATOM], BF16)
+        x_sb = keep.tile([P, HALVES, TILES, ATOM], BF16)
         wcf = keep.tile([P, GROUPS, PACK * HID], U8, align_bytes=64)
         wfc = keep.tile([P, GROUPS, PACK * ATOM], U8, align_bytes=64)
 
         def load_he(half):
-            tiles = slice(TILES_PER_HALF * half, TILES_PER_HALF * (half + 1))
-            nc.sync.dma_start(out=he_sb[:, tiles, :], in_=he_dram[:, tiles, :])
+            nc.sync.dma_start(out=he_sb[:, half, :, :], in_=he_dram[:, half, :, :])
 
-        def load_x(first, last):
-            for i in range(first, last):
-                nc.sync.dma_start(out=x_sb[:, i, :], in_=x_dram[:, i, :])
+        def load_wdf(g):
+            nc.sync.dma_start(out=wdf_sb[:, g, :, :], in_=wdf_dram[:, g, :, :])
 
-        def load_words(tile_u8, words):
-            for h in range(2):
-                cols = slice(PACK * BANK * h, PACK * BANK * (h + 1))
-                for g in range(GROUPS):
-                    nc.sync.dma_start(
-                        out=tile_u8[:, g, cols].bitcast(I32),
-                        in_=words[g].rearrange("p n t -> p (n t)")[:, cols].bitcast(I32),
-                    )
+        def load_x(i, count=1):
+            half, q = i // TILES, i % TILES
+            nc.sync.dma_start(out=x_sb[:, half, q : q + count, :], in_=x_dram[:, half, q : q + count, :])
+
+        def load_words(tile_u8, words, h):
+            cols = slice(PACK * BANK * h, PACK * BANK * (h + 1))
+            for g in range(GROUPS):
+                nc.sync.dma_start(
+                    out=tile_u8[:, g, cols].bitcast(I32),
+                    in_=words[g].rearrange("p n t -> p (n t)")[:, cols].bitcast(I32),
+                )
 
         def load_planes(tile_u8, scales):
             for quadrant in range(4):
@@ -95,15 +100,21 @@ def tile_dtnnmsg_kernel(
                 )
 
         load_he(0)
-        for g in range(GROUPS):
-            nc.sync.dma_start(out=wdf_sb[:, g, :, :], in_=wdf_dram[:, g, :, :])
-        load_x(0, 4)
+        load_wdf(0)
+        load_x(0)
+        load_x(1)
+        load_wdf(1)
+        load_x(2)
+        load_x(3)
         load_planes(planes, Wcf_w_scales)
-        load_words(wcf, Wcf_w_words)
+        load_words(wcf, Wcf_w_words, 0)
+        load_words(wcf, Wcf_w_words, 1)
         load_he(1)
-        load_x(4, 8)
+        for i in range(4, 8):
+            load_x(i)
         load_planes(planes_fc, Wfc_w_scales)
-        load_words(wfc, Wfc_w_words)
+        load_words(wfc, Wfc_w_words, 0)
+        load_words(wfc, Wfc_w_words, 1)
 
         bias2_bf = keep.tile([P, CHUNKS], BF16)
         nc.scalar.dma_start(
@@ -118,9 +129,39 @@ def tile_dtnnmsg_kernel(
         nc.scalar.dma_start(out=bias3_rows[0:ATOM_CHUNKS, :], in_=Wfc_b.rearrange("(a m) -> a m", m=P))
         nc.scalar.activation(out=warm[:], in_=warm[:], func=ACT.Tanh)
 
-        KB = BOND // P
         heT = keep.tile([P, KB, TOK], BF16)
         wdfT = keep.tile([P, KB, HID], BF16)
+        bias1 = keep.tile([P, CHUNKS], F32)
+        bias2 = keep.tile([P, CHUNKS], F32)
+        bias3 = keep.tile([P, ATOM_CHUNKS], F32)
+        bias3_rows_f = keep.tile([P, P], F32)
+        e_sb = keep.tile([P, CHUNKS, TOK], F32)
+        x_codes = keep.tile([P, GROUPS, TOK], U32, align_bytes=64)
+        x_scales = keep.tile([P, GROUPS, TOK], U8, align_bytes=64)
+        x_sorted = keep.tile([P, HALVES * TILES, ATOM // 2], F32)
+        wcf_perm = keep.tile([P, GROUPS, HID], I32, align_bytes=64)
+        planes_perm = keep.tile([P, HID], U8, align_bytes=64)
+        h_codes = keep.tile([P, GROUPS, TOK], U32, align_bytes=64)
+        h_scales = keep.tile([P, GROUPS, TOK], U8, align_bytes=64)
+        sums = keep.tile([P, ATOM_CHUNKS, NODES], F32, align_bytes=64)
+        sums_t = keep.tile([P, ATOM_CHUNKS, NODES], F32, align_bytes=64)
+        x_banks = {}
+        x_grouped = {}
+        h_prod = {}
+        h_grouped = {}
+
+        def copy(engine, out_ap, in_ap):
+            if engine == "scalar":
+                nc.scalar.copy(out=out_ap, in_=in_ap)
+            elif engine == "gpsimd":
+                nc.gpsimd.tensor_copy(out=out_ap, in_=in_ap)
+            else:
+                nc.vector.tensor_copy(out=out_ap, in_=in_ap)
+
+        def warm_up(count):
+            bank = psum_mx.tile([P, BANK], F32, tag="mx", name="warm_bank")
+            for k in range(count):
+                nc.tensor.matmul(out=bank[:], lhsT=zeros[:, 0:P], rhs=zeros[:], start=True, stop=True)
 
         def transpose_four(pool, tag, rows_of):
             bank = pool.tile([P, 4, P], BF16, tag=tag, name="four_bank")
@@ -128,95 +169,42 @@ def tile_dtnnmsg_kernel(
                 nc.tensor.transpose(bank[:, q, :], rows_of(q), ident_bf[:])
             return bank[:].rearrange("p q r -> p (q r)")
 
-        def transpose_he(half, pools):
-            for kb in range(KB):
-                bank = transpose_four(
-                    pools[kb][0], pools[kb][1], lambda q: he_sb[:, TILES_PER_HALF * half + q, P * kb : P * (kb + 1)]
-                )
-                if half == 0:
-                    nc.vector.tensor_copy(out=heT[:, kb, BANK * half : BANK * (half + 1)], in_=bank)
-                else:
-                    nc.scalar.copy(out=heT[:, kb, BANK * half : BANK * (half + 1)], in_=bank)
+        def transpose_he(half, kb, pool, tag, engine):
+            bank = transpose_four(pool, tag, lambda q: he_sb[:, half, q, P * kb : P * (kb + 1)])
+            copy(engine, heT[:, kb, BANK * half : BANK * (half + 1)], bank)
 
-        def transpose_wdf(g):
-            for kb in range(KB):
-                bank = transpose_four(psum_mx, "mx", lambda t: wdf_sb[:, g, t, P * kb : P * (kb + 1)])
-                if kb == 0 or g == 1:
-                    nc.scalar.copy(out=wdfT[:, kb, BANK * g : BANK * (g + 1)], in_=bank)
-                else:
-                    nc.vector.tensor_copy(out=wdfT[:, kb, BANK * g : BANK * (g + 1)], in_=bank)
+        def transpose_wdf(g, kb, pool, tag, engine):
+            bank = transpose_four(pool, tag, lambda t: wdf_sb[:, g, t, P * kb : P * (kb + 1)])
+            copy(engine, wdfT[:, kb, BANK * g : BANK * (g + 1)], bank)
 
-        transpose_he(0, [(psum_tr, "tr"), (psum_tr, "tr")])
-        transpose_wdf(0)
-
-        bias2 = keep.tile([P, CHUNKS], F32)
-        nc.vector.tensor_copy(out=bias2[:], in_=bias2_bf[:])
-        bias1 = keep.tile([P, CHUNKS], F32)
-        nc.vector.tensor_copy(out=bias1[:], in_=bias1_bf[:])
-        bias3_rows_f = keep.tile([P, P], F32)
-        nc.vector.tensor_copy(out=bias3_rows_f[:], in_=bias3_rows[:])
-        bias3 = keep.tile([P, ATOM_CHUNKS], F32)
-
-        e_sb = keep.tile([P, CHUNKS, TOK], F32)
-        x_codes = keep.tile([P, GROUPS, TOK], U32, align_bytes=64)
-        x_scales = keep.tile([P, GROUPS, TOK], U8, align_bytes=64)
-        wcf_perm = keep.tile([P, GROUPS, HID], I32, align_bytes=64)
-        planes_perm = keep.tile([P, HID], U8, align_bytes=64)
-        h_codes = keep.tile([P, GROUPS, TOK], U32, align_bytes=64)
-        h_scales = keep.tile([P, GROUPS, TOK], U8, align_bytes=64)
-        sums = keep.tile([P, ATOM_CHUNKS, NODES], F32)
-        x_banks = {}
-        x_sorted = keep.tile([P, TILES_PER_HALF, ATOM // 2], F32)
-
-        def sort_x(i):
-            nc.vector.tensor_copy(
-                out=x_sorted[:, i - TILES_PER_HALF, :].rearrange("p (g u w) -> p g u w", g=GROUPS, u=2),
-                in_=x_sb[:, i, :].bitcast(F32).rearrange("p (g w u) -> p g u w", g=GROUPS, u=2),
+        def sort_x(i, engine="vector"):
+            copy(
+                engine,
+                x_sorted[:, i, :].rearrange("p (g u w) -> p g u w", g=GROUPS, u=2),
+                x_sb[:, i // TILES, i % TILES, :].bitcast(F32).rearrange("p (g w u) -> p g u w", g=GROUPS, u=2),
             )
-        x_grouped = {}
-        h_prod = {}
-        h_grouped = {}
 
-        def bond_product(c, half, x_tile):
-            cols = slice(BANK * half, BANK * (half + 1))
-            acc = psum_b.tile([P, BANK], F32, tag="b", name="acc_b")
-            if x_tile is not None:
-                x_banks[x_tile] = psum_tr.tile([P, GROUPS, 2, P], F32, tag="tr", name="x_bank")
-            for kb in range(KB):
-                nc.tensor.matmul(
-                    out=acc[:],
-                    lhsT=wdfT[:, kb, P * c : P * (c + 1)],
-                    rhs=heT[:, kb, cols],
-                    start=(kb == 0),
-                    stop=(kb == KB - 1),
-                )
-                if x_tile is not None and kb == 0:
-                    words = x_sb[:, x_tile, :].bitcast(F32)
-                    for g in range(GROUPS):
-                        for u in range(2):
-                            if x_tile >= TILES_PER_HALF:
-                                first = P * (2 * g + u)
-                                rows = x_sorted[:, x_tile - TILES_PER_HALF, first : first + P]
-                            else:
-                                rows = words[:, 256 * g + u : 256 * (g + 1) : 2]
-                            nc.tensor.transpose(x_banks[x_tile][:, g, u, :], rows, ident[:])
-            return acc
-
-        def copy_e(acc, c, half):
-            cols = slice(BANK * half, BANK * (half + 1))
-            nc.scalar.activation(
-                out=e_sb[:, c, cols], in_=acc[:], func=ACT.Identity, bias=bias2[:, c : c + 1], scale=1.0
-            )
+        def transpose_x(i, is_sorted):
+            bank = psum_tr.tile([P, GROUPS, 2, P], F32, tag="tr", name="x_bank")
+            x_banks[i] = bank
+            words = x_sb[:, i // TILES, i % TILES, :].bitcast(F32)
+            for g in range(GROUPS):
+                for u in range(2):
+                    if is_sorted:
+                        first = P * (2 * g + u)
+                        rows = x_sorted[:, i, first : first + P]
+                    else:
+                        rows = words[:, 256 * g + u : 256 * (g + 1) : 2]
+                    nc.tensor.transpose(bank[:, g, u, :], rows, ident[:])
 
         def copy_x(i, engine):
             grouped = stage.tile([P, GROUPS * P * PACK], BF16, align_bytes=64, tag="x_grouped", name="x_grp")
             x_grouped[i] = grouped
-            dst = grouped[:].bitcast(F32).rearrange("p (g r u) -> p g r u", g=GROUPS, u=2)
-            src = x_banks[i][:].rearrange("p g u r -> p g r u")
-            if engine == "scalar":
-                nc.scalar.copy(out=dst, in_=src)
-            else:
-                nc.vector.tensor_copy(out=dst, in_=src)
+            copy(
+                engine,
+                grouped[:].bitcast(F32).rearrange("p (g r u) -> p g r u", g=GROUPS, u=2),
+                x_banks[i][:].rearrange("p g u r -> p g r u"),
+            )
 
         def quantise_x(i):
             toks = slice(P * i, P * (i + 1))
@@ -227,7 +215,41 @@ def tile_dtnnmsg_kernel(
                     in_=x_grouped[i][:, K_PASS * g : K_PASS * (g + 1)],
                 )
 
-        def atom_product(c, half):
+        def bond_product(b, between=None):
+            half, c = b // CHUNKS, b % CHUNKS
+            cols = slice(BANK * half, BANK * (half + 1))
+            acc = psum_b.tile([P, BANK], F32, tag="b", name="acc_b")
+            for kb in range(KB):
+                nc.tensor.matmul(
+                    out=acc[:],
+                    lhsT=wdfT[:, kb, P * c : P * (c + 1)],
+                    rhs=heT[:, kb, cols],
+                    start=(kb == 0),
+                    stop=(kb == KB - 1),
+                )
+                if between is not None and kb == 0:
+                    between()
+            nc.scalar.activation(
+                out=e_sb[:, c, cols], in_=acc[:], func=ACT.Identity, bias=bias2[:, c : c + 1], scale=1.0
+            )
+
+        def sort_wcf(h):
+            for g in range(GROUPS):
+                nc.vector.tensor_copy(
+                    out=wcf_perm[:, g, BANK * h : BANK * (h + 1)].rearrange("p (t m) -> p t m", t=PACK),
+                    in_=wcf[:, g, PACK * BANK * h : PACK * BANK * (h + 1)]
+                    .bitcast(I32)
+                    .rearrange("p (m t) -> p t m", t=PACK),
+                )
+
+        def sort_planes():
+            nc.vector.tensor_copy(
+                out=planes_perm[:].rearrange("p (h t m) -> p h m t", h=GROUPS, t=PACK),
+                in_=planes[:].rearrange("p (h m t) -> p h m t", h=GROUPS, t=PACK),
+            )
+
+        def atom_product(m):
+            half, c = m // CHUNKS, m % CHUNKS
             cols = slice(BANK * half, BANK * (half + 1))
             acc = psum_mx.tile([P, BANK], F32, tag="mx", name="acc_mx")
             for g in range(GROUPS):
@@ -242,13 +264,14 @@ def tile_dtnnmsg_kernel(
                 )
             return acc
 
-        def hidden_values(acc, c, half):
+        def hidden_values(acc, m):
+            half, c = m // CHUNKS, m % CHUNKS
             cols = slice(BANK * half, BANK * (half + 1))
-            gh, t = c // PACK, c % PACK
+            k, t = m // PACK, m % PACK
             if t == 0:
-                h_prod[(gh, half)] = stage.tile([P, PACK, BANK], BF16, tag="h_prod", name="h_prd")
+                h_prod[k] = stage.tile([P, PACK, BANK], BF16, tag="h_prod", name="h_prd")
             nc.vector.scalar_tensor_tensor(
-                out=h_prod[(gh, half)][:, t, :],
+                out=h_prod[k][:, t, :],
                 in0=acc[:],
                 scalar=bias1[:, c : c + 1],
                 in1=e_sb[:, c, cols],
@@ -256,32 +279,24 @@ def tile_dtnnmsg_kernel(
                 op1=MULT,
             )
 
-        def interleave_h(gh, half, engine):
+        def interleave_h(k, engine):
             grouped = stage.tile([P, BANK, PACK], BF16, align_bytes=64, tag="h_grouped", name="h_grp")
-            h_grouped[(gh, half)] = grouped
-            src = h_prod[(gh, half)][:].rearrange("p t r -> p r t")
+            h_grouped[k] = grouped
+            src = h_prod[k][:].rearrange("p t r -> p r t")
             if engine == "gpsimd":
-                step = BANK // 1
-                for k in range(1):
-                    nc.gpsimd.tensor_scalar(
-                        out=grouped[:, step * k : step * (k + 1), :],
-                        in0=src[:, step * k : step * (k + 1), :],
-                        scalar1=1.0,
-                        scalar2=0.0,
-                        op0=MULT,
-                        op1=ADD,
-                    )
-            elif engine == "scalar":
-                nc.scalar.copy(out=grouped[:], in_=src)
+                nc.gpsimd.tensor_scalar(
+                    out=grouped[:], in0=src, scalar1=1.0, scalar2=0.0, op0=MULT, op1=ADD
+                )
             else:
-                nc.vector.tensor_copy(out=grouped[:], in_=src)
+                copy(engine, grouped[:], src)
 
-        def quantise_h(gh, half):
+        def quantise_h(k):
+            gh, half = k % GROUPS, k // GROUPS
             cols = slice(BANK * half, BANK * (half + 1))
             nc.vector.quantize_mx(
                 out=h_codes[:, gh, cols].bitcast(FP8X4),
                 scales=h_scales[:, gh, cols],
-                in_=h_grouped[(gh, half)][:].rearrange("p r t -> p (r t)"),
+                in_=h_grouped[k][:].rearrange("p r t -> p (r t)"),
             )
 
         def hidden_product(half, a, pool, tag):
@@ -297,79 +312,79 @@ def tile_dtnnmsg_kernel(
                     start=(gh == 0),
                     stop=(gh == GROUPS - 1),
                 )
+            return acc
+
+        def tanh(acc, a):
             th = th_pool.tile([P, BANK], F32, tag="th", name="th")
             nc.scalar.activation(out=th[:], in_=acc[:], func=ACT.Tanh, bias=bias3[:, a : a + 1], scale=1.0)
-            th_nd = th[:].rearrange("p (n d) -> p n d", d=DEG)
-            if half == 0 or a < ATOM_CHUNKS - 1:
-                nc.gpsimd.tensor_tensor(
-                    out=th_nd[:, :, 8 : 16], in0=th_nd[:, :, 8 : 16], in1=th_nd[:, :, 0 : 8], op=ADD
-                )
-                th_nd = th_nd[:, :, 8 : DEG]
+            return th
+
+        def sum_neighbours(th, half, a, fold):
+            first = 0
+            if fold:
+                nc.gpsimd.tensor_tensor(out=th[:, P : 2 * P], in0=th[:, P : 2 * P], in1=th[:, 0:P], op=ADD)
+                first = P
             nc.vector.tensor_reduce(
-                out=sums[:, a, NODES_PER_HALF * half : NODES_PER_HALF * (half + 1)],
-                in_=th_nd,
-                axis=mybir.AxisListType.X,
+                out=sums[:, a, HALF_NODES * half : HALF_NODES * (half + 1)],
+                in_=th[:, first:BANK].rearrange("p (q n d) -> p n q d", n=HALF_NODES, d=RUN),
+                axis=AXES.XY,
                 op=ADD,
             )
 
-        def store(j):
-            bank = psum_tr.tile([P, P], F32, tag="tr", name="store_bank")
-            nc.tensor.transpose(bank[:], sums[:, 4 * j : 4 * (j + 1), :].rearrange("p a n -> p (a n)"), ident[:])
-            rows = stage.tile([P, P], F32, tag="rows", name="rows")
-            nc.scalar.copy(out=rows[:], in_=bank[:])
-            nc.sync.dma_start(out=out.rearrange("n (a m) -> a n m", m=P)[4 * j : 4 * (j + 1)], in_=rows[:])
+        def store(first, count, queues):
+            nc.vector.transpose(
+                out=sums_t[:, first : first + count, :].rearrange("p a n -> p (a n)"),
+                in_=sums[:, first : first + count, :].rearrange("p a n -> p (a n)"),
+            )
+            for k in range(count):
+                queues[k].dma_start(
+                    out=out.rearrange("n (a q i) -> a q n i", q=4, i=32)[first + k], in_=sums_t[:, first + k, :]
+                )
 
+        tr, mx = (psum_tr, "tr"), (psum_mx, "mx")
         LEAD = 6
-
-        def sort_wcf(h):
-            for g in range(GROUPS):
-                nc.vector.tensor_copy(
-                    out=wcf_perm[:, g, BANK * h : BANK * (h + 1)].rearrange("p (t m) -> p t m", t=PACK),
-                    in_=wcf[:, g, PACK * BANK * h : PACK * BANK * (h + 1)].bitcast(I32).rearrange("p (m t) -> p t m", t=PACK),
-                )
-        ENGINE_OF_GROUP = ["vector","gpsimd","scalar","vector"]
-        QPOS = [4,11,15,15]
-
-        def quantises_at(r):
-            for q in range(4):
-                if QPOS[q] == r:
-                    quantise_h(q % 2, q // 2)
-
-        def bond(b):
-            half, c = b // CHUNKS, b % CHUNKS
-            x_tile = TILES_PER_HALF * half + c if c < TILES_PER_HALF else None
-            acc_b = bond_product(c, half, x_tile)
-            copy_e(acc_b, c, half)
-            if x_tile is not None and x_tile >= TILES_PER_HALF - 1:
-                copy_x(x_tile, "scalar")
-            if x_tile is not None and x_tile < TILES_PER_HALF - 1:
-                copy_x(x_tile, "vector")
-                quantise_x(x_tile)
-
+        warm_up(5)
+        for kb in range(KB):
+            transpose_he(0, kb, *tr, "vector")
+        warm_up(1)
+        transpose_wdf(0, 0, *mx, "scalar")
+        transpose_wdf(0, 1, *mx, "vector")
+        nc.vector.tensor_copy(out=bias2[:], in_=bias2_bf[:])
+        nc.vector.tensor_copy(out=bias1[:], in_=bias1_bf[:])
+        nc.vector.tensor_copy(out=bias3_rows_f[:], in_=bias3_rows[:])
+        transpose_x(0, False)
+        copy_x(0, "vector")
         for b in range(LEAD):
-            bond(b)
-            if b == 2:
-                nc.vector.tensor_copy(
-                    out=planes_perm[:].rearrange("p (h t m) -> p h m t", h=GROUPS, t=PACK),
-                    in_=planes[:].rearrange("p (h m t) -> p h m t", h=GROUPS, t=PACK),
-                )
+            if b < 3:
+                bond_product(b, lambda: transpose_x(b + 1, False))
+                copy_x(b + 1, "vector" if b < 2 else "scalar")
+                quantise_x(b)
+            else:
+                bond_product(b)
             if b == 1:
-                transpose_wdf(1)
-            if b == TILES_PER_HALF - 1:
+                transpose_wdf(1, 0, *mx, "scalar")
+                transpose_wdf(1, 1, *mx, "scalar")
+            if b == 2:
+                sort_planes()
+            if b == 3:
                 sort_wcf(0)
-                quantise_x(TILES_PER_HALF - 1)
-        transpose_he(1, [(psum_tr, "tr"), (psum_mx, "mx")])
+                quantise_x(3)
         bias3_bank = psum_mx.tile([P, P], F32, tag="mx", name="bias3_bank")
         nc.tensor.transpose(bias3_bank[:], bias3_rows_f[:], ident[:])
-        sort_x(TILES_PER_HALF)
+        sort_x(4)
         for m in range(2 * CHUNKS):
-            half, c = m // CHUNKS, m % CHUNKS
-            acc = atom_product(c, half)
-            if m + LEAD < 2 * CHUNKS:
-                bond(m + LEAD)
-            hidden_values(acc, c, half)
-            if m < TILES_PER_HALF - 1:
-                sort_x(TILES_PER_HALF + 1 + m)
+            acc = atom_product(m)
+            b = m + LEAD
+            if b == CHUNKS - 1:
+                bond_product(b, lambda: [transpose_he(1, kb, *tr, "scalar") for kb in range(KB)])
+            elif CHUNKS <= b < CHUNKS + TILES:
+                bond_product(b, lambda: transpose_x(b - CHUNKS + TILES, True))
+                copy_x(b - CHUNKS + TILES, "scalar")
+            elif b < 2 * CHUNKS:
+                bond_product(b)
+            hidden_values(acc, m)
+            if m < TILES - 1:
+                sort_x(m + TILES + 1)
             if m == 1:
                 sort_wcf(1)
             if m == 3:
@@ -377,22 +392,16 @@ def tile_dtnnmsg_kernel(
             if 3 <= m <= 6:
                 quantise_x(m + 1)
             if m % PACK == PACK - 1:
-                interleave_h(c // PACK, half, ENGINE_OF_GROUP[m // PACK])
-            quantises_at(m)
-
-        banks = [(psum_b, "b"), (psum_b, "b"), (psum_tr, "tr"), (psum_tr, "tr")] + [(psum_mx, "mx")] * 4
-        if 3 == -2:
-            quantise_h(1, 1)
-        if 1 < 0:
-            quantise_h(0, 1)
-        if 3 == -1:
-            quantise_h(1, 1)
-        for a in range(ATOM_CHUNKS):
-            hidden_product(0, a, banks[a][0], banks[a][1])
-            quantises_at(16 + a)
-        for a in range(ATOM_CHUNKS):
-            hidden_product(1, a, banks[a][0], banks[a][1])
-            if a == ATOM_CHUNKS // 2 - 1 + STORE_LAG + 99:
-                store(0)
-        store(0)
-        store(1)
+                interleave_h(m // PACK, ["vector", "gpsimd", "scalar", "vector"][m // PACK])
+            for k in range(4):
+                if [4, 11, 15, 15][k] == m:
+                    quantise_h(k)
+        banks = [(psum_b, "b")] * 2 + [(psum_tr, "tr")] * 2 + [(psum_mx, "mx")] * 4
+        for half in range(HALVES):
+            for a in range(ATOM_CHUNKS):
+                acc = hidden_product(half, a, *banks[a])
+                sum_neighbours(tanh(acc, a), half, a, (half, a) != (1, ATOM_CHUNKS - 1))
+                if half == 1 and a == 3:
+                    store(0, 4, [nc.sync] * 4)
+                if half == 1 and a > 3:
+                    store(a, 1, [nc.sync])

@@ -44,9 +44,7 @@ def tile_dtnnmsg_kernel(
         keep = ctx.enter_context(tc.tile_pool(name="keep", bufs=1))
         stage = ctx.enter_context(tc.tile_pool(name="stage", bufs=4))
         th_pool = ctx.enter_context(tc.tile_pool(name="th_pool", bufs=8))
-        psum_mx = ctx.enter_context(tc.psum_pool(name="psum_mx", bufs=4))
-        psum_b = ctx.enter_context(tc.psum_pool(name="psum_b", bufs=2))
-        psum_tr = ctx.enter_context(tc.psum_pool(name="psum_tr", bufs=2))
+        psum = ctx.enter_context(tc.psum_pool(name="psum", bufs=8))
         ctx.enter_context(tc.manual_schedule())
 
         ident_bf = keep.tile([P, P], BF16)
@@ -145,10 +143,11 @@ def tile_dtnnmsg_kernel(
         h_scales = keep.tile([P, GROUPS, TOK], U8, align_bytes=64)
         sums = keep.tile([P, ATOM_CHUNKS, NODES], F32, align_bytes=64)
         sums_t = keep.tile([P, ATOM_CHUNKS, NODES], F32, align_bytes=64)
-        x_banks = {}
+        banks = {}
         x_grouped = {}
         h_prod = {}
         h_grouped = {}
+        ths = {}
 
         def copy(engine, out_ap, in_ap):
             if engine == "scalar":
@@ -159,23 +158,42 @@ def tile_dtnnmsg_kernel(
                 nc.vector.tensor_copy(out=out_ap, in_=in_ap)
 
         def warm_up(count):
-            bank = psum_mx.tile([P, BANK], F32, tag="mx", name="warm_bank")
+            bank = psum.tile([P, BANK], F32, tag="bank", name="warm_bank")
             for k in range(count):
                 nc.tensor.matmul(out=bank[:], lhsT=zeros[:, 0:P], rhs=zeros[:], start=True, stop=True)
 
-        def transpose_four(pool, tag, rows_of):
-            bank = pool.tile([P, 4, P], BF16, tag=tag, name="four_bank")
+        def transpose_four(key, rows_of):
+            bank = psum.tile([P, 4, P], BF16, tag="bank", name="four_bank")
+            banks[key] = bank
             for q in range(4):
                 nc.tensor.transpose(bank[:, q, :], rows_of(q), ident_bf[:])
-            return bank[:].rearrange("p q r -> p (q r)")
 
-        def transpose_he(half, kb, pool, tag, engine):
-            bank = transpose_four(pool, tag, lambda q: he_sb[:, half, q, P * kb : P * (kb + 1)])
-            copy(engine, heT[:, kb, BANK * half : BANK * (half + 1)], bank)
+        def transpose_he(half, kb):
+            transpose_four(("he", half, kb), lambda q: he_sb[:, half, q, P * kb : P * (kb + 1)])
 
-        def transpose_wdf(g, kb, pool, tag, engine):
-            bank = transpose_four(pool, tag, lambda t: wdf_sb[:, g, t, P * kb : P * (kb + 1)])
-            copy(engine, wdfT[:, kb, BANK * g : BANK * (g + 1)], bank)
+        def copy_he(half, kb, engine):
+            bank = banks[("he", half, kb)]
+            copy(engine, heT[:, kb, BANK * half : BANK * (half + 1)], bank[:].rearrange("p q r -> p (q r)"))
+
+        def transpose_wdf(g, kb):
+            transpose_four(("wdf", g, kb), lambda t: wdf_sb[:, g, t, P * kb : P * (kb + 1)])
+
+        def copy_wdf(g, kb, engine):
+            bank = banks[("wdf", g, kb)]
+            copy(engine, wdfT[:, kb, BANK * g : BANK * (g + 1)], bank[:].rearrange("p q r -> p (q r)"))
+
+        def copy_biases():
+            nc.vector.tensor_copy(out=bias2[:], in_=bias2_bf[:])
+            nc.vector.tensor_copy(out=bias1[:], in_=bias1_bf[:])
+            nc.vector.tensor_copy(out=bias3_rows_f[:], in_=bias3_rows[:])
+
+        def transpose_bias3():
+            bank = psum.tile([P, P], F32, tag="bank", name="bias3_bank")
+            banks["bias3"] = bank
+            nc.tensor.transpose(bank[:], bias3_rows_f[:], ident[:])
+
+        def copy_bias3():
+            nc.vector.tensor_copy(out=bias3[:], in_=banks["bias3"][:, 0:ATOM_CHUNKS])
 
         def sort_x(i, engine="vector"):
             copy(
@@ -185,8 +203,8 @@ def tile_dtnnmsg_kernel(
             )
 
         def transpose_x(i, is_sorted):
-            bank = psum_tr.tile([P, GROUPS, 2, P], F32, tag="tr", name="x_bank")
-            x_banks[i] = bank
+            bank = psum.tile([P, GROUPS, 2, P], F32, tag="bank", name="x_bank")
+            banks[("x", i)] = bank
             words = x_sb[:, i // TILES, i % TILES, :].bitcast(F32)
             for g in range(GROUPS):
                 for u in range(2):
@@ -203,7 +221,7 @@ def tile_dtnnmsg_kernel(
             copy(
                 engine,
                 grouped[:].bitcast(F32).rearrange("p (g r u) -> p g r u", g=GROUPS, u=2),
-                x_banks[i][:].rearrange("p g u r -> p g r u"),
+                banks[("x", i)][:].rearrange("p g u r -> p g r u"),
             )
 
         def quantise_x(i):
@@ -218,7 +236,8 @@ def tile_dtnnmsg_kernel(
         def bond_product(b, between=None):
             half, c = b // CHUNKS, b % CHUNKS
             cols = slice(BANK * half, BANK * (half + 1))
-            acc = psum_b.tile([P, BANK], F32, tag="b", name="acc_b")
+            acc = psum.tile([P, BANK], F32, tag="bank", name="acc_b")
+            banks[("b", b)] = acc
             for kb in range(KB):
                 nc.tensor.matmul(
                     out=acc[:],
@@ -229,6 +248,11 @@ def tile_dtnnmsg_kernel(
                 )
                 if between is not None and kb == 0:
                     between()
+
+        def copy_e(b):
+            half, c = b // CHUNKS, b % CHUNKS
+            cols = slice(BANK * half, BANK * (half + 1))
+            acc = banks[("b", b)]
             nc.scalar.activation(
                 out=e_sb[:, c, cols], in_=acc[:], func=ACT.Identity, bias=bias2[:, c : c + 1], scale=1.0
             )
@@ -251,7 +275,8 @@ def tile_dtnnmsg_kernel(
         def atom_product(m):
             half, c = m // CHUNKS, m % CHUNKS
             cols = slice(BANK * half, BANK * (half + 1))
-            acc = psum_mx.tile([P, BANK], F32, tag="mx", name="acc_mx")
+            acc = psum.tile([P, BANK], F32, tag="bank", name="acc_mx")
+            banks[("m", m)] = acc
             for g in range(GROUPS):
                 nc.tensor.matmul_mx(
                     out=acc[:],
@@ -262,13 +287,13 @@ def tile_dtnnmsg_kernel(
                     start=(g == 0),
                     stop=(g == GROUPS - 1),
                 )
-            return acc
 
-        def hidden_values(acc, m):
+        def hidden_values(m):
+            acc = banks[("m", m)]
             half, c = m // CHUNKS, m % CHUNKS
             cols = slice(BANK * half, BANK * (half + 1))
             k, t = m // PACK, m % PACK
-            if t == 0:
+            if k not in h_prod:
                 h_prod[k] = stage.tile([P, PACK, BANK], BF16, tag="h_prod", name="h_prd")
             nc.vector.scalar_tensor_tensor(
                 out=h_prod[k][:, t, :],
@@ -299,9 +324,10 @@ def tile_dtnnmsg_kernel(
                 in_=h_grouped[k][:].rearrange("p r t -> p (r t)"),
             )
 
-        def hidden_product(half, a, pool, tag):
+        def hidden_product(half, a):
             cols = slice(BANK * half, BANK * (half + 1))
-            acc = pool.tile([P, BANK], F32, tag=tag, name="acc_z")
+            acc = psum.tile([P, BANK], F32, tag="bank", name="acc_z")
+            banks[("z", half, a)] = acc
             for gh in range(GROUPS):
                 nc.tensor.matmul_mx(
                     out=acc[:],
@@ -312,18 +338,21 @@ def tile_dtnnmsg_kernel(
                     start=(gh == 0),
                     stop=(gh == GROUPS - 1),
                 )
-            return acc
 
-        def tanh(acc, a):
+        def tanh(half, a):
+            acc = banks[("z", half, a)]
             th = th_pool.tile([P, BANK], F32, tag="th", name="th")
+            ths[(half, a)] = th
             nc.scalar.activation(out=th[:], in_=acc[:], func=ACT.Tanh, bias=bias3[:, a : a + 1], scale=1.0)
-            return th
 
-        def sum_neighbours(th, half, a, fold):
-            first = 0
-            if fold:
-                nc.gpsimd.tensor_tensor(out=th[:, P : 2 * P], in0=th[:, P : 2 * P], in1=th[:, 0:P], op=ADD)
-                first = P
+        def fold(half, a, width):
+            th = ths[(half, a)]
+            nc.gpsimd.tensor_tensor(
+                out=th[:, width : 2 * width], in0=th[:, width : 2 * width], in1=th[:, 0:width], op=ADD
+            )
+
+        def sum_neighbours(half, a, first):
+            th = ths[(half, a)]
             nc.vector.tensor_reduce(
                 out=sums[:, a, HALF_NODES * half : HALF_NODES * (half + 1)],
                 in_=th[:, first:BANK].rearrange("p (q n d) -> p n q d", n=HALF_NODES, d=RUN),
@@ -331,77 +360,203 @@ def tile_dtnnmsg_kernel(
                 op=ADD,
             )
 
-        def store(first, count, queues):
+        def turn(first, count):
             nc.vector.transpose(
                 out=sums_t[:, first : first + count, :].rearrange("p a n -> p (a n)"),
                 in_=sums[:, first : first + count, :].rearrange("p a n -> p (a n)"),
             )
-            for k in range(count):
-                queues[k].dma_start(
-                    out=out.rearrange("n (a q i) -> a q n i", q=4, i=32)[first + k], in_=sums_t[:, first + k, :]
-                )
 
-        tr, mx = (psum_tr, "tr"), (psum_mx, "mx")
-        LEAD = 6
-        warm_up(5)
-        for kb in range(KB):
-            transpose_he(0, kb, *tr, "vector")
+        def store(a, queue):
+            queue.dma_start(out=out.rearrange("n (a q i) -> a q n i", q=4, i=32)[a], in_=sums_t[:, a, :])
+
+        warm_up(3)
+        transpose_he(0, 0)
+        copy_he(0, 0, "vector")
+        transpose_he(0, 1)
+        copy_he(0, 1, "vector")
+        transpose_wdf(0, 0)
+        copy_wdf(0, 0, "scalar")
+        transpose_wdf(0, 1)
+        copy_wdf(0, 1, "vector")
         warm_up(1)
-        transpose_wdf(0, 0, *mx, "scalar")
-        transpose_wdf(0, 1, *mx, "vector")
-        nc.vector.tensor_copy(out=bias2[:], in_=bias2_bf[:])
-        nc.vector.tensor_copy(out=bias1[:], in_=bias1_bf[:])
-        nc.vector.tensor_copy(out=bias3_rows_f[:], in_=bias3_rows[:])
+        copy_biases()
         transpose_x(0, False)
         copy_x(0, "vector")
-        for b in range(LEAD):
-            if b < 3:
-                bond_product(b, lambda: transpose_x(b + 1, False))
-                copy_x(b + 1, "vector" if b < 2 else "scalar")
-                quantise_x(b)
-            else:
-                bond_product(b)
-            if b == 1:
-                transpose_wdf(1, 0, *mx, "scalar")
-                transpose_wdf(1, 1, *mx, "scalar")
-            if b == 2:
-                sort_planes()
-            if b == 3:
-                sort_wcf(0)
-                quantise_x(3)
-        bias3_bank = psum_mx.tile([P, P], F32, tag="mx", name="bias3_bank")
-        nc.tensor.transpose(bias3_bank[:], bias3_rows_f[:], ident[:])
-        sort_x(4)
-        for m in range(2 * CHUNKS):
-            acc = atom_product(m)
-            b = m + LEAD
-            if b == CHUNKS - 1:
-                bond_product(b, lambda: [transpose_he(1, kb, *tr, "scalar") for kb in range(KB)])
-            elif CHUNKS <= b < CHUNKS + TILES:
-                bond_product(b, lambda: transpose_x(b - CHUNKS + TILES, True))
-                copy_x(b - CHUNKS + TILES, "scalar")
-            elif b < 2 * CHUNKS:
-                bond_product(b)
-            hidden_values(acc, m)
-            if m < TILES - 1:
-                sort_x(m + TILES + 1)
-            if m == 1:
-                sort_wcf(1)
-            if m == 3:
-                nc.vector.tensor_copy(out=bias3[:], in_=bias3_bank[:, 0:ATOM_CHUNKS])
-            if 3 <= m <= 6:
-                quantise_x(m + 1)
-            if m % PACK == PACK - 1:
-                interleave_h(m // PACK, ["vector", "gpsimd", "scalar", "vector"][m // PACK])
-            for k in range(4):
-                if [4, 11, 15, 15][k] == m:
-                    quantise_h(k)
-        banks = [(psum_b, "b")] * 2 + [(psum_tr, "tr")] * 2 + [(psum_mx, "mx")] * 4
-        for half in range(HALVES):
-            for a in range(ATOM_CHUNKS):
-                acc = hidden_product(half, a, *banks[a])
-                sum_neighbours(tanh(acc, a), half, a, (half, a) != (1, ATOM_CHUNKS - 1))
-                if half == 1 and a == 3:
-                    store(0, 4, [nc.sync] * 4)
-                if half == 1 and a > 3:
-                    store(a, 1, [nc.sync])
+        bond_product(0, lambda: [transpose_x(1, False)])
+        copy_x(1, "vector")
+        copy_e(0)
+        bond_product(1, lambda: [transpose_x(2, False)])
+        quantise_x(0)
+        copy_e(1)
+        transpose_wdf(1, 0)
+        sort_planes()
+        copy_wdf(1, 0, "scalar")
+        transpose_wdf(1, 1)
+        copy_x(2, "vector")
+        bond_product(2, lambda: [transpose_x(3, False)])
+        quantise_x(1)
+        copy_e(2)
+        bond_product(3)
+        copy_wdf(1, 1, "vector")
+        copy_e(3)
+        bond_product(4)
+        sort_wcf(0)
+        copy_e(4)
+        bond_product(5, lambda: [transpose_he(1, 0), transpose_he(1, 1)])
+        copy_x(3, "vector")
+        copy_he(1, 0, "scalar")
+        bond_product(6)
+        quantise_x(2)
+        copy_he(1, 1, "scalar")
+        transpose_bias3()
+        sort_x(4, "vector")
+        copy_e(5)
+        quantise_x(3)
+        copy_e(6)
+        atom_product(0)
+        copy_bias3()
+        atom_product(1)
+        hidden_values(0)
+        atom_product(2)
+        sort_x(5, "vector")
+        atom_product(3)
+        hidden_values(1)
+        bond_product(7, lambda: [transpose_x(4, True)])
+        sort_x(6, "vector")
+        copy_e(7)
+        bond_product(8, lambda: [transpose_x(5, True)])
+        sort_wcf(1)
+        copy_x(4, "scalar")
+        bond_product(9, lambda: [transpose_x(6, True)])
+        sort_x(7, "vector")
+        copy_e(8)
+        bond_product(10, lambda: [transpose_x(7, True)])
+        hidden_values(2)
+        copy_x(5, "scalar")
+        atom_product(4)
+        hidden_values(3)
+        copy_e(9)
+        atom_product(5)
+        interleave_h(0, "vector")
+        copy_x(6, "scalar")
+        bond_product(11)
+        quantise_x(4)
+        copy_e(10)
+        atom_product(6)
+        quantise_x(5)
+        copy_x(7, "scalar")
+        atom_product(7)
+        quantise_h(0)
+        copy_e(11)
+        bond_product(12)
+        hidden_values(4)
+        copy_e(12)
+        bond_product(13)
+        quantise_x(6)
+        copy_e(13)
+        bond_product(14)
+        hidden_values(5)
+        copy_e(14)
+        quantise_x(7)
+        atom_product(8)
+        hidden_values(6)
+        atom_product(9)
+        hidden_values(7)
+        interleave_h(1, "gpsimd")
+        atom_product(10)
+        hidden_values(8)
+        bond_product(15)
+        hidden_values(9)
+        copy_e(15)
+        atom_product(11)
+        hidden_values(10)
+        atom_product(12)
+        hidden_values(11)
+        interleave_h(2, "scalar")
+        atom_product(13)
+        quantise_h(1)
+        atom_product(14)
+        hidden_values(12)
+        atom_product(15)
+        hidden_values(13)
+        hidden_product(0, 0)
+        hidden_values(14)
+        tanh(0, 0)
+        fold(0, 0, P)
+        hidden_product(0, 1)
+        hidden_values(15)
+        tanh(0, 1)
+        fold(0, 1, P)
+        hidden_product(0, 2)
+        interleave_h(3, "vector")
+        tanh(0, 2)
+        fold(0, 2, P)
+        hidden_product(0, 3)
+        quantise_h(2)
+        tanh(0, 3)
+        fold(0, 3, P)
+        hidden_product(0, 4)
+        quantise_h(3)
+        tanh(0, 4)
+        fold(0, 4, P)
+        hidden_product(0, 5)
+        sum_neighbours(0, 0, P)
+        tanh(0, 5)
+        fold(0, 5, P)
+        hidden_product(0, 6)
+        sum_neighbours(0, 1, P)
+        tanh(0, 6)
+        fold(0, 6, P)
+        hidden_product(0, 7)
+        sum_neighbours(0, 2, P)
+        tanh(0, 7)
+        fold(0, 7, P)
+        hidden_product(1, 0)
+        sum_neighbours(0, 3, P)
+        tanh(1, 0)
+        fold(1, 0, P)
+        hidden_product(1, 1)
+        sum_neighbours(0, 4, P)
+        tanh(1, 1)
+        fold(1, 1, P)
+        hidden_product(1, 2)
+        sum_neighbours(0, 5, P)
+        tanh(1, 2)
+        fold(1, 2, P)
+        hidden_product(1, 3)
+        sum_neighbours(0, 6, P)
+        tanh(1, 3)
+        fold(1, 3, P)
+        hidden_product(1, 4)
+        sum_neighbours(0, 7, P)
+        tanh(1, 4)
+        fold(1, 4, P)
+        hidden_product(1, 5)
+        sum_neighbours(1, 0, P)
+        tanh(1, 5)
+        fold(1, 5, P)
+        hidden_product(1, 6)
+        sum_neighbours(1, 1, P)
+        tanh(1, 6)
+        fold(1, 6, P)
+        hidden_product(1, 7)
+        sum_neighbours(1, 2, P)
+        tanh(1, 7)
+        sum_neighbours(1, 3, P)
+        turn(0, 4)
+        store(0, nc.sync)
+        sum_neighbours(1, 4, P)
+        store(1, nc.sync)
+        sum_neighbours(1, 5, P)
+        store(2, nc.sync)
+        turn(4, 1)
+        store(3, nc.sync)
+        sum_neighbours(1, 6, P)
+        store(4, nc.sync)
+        turn(5, 1)
+        store(5, nc.sync)
+        sum_neighbours(1, 7, 0)
+        turn(7, 1)
+        store(7, nc.sync)
+        turn(6, 1)
+        store(6, nc.sync)

@@ -371,120 +371,121 @@ def tile_dtnnmsg_kernel(
 
         warm_up(3)
         transpose_he(0, 0)
-        copy_he(0, 0, "vector")
+        copy_he(0, 0, "scalar")
         transpose_he(0, 1)
-        copy_he(0, 1, "vector")
+        copy_he(0, 1, "scalar")
         transpose_wdf(0, 0)
-        copy_wdf(0, 0, "scalar")
+        copy_wdf(0, 0, "vector")
         transpose_wdf(0, 1)
         copy_wdf(0, 1, "vector")
         warm_up(1)
         copy_biases()
         transpose_x(0, False)
         copy_x(0, "vector")
-        bond_product(0, lambda: [transpose_x(1, False)])
-        copy_x(1, "vector")
+        bond_product(0)
         copy_e(0)
-        bond_product(1, lambda: [transpose_x(2, False)])
-        quantise_x(0)
-        copy_e(1)
         transpose_wdf(1, 0)
-        sort_planes()
-        copy_wdf(1, 0, "scalar")
+        copy_wdf(1, 0, "vector")
         transpose_wdf(1, 1)
-        copy_x(2, "vector")
-        bond_product(2, lambda: [transpose_x(3, False)])
-        quantise_x(1)
-        copy_e(2)
-        bond_product(3)
+        quantise_x(0)
+        bond_product(1)
+        sort_planes()
+        copy_e(1)
+        bond_product(2)
         copy_wdf(1, 1, "vector")
-        copy_e(3)
-        bond_product(4)
+        copy_e(2)
+        bond_product(3, lambda: [transpose_x(1, False), transpose_x(2, False)])
         sort_wcf(0)
+        copy_x(2, "scalar")
+        bond_product(4, lambda: [transpose_x(3, False)])
+        copy_x(1, "vector")
+        copy_e(3)
+        bond_product(5)
+        sort_wcf(1)
+        copy_x(3, "scalar")
+        bond_product(6, lambda: [transpose_he(1, 1)])
+        quantise_x(1)
         copy_e(4)
-        bond_product(5, lambda: [transpose_he(1, 0), transpose_he(1, 1)])
-        copy_x(3, "vector")
-        copy_he(1, 0, "scalar")
-        bond_product(6)
-        quantise_x(2)
-        copy_he(1, 1, "scalar")
-        transpose_bias3()
         sort_x(4, "vector")
+        sort_x(5, "scalar")
+        bond_product(7, lambda: [transpose_x(4, True), transpose_he(1, 0)])
+        quantise_x(2)
         copy_e(5)
         quantise_x(3)
         copy_e(6)
         atom_product(0)
-        copy_bias3()
+        copy_he(1, 1, "vector")
+        sort_x(6, "scalar")
         atom_product(1)
-        hidden_values(0)
+        copy_x(4, "vector")
+        copy_he(1, 0, "scalar")
         atom_product(2)
-        sort_x(5, "vector")
+        hidden_values(0)
+        sort_x(7, "scalar")
         atom_product(3)
         hidden_values(1)
-        bond_product(7, lambda: [transpose_x(4, True)])
-        sort_x(6, "vector")
         copy_e(7)
-        bond_product(8, lambda: [transpose_x(5, True)])
-        sort_wcf(1)
-        copy_x(4, "scalar")
-        bond_product(9, lambda: [transpose_x(6, True)])
-        sort_x(7, "vector")
-        copy_e(8)
-        bond_product(10, lambda: [transpose_x(7, True)])
-        hidden_values(2)
-        copy_x(5, "scalar")
         atom_product(4)
+        hidden_values(2)
+        bond_product(8, lambda: [transpose_x(5, True)])
         hidden_values(3)
-        copy_e(9)
+        copy_x(5, "scalar")
         atom_product(5)
+        hidden_values(4)
+        copy_e(8)
+        atom_product(6)
+        quantise_x(4)
+        bond_product(9)
+        hidden_values(5)
+        bond_product(10, lambda: [transpose_x(6, True), transpose_x(7, True)])
         interleave_h(0, "vector")
         copy_x(6, "scalar")
-        bond_product(11)
-        quantise_x(4)
-        copy_e(10)
-        atom_product(6)
-        quantise_x(5)
-        copy_x(7, "scalar")
         atom_product(7)
-        quantise_h(0)
-        copy_e(11)
+        hidden_values(6)
+        copy_x(7, "scalar")
+        bond_product(11)
+        quantise_x(5)
+        copy_e(9)
         bond_product(12)
-        hidden_values(4)
-        copy_e(12)
+        quantise_h(0)
+        copy_e(10)
         bond_product(13)
         quantise_x(6)
-        copy_e(13)
+        copy_e(11)
         bond_product(14)
-        hidden_values(5)
-        copy_e(14)
         quantise_x(7)
+        copy_e(12)
         atom_product(8)
-        hidden_values(6)
-        atom_product(9)
         hidden_values(7)
+        copy_e(13)
         interleave_h(1, "gpsimd")
-        atom_product(10)
+        atom_product(9)
         hidden_values(8)
-        bond_product(15)
+        copy_e(14)
+        atom_product(10)
         hidden_values(9)
-        copy_e(15)
         atom_product(11)
         hidden_values(10)
-        atom_product(12)
+        bond_product(15)
         hidden_values(11)
+        copy_e(15)
+        atom_product(12)
+        quantise_h(1)
         interleave_h(2, "scalar")
         atom_product(13)
-        quantise_h(1)
-        atom_product(14)
         hidden_values(12)
-        atom_product(15)
+        atom_product(14)
         hidden_values(13)
-        hidden_product(0, 0)
+        transpose_bias3()
         hidden_values(14)
+        atom_product(15)
+        hidden_values(15)
+        hidden_product(0, 0)
+        copy_bias3()
         tanh(0, 0)
         fold(0, 0, P)
         hidden_product(0, 1)
-        hidden_values(15)
+        quantise_h(2)
         tanh(0, 1)
         fold(0, 1, P)
         hidden_product(0, 2)
@@ -492,70 +493,69 @@ def tile_dtnnmsg_kernel(
         tanh(0, 2)
         fold(0, 2, P)
         hidden_product(0, 3)
-        quantise_h(2)
+        quantise_h(3)
         tanh(0, 3)
         fold(0, 3, P)
         hidden_product(0, 4)
-        quantise_h(3)
+        sum_neighbours(0, 0, P)
         tanh(0, 4)
         fold(0, 4, P)
         hidden_product(0, 5)
-        sum_neighbours(0, 0, P)
+        sum_neighbours(0, 1, P)
         tanh(0, 5)
         fold(0, 5, P)
         hidden_product(0, 6)
-        sum_neighbours(0, 1, P)
+        sum_neighbours(0, 2, P)
         tanh(0, 6)
         fold(0, 6, P)
         hidden_product(0, 7)
-        sum_neighbours(0, 2, P)
+        sum_neighbours(0, 3, P)
         tanh(0, 7)
         fold(0, 7, P)
         hidden_product(1, 0)
-        sum_neighbours(0, 3, P)
+        sum_neighbours(0, 4, P)
         tanh(1, 0)
         fold(1, 0, P)
         hidden_product(1, 1)
-        sum_neighbours(0, 4, P)
+        sum_neighbours(0, 5, P)
         tanh(1, 1)
         fold(1, 1, P)
         hidden_product(1, 2)
-        sum_neighbours(0, 5, P)
+        sum_neighbours(0, 6, P)
         tanh(1, 2)
         fold(1, 2, P)
         hidden_product(1, 3)
-        sum_neighbours(0, 6, P)
+        sum_neighbours(0, 7, P)
         tanh(1, 3)
         fold(1, 3, P)
         hidden_product(1, 4)
-        sum_neighbours(0, 7, P)
+        sum_neighbours(1, 0, P)
         tanh(1, 4)
         fold(1, 4, P)
         hidden_product(1, 5)
-        sum_neighbours(1, 0, P)
+        sum_neighbours(1, 1, P)
         tanh(1, 5)
         fold(1, 5, P)
         hidden_product(1, 6)
-        sum_neighbours(1, 1, P)
+        sum_neighbours(1, 2, P)
         tanh(1, 6)
         fold(1, 6, P)
         hidden_product(1, 7)
-        sum_neighbours(1, 2, P)
-        tanh(1, 7)
         sum_neighbours(1, 3, P)
+        tanh(1, 7)
+        sum_neighbours(1, 4, P)
         turn(0, 4)
         store(0, nc.sync)
-        sum_neighbours(1, 4, P)
-        store(1, nc.sync)
         sum_neighbours(1, 5, P)
+        store(1, nc.sync)
+        sum_neighbours(1, 6, P)
         store(2, nc.sync)
         turn(4, 1)
         store(3, nc.sync)
-        sum_neighbours(1, 6, P)
-        store(4, nc.sync)
         turn(5, 1)
-        store(5, nc.sync)
+        store(4, nc.sync)
         sum_neighbours(1, 7, 0)
+        store(5, nc.sync)
         turn(7, 1)
         store(7, nc.sync)
         turn(6, 1)

@@ -81,13 +81,10 @@ def tile_dtnnmsg_kernel(
             half, q = i // TILES, i % TILES
             nc.sync.dma_start(out=x_sb[:, half, q : q + count, :], in_=x_dram[:, half, q : q + count, :])
 
-        def load_words(tile_u8, words, h):
-            cols = slice(PACK * BANK * h, PACK * BANK * (h + 1))
-            for g in range(GROUPS):
-                nc.sync.dma_start(
-                    out=tile_u8[:, g, cols].bitcast(I32),
-                    in_=words[g].rearrange("p n t -> p (n t)")[:, cols].bitcast(I32),
-                )
+        def load_words(tile_u8, words, g):
+            nc.sync.dma_start(
+                out=tile_u8[:, g, :].bitcast(I32), in_=words[g].rearrange("p n t -> p (n t)").bitcast(I32)
+            )
 
         def load_planes(tile_u8, scales):
             for quadrant in range(4):
@@ -97,34 +94,36 @@ def tile_dtnnmsg_kernel(
                     in_=scales[:, PACK * quadrant : PACK * (quadrant + 1), :].bitcast(I32),
                 )
 
+        bias2_bf = keep.tile([P, CHUNKS], BF16)
+        bias1_bf = keep.tile([P, CHUNKS], BF16)
+
+        def load_bias(tile_bf, bias):
+            nc.sync.dma_start(
+                out=tile_bf[:].rearrange("m (g t) -> m g t", g=GROUPS),
+                in_=bias.rearrange("(g m t) -> m g t", g=GROUPS, t=PACK),
+            )
+
+        def load_bias3():
+            nc.sync.dma_start(out=bias3_rows[0:ATOM_CHUNKS, :], in_=Wfc_b.rearrange("(a m) -> a m", m=P))
+
         load_he(0)
         load_wdf(0)
-        load_x(0)
-        load_x(1)
+        load_bias(bias2_bf, Wdf_b)
+        load_x(0, 2)
         load_wdf(1)
-        load_x(2)
-        load_x(3)
+        load_x(2, 2)
         load_planes(planes, Wcf_w_scales)
         load_words(wcf, Wcf_w_words, 0)
         load_words(wcf, Wcf_w_words, 1)
+        load_bias(bias1_bf, Wcf_b)
         load_he(1)
-        for i in range(4, 8):
-            load_x(i)
+        load_x(4, 2)
+        load_x(6, 2)
+        load_bias3()
         load_planes(planes_fc, Wfc_w_scales)
         load_words(wfc, Wfc_w_words, 0)
         load_words(wfc, Wfc_w_words, 1)
 
-        bias2_bf = keep.tile([P, CHUNKS], BF16)
-        nc.scalar.dma_start(
-            out=bias2_bf[:].rearrange("m (g t) -> m g t", g=GROUPS),
-            in_=Wdf_b.rearrange("(g m t) -> m g t", g=GROUPS, t=PACK),
-        )
-        bias1_bf = keep.tile([P, CHUNKS], BF16)
-        nc.scalar.dma_start(
-            out=bias1_bf[:].rearrange("m (g t) -> m g t", g=GROUPS),
-            in_=Wcf_b.rearrange("(g m t) -> m g t", g=GROUPS, t=PACK),
-        )
-        nc.scalar.dma_start(out=bias3_rows[0:ATOM_CHUNKS, :], in_=Wfc_b.rearrange("(a m) -> a m", m=P))
         nc.scalar.activation(out=warm[:], in_=warm[:], func=ACT.Tanh)
 
         heT = keep.tile([P, KB, TOK], BF16)
@@ -182,8 +181,10 @@ def tile_dtnnmsg_kernel(
             bank = banks[("wdf", g, kb)]
             copy(engine, wdfT[:, kb, BANK * g : BANK * (g + 1)], bank[:].rearrange("p q r -> p (q r)"))
 
-        def copy_biases():
+        def copy_bias2():
             nc.vector.tensor_copy(out=bias2[:], in_=bias2_bf[:])
+
+        def copy_bias1():
             nc.vector.tensor_copy(out=bias1[:], in_=bias1_bf[:])
             nc.vector.tensor_copy(out=bias3_rows_f[:], in_=bias3_rows[:])
 
@@ -379,7 +380,7 @@ def tile_dtnnmsg_kernel(
         transpose_wdf(0, 1)
         copy_wdf(0, 1, "vector")
         warm_up(1)
-        copy_biases()
+        copy_bias2()
         transpose_x(0, False)
         copy_x(0, "vector")
         bond_product(0)
@@ -403,65 +404,66 @@ def tile_dtnnmsg_kernel(
         bond_product(5)
         sort_wcf(1)
         copy_x(3, "scalar")
-        bond_product(6, lambda: [transpose_he(1, 1)])
+        bond_product(6, lambda: [transpose_he(1, 0)])
         quantise_x(1)
         copy_e(4)
-        sort_x(4, "vector")
-        sort_x(5, "scalar")
-        bond_product(7, lambda: [transpose_x(4, True), transpose_he(1, 0)])
+        bond_product(7, lambda: [transpose_he(1, 1)])
         quantise_x(2)
-        copy_e(5)
+        copy_he(1, 0, "scalar")
         quantise_x(3)
-        copy_e(6)
+        copy_e(5)
         atom_product(0)
         copy_he(1, 1, "vector")
-        sort_x(6, "scalar")
+        copy_e(6)
         atom_product(1)
-        copy_x(4, "vector")
-        copy_he(1, 0, "scalar")
+        sort_x(4, "vector")
+        sort_x(6, "scalar")
         atom_product(2)
+        copy_bias1()
+        copy_e(7)
+        atom_product(3)
         hidden_values(0)
         sort_x(7, "scalar")
-        atom_product(3)
-        hidden_values(1)
-        copy_e(7)
         atom_product(4)
+        hidden_values(1)
+        bond_product(8, lambda: [transpose_x(4, True)])
         hidden_values(2)
-        bond_product(8, lambda: [transpose_x(5, True)])
-        hidden_values(3)
-        copy_x(5, "scalar")
         atom_product(5)
-        hidden_values(4)
-        copy_e(8)
+        hidden_values(3)
         atom_product(6)
-        quantise_x(4)
-        bond_product(9)
-        hidden_values(5)
+        sort_x(5, "vector")
+        bond_product(9, lambda: [transpose_x(5, True)])
+        hidden_values(4)
+        copy_x(5, "scalar")
         bond_product(10, lambda: [transpose_x(6, True), transpose_x(7, True)])
+        copy_x(4, "vector")
+        copy_e(8)
+        atom_product(7)
+        hidden_values(5)
+        copy_e(9)
+        bond_product(11)
         interleave_h(0, "vector")
         copy_x(6, "scalar")
-        atom_product(7)
+        bond_product(12)
         hidden_values(6)
         copy_x(7, "scalar")
-        bond_product(11)
-        quantise_x(5)
-        copy_e(9)
-        bond_product(12)
-        quantise_h(0)
-        copy_e(10)
         bond_product(13)
-        quantise_x(6)
-        copy_e(11)
+        quantise_x(4)
+        copy_e(10)
         bond_product(14)
-        quantise_x(7)
+        quantise_x(5)
+        copy_e(11)
+        quantise_h(0)
         copy_e(12)
+        quantise_x(6)
+        copy_e(13)
+        quantise_x(7)
+        copy_e(14)
         atom_product(8)
         hidden_values(7)
-        copy_e(13)
         interleave_h(1, "gpsimd")
         atom_product(9)
         hidden_values(8)
-        copy_e(14)
         atom_product(10)
         hidden_values(9)
         atom_product(11)

@@ -261,10 +261,12 @@ def tile_dtnnmsg_kernel(
         def sort_wcf(h):
             for g in range(GROUPS):
                 nc.vector.tensor_copy(
-                    out=wcf_perm[:, g, BANK * h : BANK * (h + 1)].rearrange("p (t m) -> p t m", t=PACK),
+                    out=wcf_perm[:, g, BANK * h : BANK * (h + 1)].rearrange(
+                        "p (t c i) -> p c t i", t=PACK, i=4
+                    ),
                     in_=wcf[:, g, PACK * BANK * h : PACK * BANK * (h + 1)]
                     .bitcast(I32)
-                    .rearrange("p (m t) -> p t m", t=PACK),
+                    .rearrange("p (c i t) -> p c t i", t=PACK, i=4),
                 )
 
         def sort_planes():
@@ -308,13 +310,12 @@ def tile_dtnnmsg_kernel(
         def interleave_h(k, engine):
             grouped = stage.tile([P, BANK, PACK], BF16, align_bytes=64, tag="h_grouped", name="h_grp")
             h_grouped[k] = grouped
-            src = h_prod[k][:].rearrange("p t r -> p r t")
+            src = h_prod[k][:].rearrange("p t (c i) -> p c t i", i=4)
+            dst = grouped[:].rearrange("p (c i) t -> p c t i", i=4)
             if engine == "gpsimd":
-                nc.gpsimd.tensor_scalar(
-                    out=grouped[:], in0=src, scalar1=1.0, scalar2=0.0, op0=MULT, op1=ADD
-                )
+                nc.gpsimd.tensor_scalar(out=dst, in0=src, scalar1=1.0, scalar2=0.0, op0=MULT, op1=ADD)
             else:
-                copy(engine, grouped[:], src)
+                copy(engine, dst, src)
 
         def quantise_h(k):
             gh, half = k % GROUPS, k // GROUPS

@@ -313,7 +313,14 @@ def tile_dtnnmsg_kernel(
             src = h_prod[k][:].rearrange("p t (c i) -> p c t i", i=4)
             dst = grouped[:].rearrange("p (c i) t -> p c t i", i=4)
             if engine == "gpsimd":
-                nc.gpsimd.tensor_scalar(out=dst, in0=src, scalar1=1.0, scalar2=0.0, op0=MULT, op1=ADD)
+                nc.gpsimd.tensor_scalar(
+                    out=grouped[:],
+                    in0=h_prod[k][:].rearrange("p t r -> p r t"),
+                    scalar1=1.0,
+                    scalar2=0.0,
+                    op0=MULT,
+                    op1=ADD,
+                )
             else:
                 copy(engine, dst, src)
 

@@ -52,7 +52,7 @@ def tile_dtnnmsg_kernel(
         ident = keep.tile([P, P], F32)
         make_identity(nc, ident[:])
         zeros = keep.tile([P, BANK], BF16)
-        nc.vector.memset(zeros[:], 0.0)
+        nc.vector.memset(zeros[:].bitcast(I32), 0)
         planes = keep.tile([P, HID], U8, align_bytes=64)
         nc.vector.memset(planes[:].bitcast(I32), 0)
         planes_fc = keep.tile([P, ATOM], U8, align_bytes=64)
@@ -81,9 +81,11 @@ def tile_dtnnmsg_kernel(
             half, q = i // TILES, i % TILES
             nc.sync.dma_start(out=x_sb[:, half, q : q + count, :], in_=x_dram[:, half, q : q + count, :])
 
-        def load_words(tile_u8, words, g):
+        def load_words(tile_u8, words, g, first=0, count=HID):
+            cols = slice(PACK * first, PACK * (first + count))
             nc.sync.dma_start(
-                out=tile_u8[:, g, :].bitcast(I32), in_=words[g].rearrange("p n t -> p (n t)").bitcast(I32)
+                out=tile_u8[:, g, cols].bitcast(I32),
+                in_=words[g].rearrange("p n t -> p (n t)")[:, cols].bitcast(I32),
             )
 
         def load_planes(tile_u8, scales):
@@ -109,14 +111,17 @@ def tile_dtnnmsg_kernel(
         load_he(0)
         load_wdf(0)
         load_bias(bias2_bf, Wdf_b)
-        load_x(0, 2)
+        load_x(0, 1)
+        load_x(1, 1)
         load_wdf(1)
         load_x(2, 2)
         load_planes(planes, Wcf_w_scales)
-        load_words(wcf, Wcf_w_words, 0)
-        load_words(wcf, Wcf_w_words, 1)
+        load_words(wcf, Wcf_w_words, 0, 0, 512)
+        load_words(wcf, Wcf_w_words, 1, 0, 512)
         load_bias(bias1_bf, Wcf_b)
         load_he(1)
+        load_words(wcf, Wcf_w_words, 0, 512, 512)
+        load_words(wcf, Wcf_w_words, 1, 512, 512)
         load_x(4, 2)
         load_x(6, 2)
         load_bias3()
@@ -186,6 +191,8 @@ def tile_dtnnmsg_kernel(
 
         def copy_bias1():
             nc.vector.tensor_copy(out=bias1[:], in_=bias1_bf[:])
+
+        def copy_bias3_rows():
             nc.vector.tensor_copy(out=bias3_rows_f[:], in_=bias3_rows[:])
 
         def transpose_bias3():
@@ -269,10 +276,11 @@ def tile_dtnnmsg_kernel(
                     .rearrange("p (c i t) -> p c t i", t=PACK, i=4),
                 )
 
-        def sort_planes():
+        def sort_planes(h):
+            cols = slice(BANK * h, BANK * (h + 1))
             nc.vector.tensor_copy(
-                out=planes_perm[:].rearrange("p (h t m) -> p h m t", h=GROUPS, t=PACK),
-                in_=planes[:].rearrange("p (h m t) -> p h m t", h=GROUPS, t=PACK),
+                out=planes_perm[:, cols].rearrange("p (t c i) -> p c t i", t=PACK, i=4),
+                in_=planes[:, cols].rearrange("p (c i t) -> p c t i", t=PACK, i=4),
             )
 
         def atom_product(m):
@@ -398,42 +406,43 @@ def tile_dtnnmsg_kernel(
         transpose_wdf(1, 1)
         quantise_x(0)
         bond_product(1)
-        sort_planes()
+        copy_wdf(1, 1, "vector")
         copy_e(1)
         bond_product(2)
-        copy_wdf(1, 1, "vector")
+        sort_planes(0)
         copy_e(2)
         bond_product(3, lambda: [transpose_x(1, False), transpose_x(2, False)])
-        sort_wcf(0)
+        copy_x(1, "vector")
         copy_x(2, "scalar")
         bond_product(4, lambda: [transpose_x(3, False)])
-        copy_x(1, "vector")
+        sort_wcf(0)
         copy_e(3)
         bond_product(5)
-        sort_wcf(1)
-        copy_x(3, "scalar")
-        bond_product(6, lambda: [transpose_he(1, 0)])
         quantise_x(1)
-        copy_e(4)
-        bond_product(7, lambda: [transpose_he(1, 1)])
+        copy_x(3, "scalar")
+        bond_product(6)
         quantise_x(2)
-        copy_he(1, 0, "scalar")
+        copy_e(4)
         quantise_x(3)
         copy_e(5)
         atom_product(0)
-        copy_he(1, 1, "vector")
+        copy_bias1()
         copy_e(6)
         atom_product(1)
-        sort_x(4, "vector")
-        sort_x(6, "scalar")
-        atom_product(2)
-        copy_bias1()
-        copy_e(7)
-        atom_product(3)
+        sort_planes(1)
+        bond_product(7, lambda: [transpose_he(1, 0), transpose_he(1, 1)])
         hidden_values(0)
-        sort_x(7, "scalar")
+        copy_he(1, 0, "scalar")
+        atom_product(2)
+        sort_wcf(1)
+        sort_x(6, "scalar")
+        atom_product(3)
+        copy_he(1, 1, "vector")
+        copy_e(7)
         atom_product(4)
         hidden_values(1)
+        sort_x(7, "scalar")
+        sort_x(4, "vector")
         bond_product(8, lambda: [transpose_x(4, True)])
         hidden_values(2)
         atom_product(5)
@@ -471,86 +480,87 @@ def tile_dtnnmsg_kernel(
         hidden_values(7)
         interleave_h(1, "gpsimd")
         atom_product(9)
-        hidden_values(8)
+        copy_bias3_rows()
         atom_product(10)
-        hidden_values(9)
+        hidden_values(8)
         atom_product(11)
-        hidden_values(10)
+        hidden_values(9)
         bond_product(15)
-        hidden_values(11)
+        hidden_values(10)
         copy_e(15)
         atom_product(12)
-        quantise_h(1)
+        hidden_values(11)
         interleave_h(2, "scalar")
         atom_product(13)
-        hidden_values(12)
+        quantise_h(1)
         atom_product(14)
-        hidden_values(13)
+        hidden_values(12)
         transpose_bias3()
-        hidden_values(14)
+        hidden_values(13)
         atom_product(15)
-        hidden_values(15)
+        hidden_values(14)
         hidden_product(0, 0)
+        hidden_values(15)
+        hidden_product(0, 1)
         copy_bias3()
         tanh(0, 0)
         fold(0, 0, P)
-        hidden_product(0, 1)
+        hidden_product(0, 2)
         quantise_h(2)
         tanh(0, 1)
         fold(0, 1, P)
-        hidden_product(0, 2)
+        hidden_product(0, 3)
         interleave_h(3, "vector")
         tanh(0, 2)
         fold(0, 2, P)
-        hidden_product(0, 3)
+        hidden_product(0, 4)
         quantise_h(3)
         tanh(0, 3)
         fold(0, 3, P)
-        hidden_product(0, 4)
+        hidden_product(0, 5)
         sum_neighbours(0, 0, P)
         tanh(0, 4)
         fold(0, 4, P)
-        hidden_product(0, 5)
+        hidden_product(0, 6)
         sum_neighbours(0, 1, P)
         tanh(0, 5)
         fold(0, 5, P)
-        hidden_product(0, 6)
+        hidden_product(0, 7)
         sum_neighbours(0, 2, P)
         tanh(0, 6)
         fold(0, 6, P)
-        hidden_product(0, 7)
+        hidden_product(1, 0)
         sum_neighbours(0, 3, P)
         tanh(0, 7)
         fold(0, 7, P)
-        hidden_product(1, 0)
+        hidden_product(1, 1)
         sum_neighbours(0, 4, P)
         tanh(1, 0)
         fold(1, 0, P)
-        hidden_product(1, 1)
+        hidden_product(1, 2)
         sum_neighbours(0, 5, P)
         tanh(1, 1)
         fold(1, 1, P)
-        hidden_product(1, 2)
+        hidden_product(1, 3)
         sum_neighbours(0, 6, P)
         tanh(1, 2)
         fold(1, 2, P)
-        hidden_product(1, 3)
+        hidden_product(1, 4)
         sum_neighbours(0, 7, P)
         tanh(1, 3)
         fold(1, 3, P)
-        hidden_product(1, 4)
+        hidden_product(1, 5)
         sum_neighbours(1, 0, P)
         tanh(1, 4)
         fold(1, 4, P)
-        hidden_product(1, 5)
+        hidden_product(1, 6)
         sum_neighbours(1, 1, P)
         tanh(1, 5)
         fold(1, 5, P)
-        hidden_product(1, 6)
+        hidden_product(1, 7)
         sum_neighbours(1, 2, P)
         tanh(1, 6)
         fold(1, 6, P)
-        hidden_product(1, 7)
         sum_neighbours(1, 3, P)
         tanh(1, 7)
         sum_neighbours(1, 4, P)

@@ -32,6 +32,9 @@ ATOM_CHUNKS = ATOM // P
 HALF_NODES = BANK // DEG
 KB = BOND // P
 RUN = P // HALF_NODES
+LEAD = 7
+X_IN_BOND = {1: (1,), 2: (2,), 3: (3,), 8: (4,), 9: (5,), 10: (6, 7)}
+BONDS_BEHIND = {1: (7,), 4: (8,), 6: (9, 10), 7: (11, 12, 13, 14), 11: (15,)}
 
 FLOPS = 2 * TOK * (ATOM * HID + BOND * HID + HID * ATOM)
 
@@ -203,20 +206,20 @@ def tile_dtnnmsg_kernel(
         def copy_bias3():
             nc.vector.tensor_copy(out=bias3[:], in_=banks["bias3"][:, 0:ATOM_CHUNKS])
 
-        def sort_x(i, engine="vector"):
+        def sort_x(i):
             copy(
-                engine,
+                "scalar",
                 x_sorted[:, i, :].rearrange("p (g u w) -> p g u w", g=GROUPS, u=2),
                 x_sb[:, i // TILES, i % TILES, :].bitcast(F32).rearrange("p (g w u) -> p g u w", g=GROUPS, u=2),
             )
 
-        def transpose_x(i, is_sorted):
+        def transpose_x(i):
             bank = psum.tile([P, GROUPS, 2, P], F32, tag="bank", name="x_bank")
             banks[("x", i)] = bank
             words = x_sb[:, i // TILES, i % TILES, :].bitcast(F32)
             for g in range(GROUPS):
                 for u in range(2):
-                    if is_sorted:
+                    if i >= TILES:
                         first = P * (2 * g + u)
                         rows = x_sorted[:, i, first : first + P]
                     else:
@@ -241,7 +244,7 @@ def tile_dtnnmsg_kernel(
                     in_=x_grouped[i][:, K_PASS * g : K_PASS * (g + 1)],
                 )
 
-        def bond_product(b, between=None):
+        def bond_product(b, between):
             half, c = b // CHUNKS, b % CHUNKS
             cols = slice(BANK * half, BANK * (half + 1))
             acc = psum.tile([P, BANK], F32, tag="bank", name="acc_b")
@@ -254,7 +257,7 @@ def tile_dtnnmsg_kernel(
                     start=(kb == 0),
                     stop=(kb == KB - 1),
                 )
-                if between is not None and kb == 0:
+                if kb == 0:
                     between()
 
         def copy_e(b):
@@ -362,14 +365,12 @@ def tile_dtnnmsg_kernel(
             ths[(half, a)] = th
             nc.scalar.activation(out=th[:], in_=acc[:], func=ACT.Tanh, bias=bias3[:, a : a + 1], scale=1.0)
 
-        def fold(half, a, width):
+        def sum_neighbours(half, a, fold):
             th = ths[(half, a)]
-            nc.gpsimd.tensor_tensor(
-                out=th[:, width : 2 * width], in0=th[:, width : 2 * width], in1=th[:, 0:width], op=ADD
-            )
-
-        def sum_neighbours(half, a, first):
-            th = ths[(half, a)]
+            first = 0
+            if fold:
+                nc.gpsimd.tensor_tensor(out=th[:, P : 2 * P], in0=th[:, P : 2 * P], in1=th[:, 0:P], op=ADD)
+                first = P
             nc.vector.tensor_reduce(
                 out=sums[:, a, HALF_NODES * half : HALF_NODES * (half + 1)],
                 in_=th[:, first:BANK].rearrange("p (q n d) -> p n q d", n=HALF_NODES, d=RUN),
@@ -377,206 +378,91 @@ def tile_dtnnmsg_kernel(
                 op=ADD,
             )
 
-        def turn(first, count):
+        def turn_and_store(first, count):
             nc.vector.transpose(
                 out=sums_t[:, first : first + count, :].rearrange("p a n -> p (a n)"),
                 in_=sums[:, first : first + count, :].rearrange("p a n -> p (a n)"),
             )
-
-        def store(a, queue):
-            queue.dma_start(out=out.rearrange("n (a q i) -> a q n i", q=4, i=32)[a], in_=sums_t[:, a, :])
+            for a in range(first, first + count):
+                nc.sync.dma_start(out=out.rearrange("n (a q i) -> a q n i", q=4, i=32)[a], in_=sums_t[:, a, :])
 
         warm_up(3)
-        transpose_he(0, 0)
-        copy_he(0, 0, "scalar")
-        transpose_he(0, 1)
-        copy_he(0, 1, "scalar")
-        transpose_wdf(0, 0)
-        copy_wdf(0, 0, "vector")
-        transpose_wdf(0, 1)
-        copy_wdf(0, 1, "vector")
+        for kb in range(KB):
+            transpose_he(0, kb)
+            copy_he(0, kb, "scalar")
+        for kb in range(KB):
+            transpose_wdf(0, kb)
+            copy_wdf(0, kb, "vector")
         warm_up(1)
         copy_bias2()
-        transpose_x(0, False)
+        transpose_x(0)
         copy_x(0, "vector")
-        bond_product(0)
-        copy_e(0)
-        transpose_wdf(1, 0)
-        copy_wdf(1, 0, "vector")
-        transpose_wdf(1, 1)
-        quantise_x(0)
-        bond_product(1)
-        copy_wdf(1, 1, "vector")
-        copy_e(1)
-        bond_product(2)
+        for b in range(LEAD):
+            tiles = X_IN_BOND.get(b, ())
+            bond_product(b, lambda: [transpose_x(i) for i in tiles])
+            for i in tiles:
+                copy_x(i, "vector" if i == 1 else "scalar")
+            copy_e(b)
+            if b == 0:
+                for kb in range(KB):
+                    transpose_wdf(1, kb)
+                    copy_wdf(1, kb, "vector")
+                quantise_x(0)
         sort_planes(0)
-        copy_e(2)
-        bond_product(3, lambda: [transpose_x(1, False), transpose_x(2, False)])
-        copy_x(1, "vector")
-        copy_x(2, "scalar")
-        bond_product(4, lambda: [transpose_x(3, False)])
-        sort_wcf(0)
-        copy_e(3)
-        bond_product(5)
         quantise_x(1)
-        copy_x(3, "scalar")
-        bond_product(6)
         quantise_x(2)
-        copy_e(4)
+        sort_wcf(0)
         quantise_x(3)
-        copy_e(5)
-        atom_product(0)
         copy_bias1()
-        copy_e(6)
-        atom_product(1)
         sort_planes(1)
-        bond_product(7, lambda: [transpose_he(1, 0), transpose_he(1, 1)])
-        hidden_values(0)
-        copy_he(1, 0, "scalar")
-        atom_product(2)
-        sort_wcf(1)
-        sort_x(6, "scalar")
-        atom_product(3)
-        copy_he(1, 1, "vector")
-        copy_e(7)
-        atom_product(4)
-        hidden_values(1)
-        sort_x(7, "scalar")
-        sort_x(4, "vector")
-        bond_product(8, lambda: [transpose_x(4, True)])
-        hidden_values(2)
-        atom_product(5)
-        hidden_values(3)
-        atom_product(6)
-        sort_x(5, "vector")
-        bond_product(9, lambda: [transpose_x(5, True)])
-        hidden_values(4)
-        copy_x(5, "scalar")
-        bond_product(10, lambda: [transpose_x(6, True), transpose_x(7, True)])
-        copy_x(4, "vector")
-        copy_e(8)
-        atom_product(7)
-        hidden_values(5)
-        copy_e(9)
-        bond_product(11)
-        interleave_h(0, "vector")
-        copy_x(6, "scalar")
-        bond_product(12)
-        hidden_values(6)
-        copy_x(7, "scalar")
-        bond_product(13)
-        quantise_x(4)
-        copy_e(10)
-        bond_product(14)
-        quantise_x(5)
-        copy_e(11)
-        quantise_h(0)
-        copy_e(12)
-        quantise_x(6)
-        copy_e(13)
-        quantise_x(7)
-        copy_e(14)
-        atom_product(8)
-        hidden_values(7)
-        interleave_h(1, "gpsimd")
-        atom_product(9)
-        copy_bias3_rows()
-        atom_product(10)
-        hidden_values(8)
-        atom_product(11)
-        hidden_values(9)
-        bond_product(15)
-        hidden_values(10)
-        copy_e(15)
-        atom_product(12)
-        hidden_values(11)
-        interleave_h(2, "scalar")
-        atom_product(13)
-        quantise_h(1)
-        atom_product(14)
-        hidden_values(12)
-        transpose_bias3()
-        hidden_values(13)
-        atom_product(15)
-        hidden_values(14)
-        hidden_product(0, 0)
-        hidden_values(15)
-        hidden_product(0, 1)
+
+        for m in range(HALVES * CHUNKS):
+            atom_product(m)
+            for b in BONDS_BEHIND.get(m, ()):
+                tiles = X_IN_BOND.get(b, ())
+                if b == LEAD:
+                    bond_product(b, lambda: [transpose_he(1, kb) for kb in range(KB)])
+                    copy_he(1, 0, "scalar")
+                    copy_he(1, 1, "vector")
+                else:
+                    bond_product(b, lambda: [transpose_x(i) for i in tiles])
+                for i in tiles:
+                    copy_x(i, "vector" if i == TILES else "scalar")
+                copy_e(b)
+            if m == 14:
+                transpose_bias3()
+            hidden_values(m)
+            if m == 0:
+                sort_wcf(1)
+            if 2 <= m < 2 + TILES:
+                sort_x(m - 2 + TILES)
+            if m == 4:
+                interleave_h(0, "vector")
+            if m == 6:
+                quantise_x(4)
+                quantise_x(5)
+                quantise_h(0)
+                quantise_x(6)
+                quantise_x(7)
+            if m == 7:
+                copy_bias3_rows()
+                interleave_h(1, "gpsimd")
+            if m == 11:
+                interleave_h(2, "scalar")
+                quantise_h(1)
         copy_bias3()
-        tanh(0, 0)
-        fold(0, 0, P)
-        hidden_product(0, 2)
         quantise_h(2)
-        tanh(0, 1)
-        fold(0, 1, P)
-        hidden_product(0, 3)
         interleave_h(3, "vector")
-        tanh(0, 2)
-        fold(0, 2, P)
-        hidden_product(0, 4)
         quantise_h(3)
-        tanh(0, 3)
-        fold(0, 3, P)
-        hidden_product(0, 5)
-        sum_neighbours(0, 0, P)
-        tanh(0, 4)
-        fold(0, 4, P)
-        hidden_product(0, 6)
-        sum_neighbours(0, 1, P)
-        tanh(0, 5)
-        fold(0, 5, P)
-        hidden_product(0, 7)
-        sum_neighbours(0, 2, P)
-        tanh(0, 6)
-        fold(0, 6, P)
-        hidden_product(1, 0)
-        sum_neighbours(0, 3, P)
-        tanh(0, 7)
-        fold(0, 7, P)
-        hidden_product(1, 1)
-        sum_neighbours(0, 4, P)
-        tanh(1, 0)
-        fold(1, 0, P)
-        hidden_product(1, 2)
-        sum_neighbours(0, 5, P)
-        tanh(1, 1)
-        fold(1, 1, P)
-        hidden_product(1, 3)
-        sum_neighbours(0, 6, P)
-        tanh(1, 2)
-        fold(1, 2, P)
-        hidden_product(1, 4)
-        sum_neighbours(0, 7, P)
-        tanh(1, 3)
-        fold(1, 3, P)
-        hidden_product(1, 5)
-        sum_neighbours(1, 0, P)
-        tanh(1, 4)
-        fold(1, 4, P)
-        hidden_product(1, 6)
-        sum_neighbours(1, 1, P)
-        tanh(1, 5)
-        fold(1, 5, P)
-        hidden_product(1, 7)
-        sum_neighbours(1, 2, P)
-        tanh(1, 6)
-        fold(1, 6, P)
-        sum_neighbours(1, 3, P)
-        tanh(1, 7)
-        sum_neighbours(1, 4, P)
-        turn(0, 4)
-        store(0, nc.sync)
-        sum_neighbours(1, 5, P)
-        store(1, nc.sync)
-        sum_neighbours(1, 6, P)
-        store(2, nc.sync)
-        turn(4, 1)
-        store(3, nc.sync)
-        turn(5, 1)
-        store(4, nc.sync)
-        sum_neighbours(1, 7, 0)
-        store(5, nc.sync)
-        turn(7, 1)
-        store(7, nc.sync)
-        turn(6, 1)
-        store(6, nc.sync)
+
+        for half in range(HALVES):
+            for a in range(ATOM_CHUNKS):
+                hidden_product(half, a)
+                tanh(half, a)
+                sum_neighbours(half, a, 2 <= ATOM_CHUNKS * half + a < HALVES * ATOM_CHUNKS - 1)
+                if half == 1 and a == 4:
+                    turn_and_store(0, 4)
+                if half == 1 and a == 6:
+                    for k in range(4, 7):
+                        turn_and_store(k, 1)
+        turn_and_store(7, 1)

@@ -56,12 +56,12 @@ def tile_dtnnmsg_kernel(
         make_identity(nc, ident[:])
         zeros = keep.tile([P, BANK], BF16)
         nc.vector.memset(zeros[:].bitcast(I32), 0)
+        bias_rows = keep.tile([P, BANK], BF16)
+        nc.vector.memset(bias_rows[:].bitcast(I32), 0)
         planes = keep.tile([P, HID], U8, align_bytes=64)
         nc.vector.memset(planes[:].bitcast(I32), 0)
         planes_fc = keep.tile([P, ATOM], U8, align_bytes=64)
         nc.vector.memset(planes_fc[:].bitcast(I32), 0)
-        bias3_rows = keep.tile([P, P], BF16)
-        nc.vector.memset(bias3_rows[:], 0.0)
         warm = keep.tile([P, 1], F32)
         nc.vector.memset(warm[:], 0.0)
 
@@ -99,21 +99,15 @@ def tile_dtnnmsg_kernel(
                     in_=scales[:, PACK * quadrant : PACK * (quadrant + 1), :].bitcast(I32),
                 )
 
-        bias2_bf = keep.tile([P, CHUNKS], BF16)
-        bias1_bf = keep.tile([P, CHUNKS], BF16)
-
-        def load_bias(tile_bf, bias):
-            nc.sync.dma_start(
-                out=tile_bf[:].rearrange("m (g t) -> m g t", g=GROUPS),
-                in_=bias.rearrange("(g m t) -> m g t", g=GROUPS, t=PACK),
-            )
-
-        def load_bias3():
-            nc.sync.dma_start(out=bias3_rows[0:ATOM_CHUNKS, :], in_=Wfc_b.rearrange("(a m) -> a m", m=P))
+        def load_biases():
+            for k, bias in enumerate((Wdf_b, Wcf_b, Wfc_b)):
+                nc.sync.dma_start(
+                    out=bias_rows[GROUPS * k : GROUPS * (k + 1), :], in_=bias.rearrange("(g c) -> g c", g=GROUPS)
+                )
 
         load_he(0)
+        load_biases()
         load_wdf(0)
-        load_bias(bias2_bf, Wdf_b)
         load_x(0, 1)
         load_x(1, 1)
         load_wdf(1)
@@ -121,13 +115,11 @@ def tile_dtnnmsg_kernel(
         load_planes(planes, Wcf_w_scales)
         load_words(wcf, Wcf_w_words, 0, 0, 512)
         load_words(wcf, Wcf_w_words, 1, 0, 512)
-        load_bias(bias1_bf, Wcf_b)
         load_he(1)
         load_words(wcf, Wcf_w_words, 0, 512, 512)
         load_words(wcf, Wcf_w_words, 1, 512, 512)
         load_x(4, 2)
         load_x(6, 2)
-        load_bias3()
         load_planes(planes_fc, Wfc_w_scales)
         load_words(wfc, Wfc_w_words, 0)
         load_words(wfc, Wfc_w_words, 1)
@@ -136,10 +128,8 @@ def tile_dtnnmsg_kernel(
 
         heT = keep.tile([P, KB, TOK], BF16)
         wdfT = keep.tile([P, KB, HID], BF16)
-        bias1 = keep.tile([P, CHUNKS], F32)
-        bias2 = keep.tile([P, CHUNKS], F32)
+        bias21 = keep.tile([P, 2, CHUNKS], F32)
         bias3 = keep.tile([P, ATOM_CHUNKS], F32)
-        bias3_rows_f = keep.tile([P, P], F32)
         e_sb = keep.tile([P, CHUNKS, TOK], F32)
         x_codes = keep.tile([P, GROUPS, TOK], U32, align_bytes=64)
         x_scales = keep.tile([P, GROUPS, TOK], U8, align_bytes=64)
@@ -189,22 +179,20 @@ def tile_dtnnmsg_kernel(
             bank = banks[("wdf", g, kb)]
             copy(engine, wdfT[:, kb, BANK * g : BANK * (g + 1)], bank[:].rearrange("p q r -> p (q r)"))
 
-        def copy_bias2():
-            nc.vector.tensor_copy(out=bias2[:], in_=bias2_bf[:])
-
-        def copy_bias1():
-            nc.vector.tensor_copy(out=bias1[:], in_=bias1_bf[:])
-
-        def copy_bias3_rows():
-            nc.vector.tensor_copy(out=bias3_rows_f[:], in_=bias3_rows[:])
-
-        def transpose_bias3():
-            bank = psum.tile([P, P], F32, tag="bank", name="bias3_bank")
-            banks["bias3"] = bank
-            nc.tensor.transpose(bank[:], bias3_rows_f[:], ident[:])
-
-        def copy_bias3():
-            nc.vector.tensor_copy(out=bias3[:], in_=banks["bias3"][:, 0:ATOM_CHUNKS])
+        def turn_biases():
+            bank = psum.tile([P, 2 * PACK, P], BF16, tag="bank", name="bias_bank")
+            for t in range(PACK):
+                nc.tensor.transpose(bank[:, t, :], bias_rows[:, t:BANK:PACK], ident_bf[:])
+            for q in range(BANK // P):
+                nc.tensor.transpose(bank[:, PACK + q, :], bias_rows[:, P * q : P * (q + 1)], ident_bf[:])
+            nc.vector.tensor_copy(
+                out=bias21[:].rearrange("p b (g t) -> p (b g) t", g=GROUPS),
+                in_=bank[:, 0:PACK, 0 : 2 * GROUPS].rearrange("p t r -> p r t"),
+            )
+            nc.vector.tensor_copy(
+                out=bias3[:].rearrange("p (g q) -> p g q", g=GROUPS),
+                in_=bank[:, PACK : 2 * PACK, 2 * GROUPS : 3 * GROUPS].rearrange("p q r -> p r q"),
+            )
 
         def sort_x(i):
             copy(
@@ -265,7 +253,7 @@ def tile_dtnnmsg_kernel(
             cols = slice(BANK * half, BANK * (half + 1))
             acc = banks[("b", b)]
             nc.scalar.activation(
-                out=e_sb[:, c, cols], in_=acc[:], func=ACT.Identity, bias=bias2[:, c : c + 1], scale=1.0
+                out=e_sb[:, c, cols], in_=acc[:], func=ACT.Identity, bias=bias21[:, 0, c : c + 1], scale=1.0
             )
 
         def sort_wcf(h):
@@ -312,7 +300,7 @@ def tile_dtnnmsg_kernel(
             nc.vector.scalar_tensor_tensor(
                 out=h_prod[k][:, t, :],
                 in0=acc[:],
-                scalar=bias1[:, c : c + 1],
+                scalar=bias21[:, 1, c : c + 1],
                 in1=e_sb[:, c, cols],
                 op0=ADD,
                 op1=MULT,
@@ -365,6 +353,20 @@ def tile_dtnnmsg_kernel(
             ths[(half, a)] = th
             nc.scalar.activation(out=th[:], in_=acc[:], func=ACT.Tanh, bias=bias3[:, a : a + 1], scale=1.0)
 
+        def tanh_and_sum(half, a):
+            acc = banks[("z", half, a)][:].rearrange("p (q n d) -> p n q d", n=HALF_NODES, d=RUN)
+            th = th_pool.tile([P, HALF_NODES, TILES, RUN], F32, tag="th", name="th")
+            for n in range(HALF_NODES):
+                column = HALF_NODES * half + n
+                nc.scalar.activation(
+                    out=th[:, n],
+                    in_=acc[:, n],
+                    func=ACT.Tanh,
+                    bias=bias3[:, a : a + 1],
+                    scale=1.0,
+                    accum_out=sums[:, a, column : column + 1],
+                )
+
         def sum_neighbours(half, a, fold):
             th = ths[(half, a)]
             first = 0
@@ -386,15 +388,14 @@ def tile_dtnnmsg_kernel(
             for a in range(first, first + count):
                 nc.sync.dma_start(out=out.rearrange("n (a q i) -> a q n i", q=4, i=32)[a], in_=sums_t[:, a, :])
 
-        warm_up(3)
+        warm_up(4)
         for kb in range(KB):
             transpose_he(0, kb)
             copy_he(0, kb, "scalar")
+        turn_biases()
         for kb in range(KB):
             transpose_wdf(0, kb)
             copy_wdf(0, kb, "vector")
-        warm_up(1)
-        copy_bias2()
         transpose_x(0)
         copy_x(0, "vector")
         for b in range(LEAD):
@@ -413,7 +414,6 @@ def tile_dtnnmsg_kernel(
         quantise_x(2)
         sort_wcf(0)
         quantise_x(3)
-        copy_bias1()
         sort_planes(1)
 
         for m in range(HALVES * CHUNKS):
@@ -429,8 +429,6 @@ def tile_dtnnmsg_kernel(
                 for i in tiles:
                     copy_x(i, "vector" if i == TILES else "scalar")
                 copy_e(b)
-            if m == 14:
-                transpose_bias3()
             hidden_values(m)
             if m == 0:
                 sort_wcf(1)
@@ -445,19 +443,20 @@ def tile_dtnnmsg_kernel(
                 quantise_x(6)
                 quantise_x(7)
             if m == 7:
-                copy_bias3_rows()
                 interleave_h(1, "gpsimd")
             if m == 11:
                 interleave_h(2, "scalar")
                 quantise_h(1)
-        copy_bias3()
-        quantise_h(2)
         interleave_h(3, "vector")
+        quantise_h(2)
         quantise_h(3)
 
         for half in range(HALVES):
             for a in range(ATOM_CHUNKS):
                 hidden_product(half, a)
+                if (half, a) == (1, ATOM_CHUNKS - 1):
+                    tanh_and_sum(half, a)
+                    continue
                 tanh(half, a)
                 sum_neighbours(half, a, 2 <= ATOM_CHUNKS * half + a < HALVES * ATOM_CHUNKS - 1)
                 if half == 1 and a == 4:

from contextlib import ExitStack

import concourse.mybir as mybir
from concourse.masks import make_identity

F32 = mybir.dt.float32
BF16 = mybir.dt.bfloat16
I32 = mybir.dt.int32
U32 = mybir.dt.uint32
U8 = mybir.dt.uint8
FP8X4 = mybir.dt.float8_e4m3fn_x4
ADD = mybir.AluOpType.add
MULT = mybir.AluOpType.mult
ACT = mybir.ActivationFunctionType
AXES = mybir.AxisListType

P = 128
PACK = 4
K_PASS = P * PACK
NODES = 32
DEG = 32
ATOM = 1024
BOND = 256
HID = 1024
TOK = NODES * DEG
BANK = 512
HALVES = TOK // BANK
TILES = BANK // P
GROUPS = ATOM // K_PASS
CHUNKS = HID // P
ATOM_CHUNKS = ATOM // P
HALF_NODES = BANK // DEG
KB = BOND // P
RUN = P // HALF_NODES
LEAD = 7
X_IN_BOND = {1: (1,), 2: (2,), 3: (3,), 8: (4,), 9: (5,), 10: (6, 7)}
BONDS_BEHIND = {1: (7,), 4: (8,), 6: (9, 10), 7: (11, 12, 13, 14), 11: (15,)}

FLOPS = 2 * TOK * (ATOM * HID + BOND * HID + HID * ATOM)


def tile_dtnnmsg_kernel(
    tc, src_h, he, Wcf_w_words, Wcf_w_scales, Wcf_b, Wdf_w, Wdf_b, Wfc_w_words, Wfc_w_scales, Wfc_b, out
):
    nc = tc.nc
    with ExitStack() as ctx:
        keep = ctx.enter_context(tc.tile_pool(name="keep", bufs=1))
        stage = ctx.enter_context(tc.tile_pool(name="stage", bufs=4))
        th_pool = ctx.enter_context(tc.tile_pool(name="th_pool", bufs=8))
        psum = ctx.enter_context(tc.psum_pool(name="psum", bufs=8))
        ctx.enter_context(tc.manual_schedule())

        ident_bf = keep.tile([P, P], BF16)
        make_identity(nc, ident_bf[:])
        ident = keep.tile([P, P], F32)
        make_identity(nc, ident[:])
        zeros = keep.tile([P, BANK], BF16)
        nc.vector.memset(zeros[:].bitcast(I32), 0)
        bias_rows = keep.tile([P, BANK], BF16)
        nc.vector.memset(bias_rows[:].bitcast(I32), 0)
        planes = keep.tile([P, HID], U8, align_bytes=64)
        nc.vector.memset(planes[:].bitcast(I32), 0)
        planes_fc = keep.tile([P, ATOM], U8, align_bytes=64)
        nc.vector.memset(planes_fc[:].bitcast(I32), 0)
        warm = keep.tile([P, 1], F32)
        nc.vector.memset(warm[:], 0.0)

        x_dram = src_h.flatten_outer_dims().rearrange("(h p q) a -> p h q a", h=HALVES, q=TILES)
        he_dram = he.flatten_outer_dims().rearrange("(h p q) b -> p h q b", h=HALVES, q=TILES)
        wdf_dram = Wdf_w.rearrange("(g m t) b -> m g t b", g=GROUPS, t=PACK)
        he_sb = keep.tile([P, HALVES, TILES, BOND], BF16)
        wdf_sb = keep.tile([P, GROUPS, PACK, BOND], BF16)
        x_sb = keep.tile([P, HALVES, TILES, ATOM], BF16)
        wcf = keep.tile([P, GROUPS, PACK * HID], U8, align_bytes=64)
        wfc = keep.tile([P, GROUPS, PACK * ATOM], U8, align_bytes=64)

        def load_he(half):
            nc.sync.dma_start(out=he_sb[:, half, :, :], in_=he_dram[:, half, :, :])

        def load_wdf(g):
            nc.sync.dma_start(out=wdf_sb[:, g, :, :], in_=wdf_dram[:, g, :, :])

        def load_x(i, count=1):
            half, q = i // TILES, i % TILES
            nc.sync.dma_start(out=x_sb[:, half, q : q + count, :], in_=x_dram[:, half, q : q + count, :])

        def load_words(tile_u8, words, g, first=0, count=HID):
            cols = slice(PACK * first, PACK * (first + count))
            nc.sync.dma_start(
                out=tile_u8[:, g, cols].bitcast(I32),
                in_=words[g].rearrange("p n t -> p (n t)")[:, cols].bitcast(I32),
            )

        def load_planes(tile_u8, scales):
            for quadrant in range(4):
                start = 32 * quadrant
                nc.sync.dma_start(
                    out=tile_u8[start : start + PACK * GROUPS, :].bitcast(I32),
                    in_=scales[:, PACK * quadrant : PACK * (quadrant + 1), :].bitcast(I32),
                )

        def load_biases():
            for k, bias in enumerate((Wdf_b, Wcf_b, Wfc_b)):
                nc.sync.dma_start(
                    out=bias_rows[GROUPS * k : GROUPS * (k + 1), :], in_=bias.rearrange("(g c) -> g c", g=GROUPS)
                )

        load_he(0)
        load_biases()
        load_wdf(0)
        load_x(0, 1)
        load_x(1, 1)
        load_wdf(1)
        load_x(2, 2)
        load_planes(planes, Wcf_w_scales)
        load_words(wcf, Wcf_w_words, 0, 0, 512)
        load_words(wcf, Wcf_w_words, 1, 0, 512)
        load_he(1)
        load_words(wcf, Wcf_w_words, 0, 512, 512)
        load_words(wcf, Wcf_w_words, 1, 512, 512)
        load_x(4, 2)
        load_x(6, 2)
        load_planes(planes_fc, Wfc_w_scales)
        load_words(wfc, Wfc_w_words, 0)
        load_words(wfc, Wfc_w_words, 1)

        nc.scalar.activation(out=warm[:], in_=warm[:], func=ACT.Tanh)

        heT = keep.tile([P, KB, TOK], BF16)
        wdfT = keep.tile([P, KB, HID], BF16)
        bias21 = keep.tile([P, 2, CHUNKS], F32)
        bias3 = keep.tile([P, ATOM_CHUNKS], F32)
        e_sb = keep.tile([P, CHUNKS, TOK], F32)
        x_codes = keep.tile([P, GROUPS, TOK], U32, align_bytes=64)
        x_scales = keep.tile([P, GROUPS, TOK], U8, align_bytes=64)
        x_sorted = keep.tile([P, HALVES * TILES, ATOM // 2], F32)
        wcf_perm = keep.tile([P, GROUPS, HID], I32, align_bytes=64)
        planes_perm = keep.tile([P, HID], U8, align_bytes=64)
        h_codes = keep.tile([P, GROUPS, TOK], U32, align_bytes=64)
        h_scales = keep.tile([P, GROUPS, TOK], U8, align_bytes=64)
        sums = keep.tile([P, ATOM_CHUNKS, NODES], F32, align_bytes=64)
        sums_t = keep.tile([P, ATOM_CHUNKS, NODES], F32, align_bytes=64)
        banks = {}
        x_grouped = {}
        h_prod = {}
        h_grouped = {}
        ths = {}

        def copy(engine, out_ap, in_ap):
            if engine == "scalar":
                nc.scalar.copy(out=out_ap, in_=in_ap)
            elif engine == "gpsimd":
                nc.gpsimd.tensor_copy(out=out_ap, in_=in_ap)
            else:
                nc.vector.tensor_copy(out=out_ap, in_=in_ap)

        def warm_up(count):
            bank = psum.tile([P, BANK], F32, tag="bank", name="warm_bank")
            for k in range(count):
                nc.tensor.matmul(out=bank[:], lhsT=zeros[:, 0:P], rhs=zeros[:], start=True, stop=True)

        def transpose_four(key, rows_of):
            bank = psum.tile([P, 4, P], BF16, tag="bank", name="four_bank")
            banks[key] = bank
            for q in range(4):
                nc.tensor.transpose(bank[:, q, :], rows_of(q), ident_bf[:])

        def transpose_he(half, kb):
            transpose_four(("he", half, kb), lambda q: he_sb[:, half, q, P * kb : P * (kb + 1)])

        def copy_he(half, kb, engine):
            bank = banks[("he", half, kb)]
            copy(engine, heT[:, kb, BANK * half : BANK * (half + 1)], bank[:].rearrange("p q r -> p (q r)"))

        def transpose_wdf(g, kb):
            transpose_four(("wdf", g, kb), lambda t: wdf_sb[:, g, t, P * kb : P * (kb + 1)])

        def copy_wdf(g, kb, engine):
            bank = banks[("wdf", g, kb)]
            copy(engine, wdfT[:, kb, BANK * g : BANK * (g + 1)], bank[:].rearrange("p q r -> p (q r)"))

        def turn_biases():
            bank = psum.tile([P, 2 * PACK, P], BF16, tag="bank", name="bias_bank")
            for t in range(PACK):
                nc.tensor.transpose(bank[:, t, :], bias_rows[:, t:BANK:PACK], ident_bf[:])
            for q in range(BANK // P):
                nc.tensor.transpose(bank[:, PACK + q, :], bias_rows[:, P * q : P * (q + 1)], ident_bf[:])
            nc.vector.tensor_copy(
                out=bias21[:].rearrange("p b (g t) -> p (b g) t", g=GROUPS),
                in_=bank[:, 0:PACK, 0 : 2 * GROUPS].rearrange("p t r -> p r t"),
            )
            nc.vector.tensor_copy(
                out=bias3[:].rearrange("p (g q) -> p g q", g=GROUPS),
                in_=bank[:, PACK : 2 * PACK, 2 * GROUPS : 3 * GROUPS].rearrange("p q r -> p r q"),
            )

        def sort_x(i):
            copy(
                "scalar",
                x_sorted[:, i, :].rearrange("p (g u w) -> p g u w", g=GROUPS, u=2),
                x_sb[:, i // TILES, i % TILES, :].bitcast(F32).rearrange("p (g w u) -> p g u w", g=GROUPS, u=2),
            )

        def transpose_x(i):
            bank = psum.tile([P, GROUPS, 2, P], F32, tag="bank", name="x_bank")
            banks[("x", i)] = bank
            words = x_sb[:, i // TILES, i % TILES, :].bitcast(F32)
            for g in range(GROUPS):
                for u in range(2):
                    if i >= TILES:
                        first = P * (2 * g + u)
                        rows = x_sorted[:, i, first : first + P]
                    else:
                        rows = words[:, 256 * g + u : 256 * (g + 1) : 2]
                    nc.tensor.transpose(bank[:, g, u, :], rows, ident[:])

        def copy_x(i, engine):
            grouped = stage.tile([P, GROUPS * P * PACK], BF16, align_bytes=64, tag="x_grouped", name="x_grp")
            x_grouped[i] = grouped
            copy(
                engine,
                grouped[:].bitcast(F32).rearrange("p (g r u) -> p g r u", g=GROUPS, u=2),
                banks[("x", i)][:].rearrange("p g u r -> p g r u"),
            )

        def quantise_x(i):
            toks = slice(P * i, P * (i + 1))
            for g in range(GROUPS):
                nc.vector.quantize_mx(
                    out=x_codes[:, g, toks].bitcast(FP8X4),
                    scales=x_scales[:, g, toks],
                    in_=x_grouped[i][:, K_PASS * g : K_PASS * (g + 1)],
                )

        def bond_product(b, between):
            half, c = b // CHUNKS, b % CHUNKS
            cols = slice(BANK * half, BANK * (half + 1))
            acc = psum.tile([P, BANK], F32, tag="bank", name="acc_b")
            banks[("b", b)] = acc
            for kb in range(KB):
                nc.tensor.matmul(
                    out=acc[:],
                    lhsT=wdfT[:, kb, P * c : P * (c + 1)],
                    rhs=heT[:, kb, cols],
                    start=(kb == 0),
                    stop=(kb == KB - 1),
                )
                if kb == 0:
                    between()

        def copy_e(b):
            half, c = b // CHUNKS, b % CHUNKS
            cols = slice(BANK * half, BANK * (half + 1))
            acc = banks[("b", b)]
            nc.scalar.activation(
                out=e_sb[:, c, cols], in_=acc[:], func=ACT.Identity, bias=bias21[:, 0, c : c + 1], scale=1.0
            )

        def sort_wcf(h):
            for g in range(GROUPS):
                nc.vector.tensor_copy(
                    out=wcf_perm[:, g, BANK * h : BANK * (h + 1)].rearrange(
                        "p (t c i) -> p c t i", t=PACK, i=4
                    ),
                    in_=wcf[:, g, PACK * BANK * h : PACK * BANK * (h + 1)]
                    .bitcast(I32)
                    .rearrange("p (c i t) -> p c t i", t=PACK, i=4),
                )

        def sort_planes(h):
            cols = slice(BANK * h, BANK * (h + 1))
            nc.vector.tensor_copy(
                out=planes_perm[:, cols].rearrange("p (t c i) -> p c t i", t=PACK, i=4),
                in_=planes[:, cols].rearrange("p (c i t) -> p c t i", t=PACK, i=4),
            )

        def atom_product(m):
            half, c = m // CHUNKS, m % CHUNKS
            cols = slice(BANK * half, BANK * (half + 1))
            acc = psum.tile([P, BANK], F32, tag="bank", name="acc_mx")
            banks[("m", m)] = acc
            for g in range(GROUPS):
                nc.tensor.matmul_mx(
                    out=acc[:],
                    lhsT=wcf_perm[:, g, P * c : P * (c + 1)].bitcast(FP8X4),
                    lhsT_scale=planes_perm[PACK * g : P, P * c : P * (c + 1)],
                    rhs=x_codes[:, g, cols].bitcast(FP8X4),
                    rhs_scale=x_scales[:, g, cols],
                    start=(g == 0),
                    stop=(g == GROUPS - 1),
                )

        def hidden_values(m):
            acc = banks[("m", m)]
            half, c = m // CHUNKS, m % CHUNKS
            cols = slice(BANK * half, BANK * (half + 1))
            k, t = m // PACK, m % PACK
            if k not in h_prod:
                h_prod[k] = stage.tile([P, PACK, BANK], BF16, tag="h_prod", name="h_prd")
            nc.vector.scalar_tensor_tensor(
                out=h_prod[k][:, t, :],
                in0=acc[:],
                scalar=bias21[:, 1, c : c + 1],
                in1=e_sb[:, c, cols],
                op0=ADD,
                op1=MULT,
            )

        def interleave_h(k, engine):
            grouped = stage.tile([P, BANK, PACK], BF16, align_bytes=64, tag="h_grouped", name="h_grp")
            h_grouped[k] = grouped
            src = h_prod[k][:].rearrange("p t (c i) -> p c t i", i=4)
            dst = grouped[:].rearrange("p (c i) t -> p c t i", i=4)
            if engine == "gpsimd":
                nc.gpsimd.tensor_scalar(
                    out=grouped[:],
                    in0=h_prod[k][:].rearrange("p t r -> p r t"),
                    scalar1=1.0,
                    scalar2=0.0,
                    op0=MULT,
                    op1=ADD,
                )
            else:
                copy(engine, dst, src)

        def quantise_h(k):
            gh, half = k % GROUPS, k // GROUPS
            cols = slice(BANK * half, BANK * (half + 1))
            nc.vector.quantize_mx(
                out=h_codes[:, gh, cols].bitcast(FP8X4),
                scales=h_scales[:, gh, cols],
                in_=h_grouped[k][:].rearrange("p r t -> p (r t)"),
            )

        def hidden_product(half, a):
            cols = slice(BANK * half, BANK * (half + 1))
            acc = psum.tile([P, BANK], F32, tag="bank", name="acc_z")
            banks[("z", half, a)] = acc
            for gh in range(GROUPS):
                nc.tensor.matmul_mx(
                    out=acc[:],
                    lhsT=wfc[:, gh, PACK * P * a : PACK * P * (a + 1)].bitcast(FP8X4),
                    lhsT_scale=planes_fc[PACK * gh : P, P * a : P * (a + 1)],
                    rhs=h_codes[:, gh, cols].bitcast(FP8X4),
                    rhs_scale=h_scales[:, gh, cols],
                    start=(gh == 0),
                    stop=(gh == GROUPS - 1),
                )

        def tanh(half, a):
            acc = banks[("z", half, a)]
            th = th_pool.tile([P, BANK], F32, tag="th", name="th")
            ths[(half, a)] = th
            nc.scalar.activation(out=th[:], in_=acc[:], func=ACT.Tanh, bias=bias3[:, a : a + 1], scale=1.0)

        def tanh_and_sum(half, a):
            acc = banks[("z", half, a)][:].rearrange("p (q n d) -> p n q d", n=HALF_NODES, d=RUN)
            th = th_pool.tile([P, HALF_NODES, TILES, RUN], F32, tag="th", name="th")
            for n in range(HALF_NODES):
                column = HALF_NODES * half + n
                nc.scalar.activation(
                    out=th[:, n],
                    in_=acc[:, n],
                    func=ACT.Tanh,
                    bias=bias3[:, a : a + 1],
                    scale=1.0,
                    accum_out=sums[:, a, column : column + 1],
                )

        def sum_neighbours(half, a, fold):
            th = ths[(half, a)]
            first = 0
            if fold:
                nc.gpsimd.tensor_tensor(out=th[:, P : 2 * P], in0=th[:, P : 2 * P], in1=th[:, 0:P], op=ADD)
                first = P
            nc.vector.tensor_reduce(
                out=sums[:, a, HALF_NODES * half : HALF_NODES * (half + 1)],
                in_=th[:, first:BANK].rearrange("p (q n d) -> p n q d", n=HALF_NODES, d=RUN),
                axis=AXES.XY,
                op=ADD,
            )

        def turn_and_store(first, count):
            nc.vector.transpose(
                out=sums_t[:, first : first + count, :].rearrange("p a n -> p (a n)"),
                in_=sums[:, first : first + count, :].rearrange("p a n -> p (a n)"),
            )
            for a in range(first, first + count):
                nc.sync.dma_start(out=out.rearrange("n (a q i) -> a q n i", q=4, i=32)[a], in_=sums_t[:, a, :])

        warm_up(4)
        for kb in range(KB):
            transpose_he(0, kb)
            copy_he(0, kb, "scalar")
        turn_biases()
        for kb in range(KB):
            transpose_wdf(0, kb)
            copy_wdf(0, kb, "vector")
        transpose_x(0)
        copy_x(0, "vector")
        for b in range(LEAD):
            tiles = X_IN_BOND.get(b, ())
            bond_product(b, lambda: [transpose_x(i) for i in tiles])
            for i in tiles:
                copy_x(i, "vector" if i == 1 else "scalar")
            copy_e(b)
            if b == 0:
                for kb in range(KB):
                    transpose_wdf(1, kb)
                    copy_wdf(1, kb, "vector")
                quantise_x(0)
        sort_planes(0)
        quantise_x(1)
        quantise_x(2)
        sort_wcf(0)
        quantise_x(3)
        sort_planes(1)

        for m in range(HALVES * CHUNKS):
            atom_product(m)
            for b in BONDS_BEHIND.get(m, ()):
                tiles = X_IN_BOND.get(b, ())
                if b == LEAD:
                    bond_product(b, lambda: [transpose_he(1, kb) for kb in range(KB)])
                    copy_he(1, 0, "scalar")
                    copy_he(1, 1, "vector")
                else:
                    bond_product(b, lambda: [transpose_x(i) for i in tiles])
                for i in tiles:
                    copy_x(i, "vector" if i == TILES else "scalar")
                copy_e(b)
            hidden_values(m)
            if m == 0:
                sort_wcf(1)
            if 2 <= m < 2 + TILES:
                sort_x(m - 2 + TILES)
            if m == 4:
                interleave_h(0, "vector")
            if m == 6:
                quantise_x(4)
                quantise_x(5)
                quantise_h(0)
                quantise_x(6)
                quantise_x(7)
            if m == 7:
                interleave_h(1, "gpsimd")
            if m == 11:
                interleave_h(2, "scalar")
                quantise_h(1)
        interleave_h(3, "vector")
        quantise_h(2)
        quantise_h(3)

        for half in range(HALVES):
            for a in range(ATOM_CHUNKS):
                hidden_product(half, a)
                if (half, a) == (1, ATOM_CHUNKS - 1):
                    tanh_and_sum(half, a)
                    continue
                tanh(half, a)
                sum_neighbours(half, a, 2 <= ATOM_CHUNKS * half + a < HALVES * ATOM_CHUNKS - 1)
                if half == 1 and a == 4:
                    turn_and_store(0, 4)
                if half == 1 and a == 6:
                    for k in range(4, 7):
                        turn_and_store(k, 1)
        turn_and_store(7, 1)
